import numpy as np
import ml_dtypes


def mxq(x, axis, fmt="e4m3"):
    dtype, down = {"e4m3": (ml_dtypes.float8_e4m3fn, 7), "e5m2": (ml_dtypes.float8_e5m2, 14)}[fmt]
    v = np.moveaxis(np.asarray(x, np.float32).astype(ml_dtypes.bfloat16).astype(np.float64), axis, -1)
    blocks = v.reshape(v.shape[:-1] + (-1, 32))
    amax = np.abs(blocks).max(-1, keepdims=True)
    byte = np.maximum(np.where(amax > 0, np.frexp(amax)[1] - 1 + 127, 0) - down, 1)
    scale = np.exp2(byte - 127.0)
    codes = (blocks / scale).astype(np.float32).astype(dtype).astype(np.float64)
    return np.moveaxis((codes * scale).reshape(v.shape), -1, axis)


WIDE = False


def mx_kscale(k):
    if not WIDE:
        return np.ones(k)
    levels = np.array([10, -10, 5, -5, 0])
    a = np.random.permutation(np.resize(levels, k // 512 * 4)).reshape(k // 512, 4)
    idx = np.arange(k)
    return np.exp2(a[idx // 512, idx % 128 // 32])


BF16 = ml_dtypes.bfloat16


def bf(x):
    return np.asarray(x, np.float32).astype(BF16)


def f64(x):
    return np.asarray(x).astype(np.float64)


B, C, DW, F1, F2, G, J = 512, 4096, 300, 512, 128, 2048, 2048
SLOPE = 0.2
PE = 2.0 / np.sqrt(C)


def leaky_relu(v):
    return np.where(v >= 0.0, v, SLOPE * v)


def gen_adj(a):
    d = a.sum(1) ** -0.5
    return d[:, None] * a.T * d[None, :]


def setup_inputs():
    s = mx_kscale(F1)
    return {"x_pre": bf(np.random.standard_normal((C, F1)) * s),
            "A": bf(np.random.uniform(size=(C, C)) * (np.random.uniform(size=(C, C)) < PE)),
            "W_gc2": bf(np.random.standard_normal((F1, F2)) * 2.6 / np.sqrt(F1) / s[:, None])}


def reference(x_pre, A, W_gc2):
    adj = gen_adj(f64(A))
    h = leaky_relu(f64(x_pre))
    support = mxq(h, 1, "e4m3") @ mxq(f64(W_gc2), 0, "e4m3")
    return mxq(adj, 1, "e4m3") @ mxq(support, 0, "e4m3")

@@ -1,0 +1,276 @@
+from contextlib import ExitStack
+
+import concourse.mybir as mybir
+from concourse.masks import make_identity
+
+F32 = mybir.dt.float32
+BF16 = mybir.dt.bfloat16
+U32 = mybir.dt.uint32
+U8 = mybir.dt.uint8
+FP8X4 = mybir.dt.float8_e4m3fn_x4
+ALU = mybir.AluOpType
+ACT = mybir.ActivationFunctionType
+
+P = 128
+C = 4096
+F1 = 512
+F2 = 128
+NB = 8
+BLK = 512
+SLOPE = 0.2
+FLOPS = 2 * C * F1 * F2 + 2 * C * C * F2
+
+GROUPS = ((0, 3), (3, 3), (6, 2))
+V_SUMS = {(0, 1), (0, 2), (1, 1), (1, 2), (2, 1), (2, 2), (3, 2), (4, 2), (5, 2), (6, 2), (7, 2)}
+
+
+def tile_gcnresnet_pa_t_kernel(tc, x_pre, A, W_gc2, out):
+    nc = tc.nc
+    a_view = A.rearrange("(c p t) i -> c p t i", p=P, t=4)
+    x_view = x_pre.rearrange("(c p t) k -> c p t k", p=P, t=4)
+    out_view = out.rearrange("(b u p) f -> b p u f", u=4, p=P)
+
+    with ExitStack() as ctx:
+        const = ctx.enter_context(tc.tile_pool(name="const", bufs=1))
+        apool = ctx.enter_context(tc.tile_pool(name="apool", bufs=7))
+        a8pool = ctx.enter_context(tc.tile_pool(name="a8pool", bufs=2))
+        t1pool = ctx.enter_context(tc.tile_pool(name="t1pool", bufs=2))
+        gpool = ctx.enter_context(tc.tile_pool(name="gpool", bufs=2))
+        cpool = ctx.enter_context(tc.tile_pool(name="cpool", bufs=3))
+        xpool = ctx.enter_context(tc.tile_pool(name="xpool", bufs=2))
+        small = ctx.enter_context(tc.tile_pool(name="small", bufs=2))
+        opool = ctx.enter_context(tc.tile_pool(name="opool", bufs=2))
+        dpsum = ctx.enter_context(tc.psum_pool(name="dpsum", bufs=3))
+        accps = ctx.enter_context(tc.psum_pool(name="accps", bufs=3))
+        misc = ctx.enter_context(tc.psum_pool(name="misc", bufs=1))
+
+        ident = const.tile([P, P], F32, name="ident")
+        make_identity(nc, ident[:])
+        neghalf = const.tile([P, 4], F32, name="neghalf")
+        nc.gpsimd.memset(neghalf[:], -0.5)
+        rs_s = const.tile([P, NB, 3, 4], F32, name="rs_s")
+        rs_v = const.tile([P, NB, 3, 4], F32, name="rs_v")
+        dinv = const.tile([P, NB, 4], F32, name="dinv")
+        sup_codes = const.tile([P, NB, F2], U32, name="sup_codes", align_bytes=64)
+        sup_scales = const.tile([P, NB, F2], U8, name="sup_scales", align_bytes=64)
+        w_codes = const.tile([P, F2], U32, name="w_codes", align_bytes=64)
+        w_scales = const.tile([P, F2], U8, name="w_scales", align_bytes=64)
+
+        a_tiles = {}
+
+        def load_a(c, g):
+            b0, nb = GROUPS[g]
+            if nb == 3:
+                t = apool.tile([P, 4, nb * BLK], BF16, name="a12")
+            else:
+                t = a8pool.tile([P, 4, nb * BLK], BF16, name="a8")
+            nc.sync.dma_start(out=t[:], in_=a_view[c][:, :, b0 * BLK : (b0 + nb) * BLK])
+            a_tiles[(c, g)] = t
+
+        def load_w():
+            w_raw = const.tile([P, 4, F2], BF16, name="w_raw")
+            for u in range(2):
+                nc.sync.dma_start(
+                    out=w_raw[:, 2 * u : 2 * u + 2, :],
+                    in_=W_gc2[256 * u : 256 * u + 256, :].rearrange("(q e) f -> q e f", e=2),
+                )
+            w_grp = const.tile([P, F2, 4], BF16, name="w_grp", align_bytes=64)
+            nc.vector.tensor_copy(out=w_grp[:], in_=w_raw[:].rearrange("q s f -> q f s"))
+            nc.vector.quantize_mx(
+                out=w_codes[:].bitcast(FP8X4),
+                scales=w_scales[:],
+                in_=w_grp[:].rearrange("q f s -> q (f s)"),
+            )
+
+        x_tiles = {}
+
+        def load_x(c):
+            x_raw = xpool.tile([P, 4, F1], BF16, name="x_raw")
+            nc.sync.dma_start(out=x_raw[:], in_=x_view[c])
+            x_tiles[c] = x_raw
+
+        def support(c):
+            x_words = x_tiles[c][:].bitcast(F32)
+            x_grp = xpool.tile([P, BLK, 4], BF16, name="x_grp", align_bytes=64)
+            x_grp_w = x_grp[:].bitcast(F32)
+            for half in range(2):
+                tp = misc.tile([P, 2, 2, P], F32, name="tp", tag="tp")
+                for tt in range(2):
+                    for u in range(2):
+                        nc.tensor.transpose(
+                            tp[:, tt, u, :], x_words[:, 2 * half + tt, P * u : P * u + P], ident[:]
+                        )
+                nc.scalar.copy(
+                    out=x_grp_w[:, 256 * half : 256 * half + 256, :].rearrange("q (t p) u -> q t p u", t=2),
+                    in_=tp[:].rearrange("q t u p -> q t p u"),
+                )
+            x_flat = x_grp[:].rearrange("q n s -> q (n s)")
+            y = xpool.tile([P, 4 * BLK], BF16, name="y")
+            nc.vector.tensor_scalar(out=y[:], in0=x_flat, scalar1=SLOPE, scalar2=None, op0=ALU.mult)
+            h_grp = xpool.tile([P, 4 * BLK], BF16, name="h_grp", align_bytes=64)
+            nc.vector.tensor_tensor(out=h_grp[:], in0=x_flat, in1=y[:], op=ALU.max)
+            h_codes = xpool.tile([P, BLK], U32, name="h_codes", align_bytes=64)
+            h_scales = xpool.tile([P, BLK], U8, name="h_scales", align_bytes=64)
+            nc.vector.quantize_mx(out=h_codes[:].bitcast(FP8X4), scales=h_scales[:], in_=h_grp[:])
+            sp = misc.tile([P, 4, F2], F32, name="sp", tag="sp")
+            for t in range(4):
+                nc.tensor.matmul_mx(
+                    out=sp[:, t, :],
+                    lhsT=h_codes[:, P * t : P * t + P].bitcast(FP8X4),
+                    lhsT_scale=h_scales[:, P * t : P * t + P],
+                    rhs=w_codes[:].bitcast(FP8X4),
+                    rhs_scale=w_scales[:],
+                    start=True,
+                    stop=True,
+                )
+            s_grp = xpool.tile([P, F2, 4], BF16, name="s_grp", align_bytes=64)
+            nc.scalar.copy(out=s_grp[:], in_=sp[:].rearrange("p t f -> p f t"))
+            nc.vector.quantize_mx(
+                out=sup_codes[:, c, :].bitcast(FP8X4),
+                scales=sup_scales[:, c, :],
+                in_=s_grp[:].rearrange("p f t -> p (f t)"),
+            )
+
+        def row_sums(c, g):
+            t_a = a_tiles[(c, g)]
+            for t in range(4):
+                if (c, g) in V_SUMS:
+                    nc.vector.tensor_scalar(
+                        out=t_a[:, t, :],
+                        in0=t_a[:, t, :],
+                        scalar1=1.0,
+                        scalar2=None,
+                        op0=ALU.mult,
+                        op1=ALU.add,
+                        accum_out=rs_v[:, c, g, t : t + 1],
+                    )
+                else:
+                    nc.scalar.activation(
+                        out=t_a[:, t, :], in_=t_a[:, t, :], func=ACT.Copy, accum_out=rs_s[:, c, g, t : t + 1]
+                    )
+
+        def part(c, g):
+            return rs_v[:, c, g, :] if (c, g) in V_SUMS else rs_s[:, c, g, :]
+
+        def chain(c):
+            s1 = small.tile([P, 4], F32, name="s1")
+            nc.gpsimd.tensor_tensor(out=s1[:], in0=part(c, 0), in1=part(c, 1), op=ALU.add)
+            s2 = small.tile([P, 4], F32, name="s2")
+            nc.gpsimd.tensor_tensor(out=s2[:], in0=s1[:], in1=part(c, 2), op=ALU.add)
+            nc.gpsimd.tensor_tensor(out=dinv[:, c, :], in0=s2[:], in1=neghalf[:], op=ALU.pow)
+
+        dbc = {}
+
+        def spread(b):
+            t_d = dpsum.tile([P, BLK], F32, name="dbc")
+            for t in range(4):
+                nc.tensor.transpose(
+                    t_d[:].rearrange("m (q t) -> m t q", t=4)[:, t, :],
+                    dinv[:, b, t : t + 1].to_broadcast([P, P]),
+                    ident[:],
+                )
+            dbc[b] = t_d
+
+        t1_tiles = {}
+
+        def scale_rows(c, g, engines, per_block):
+            b0, nb = GROUPS[g]
+            t_a = a_tiles[(c, g)]
+            t1 = t1pool.tile([P, 4, 3 * BLK], F32, name="t1")
+            pieces = [(k * BLK, BLK) for k in range(nb)] if per_block else [(0, nb * BLK)]
+            for lo, w in pieces:
+                for t in range(4):
+                    if engines[t] == "G":
+                        nc.gpsimd.tensor_scalar(
+                            out=t1[:, t, lo : lo + w],
+                            in0=t_a[:, t, lo : lo + w],
+                            scalar1=dinv[:, c, t : t + 1],
+                            scalar2=0.0,
+                            op0=ALU.mult,
+                            op1=ALU.add,
+                        )
+                    else:
+                        nc.scalar.activation(
+                            out=t1[:, t, lo : lo + w],
+                            in_=t_a[:, t, lo : lo + w],
+                            func=ACT.Copy,
+                            scale=dinv[:, c, t : t + 1],
+                        )
+            t1_tiles[(c, g)] = t1
+
+        acc = {}
+        done = {}
+
+        def block(c, g, b):
+            b0, nb = GROUPS[g]
+            lo = (b - b0) * BLK
+            t1 = t1_tiles[(c, g)]
+            grp = gpool.tile([P, BLK, 4], BF16, name="grp", align_bytes=64)
+            nc.vector.tensor_tensor(
+                out=grp[:],
+                in0=t1[:, :, lo : lo + BLK].rearrange("p t i -> p i t"),
+                in1=dbc[b][:].unsqueeze(2).to_broadcast([P, BLK, 4]),
+                op=ALU.mult,
+            )
+            codes = cpool.tile([P, BLK], U32, name="codes", align_bytes=64)
+            scales = cpool.tile([P, BLK], U8, name="scales", align_bytes=64)
+            nc.vector.quantize_mx(
+                out=codes[:].bitcast(FP8X4), scales=scales[:], in_=grp[:].rearrange("p i t -> p (i t)")
+            )
+            if b not in acc:
+                acc[b] = accps.tile([P, BLK], F32, name="acc")
+                done[b] = 0
+            nc.tensor.matmul_mx(
+                out=acc[b][:],
+                lhsT=sup_codes[:, c, :].bitcast(FP8X4),
+                lhsT_scale=sup_scales[:, c, :],
+                rhs=codes[:].bitcast(FP8X4),
+                rhs_scale=scales[:],
+                start=(done[b] == 0),
+                stop=(done[b] == NB - 1),
+            )
+            done[b] += 1
+
+        def close(b):
+            o_t = opool.tile([P, BLK], F32, name="o_t")
+            nc.scalar.copy(out=o_t[:], in_=acc[b][:])
+            tq = misc.tile([P, 4, F2], F32, name="tq", tag="tp")
+            for u in range(4):
+                nc.tensor.transpose(tq[:, u, :], o_t[:, P * u : P * u + P], ident[:])
+            o_s = opool.tile([P, 4, F2], F32, name="o_s")
+            nc.scalar.copy(out=o_s[:], in_=tq[:])
+            nc.sync.dma_start(out=out_view[b], in_=o_s[:])
+
+        for g in range(3):
+            load_a(0, g)
+        load_w()
+        load_x(0)
+        for c in range(NB):
+            if c + 1 < NB:
+                load_x(c + 1)
+                for g in range(3):
+                    load_a(c + 1, g)
+            for g in range(3):
+                row_sums(c, g)
+            support(c)
+            chain(c)
+            if c < 3:
+                spread(c)
+                for r in range(c):
+                    block(r, 0, c)
+            scale_rows(c, 0, "GGGG", c < 3)
+            for b in range(min(c + 1, 3)):
+                block(c, 0, b)
+        for b in range(3):
+            close(b)
+        for g in (1, 2):
+            b0, nb = GROUPS[g]
+            for b in range(b0, b0 + nb):
+                spread(b)
+            for c in range(NB):
+                load_a(c, g)
+                scale_rows(c, g, "GSGS", False)
+                for b in range(b0, b0 + nb):
+                    block(c, g, b)
+            for b in range(b0, b0 + nb):
+                close(b)

@@ -180,7 +180,15 @@ def tile_gcnresnet_pa_t_kernel(tc, x_pre, A, W_gc2, out):
             pieces = [(k * BLK, BLK) for k in range(nb)] if per_block else [(0, nb * BLK)]
             for lo, w in pieces:
                 for t in range(4):
-                    if engines[t] == "G":
+                    if engines[t] == "V":
+                        nc.vector.tensor_scalar(
+                            out=t1[:, t, lo : lo + w],
+                            in0=t_a[:, t, lo : lo + w],
+                            scalar1=dinv[:, c, t : t + 1],
+                            scalar2=None,
+                            op0=ALU.mult,
+                        )
+                    elif engines[t] == "G":
                         nc.gpsimd.tensor_scalar(
                             out=t1[:, t, lo : lo + w],
                             in0=t_a[:, t, lo : lo + w],
@@ -258,7 +266,7 @@ def tile_gcnresnet_pa_t_kernel(tc, x_pre, A, W_gc2, out):
                 spread(c)
                 for r in range(c):
                     block(r, 0, c)
-            scale_rows(c, 0, "GGGG", c < 3)
+            scale_rows(c, 0, "VVVV", c < 3)
             for b in range(min(c + 1, 3)):
                 block(c, 0, b)
         for b in range(3):
@@ -269,7 +277,7 @@ def tile_gcnresnet_pa_t_kernel(tc, x_pre, A, W_gc2, out):
                 spread(b)
             for c in range(NB):
                 load_a(c, g)
-                scale_rows(c, g, "GSGS", False)
+                scale_rows(c, g, "SSSS", False)
                 for b in range(b0, b0 + nb):
                     block(c, g, b)
             for b in range(b0, b0 + nb):

@@ -215,9 +215,9 @@ def tile_gcnresnet_pa_t_kernel(tc, x_pre, A, W_gc2, out):
             t1 = t1_tiles[(c, g)]
             grp = gpool.tile([P, BLK, 4], BF16, name="grp", align_bytes=64)
             nc.vector.tensor_tensor(
-                out=grp[:],
-                in0=t1[:, :, lo : lo + BLK].rearrange("p t i -> p i t"),
-                in1=dbc[b][:].unsqueeze(2).to_broadcast([P, BLK, 4]),
+                out=grp[:].rearrange("p (c i) t -> p c t i", i=4),
+                in0=t1[:, :, lo : lo + BLK].rearrange("p t (c i) -> p c t i", i=4),
+                in1=dbc[b][:].rearrange("p (c i) -> p c i", i=4).unsqueeze(2).to_broadcast([P, BLK // 4, 4, 4]),
                 op=ALU.mult,
             )
             codes = cpool.tile([P, BLK], U32, name="codes", align_bytes=64)

@@ -17,11 +17,16 @@ F1 = 512
 F2 = 128
 NB = 8
 BLK = 512
+QW = 1024
 SLOPE = 0.2
 FLOPS = 2 * C * F1 * F2 + 2 * C * C * F2
 
-GROUPS = ((0, 3), (3, 3), (6, 2))
-V_SUMS = {(0, 1), (0, 2), (1, 1), (1, 2), (2, 1), (2, 2), (3, 2), (4, 2), (5, 2), (6, 2), (7, 2)}
+V_SUMS = {(0, 2), (0, 3), (1, 2), (1, 3), (2, 3), (3, 3), (4, 3), (5, 3)}
+T1_ROUND0 = "GGGG"
+T1_ROUND1 = "SSSS"
+S_ROUND0 = "VVVV"
+S_ROUND1 = "VVVG"
+A_BUFS = 13
 
 
 def tile_gcnresnet_pa_t_kernel(tc, x_pre, A, W_gc2, out):
@@ -32,24 +37,24 @@ def tile_gcnresnet_pa_t_kernel(tc, x_pre, A, W_gc2, out):
 
     with ExitStack() as ctx:
         const = ctx.enter_context(tc.tile_pool(name="const", bufs=1))
-        apool = ctx.enter_context(tc.tile_pool(name="apool", bufs=7))
-        a8pool = ctx.enter_context(tc.tile_pool(name="a8pool", bufs=2))
-        t1pool = ctx.enter_context(tc.tile_pool(name="t1pool", bufs=2))
+        apool = ctx.enter_context(tc.tile_pool(name="apool", bufs=A_BUFS))
+        t1pool = ctx.enter_context(tc.tile_pool(name="t1pool", bufs=3))
         gpool = ctx.enter_context(tc.tile_pool(name="gpool", bufs=2))
         cpool = ctx.enter_context(tc.tile_pool(name="cpool", bufs=3))
         xpool = ctx.enter_context(tc.tile_pool(name="xpool", bufs=2))
+        x1pool = ctx.enter_context(tc.tile_pool(name="x1pool", bufs=1))
         small = ctx.enter_context(tc.tile_pool(name="small", bufs=2))
         opool = ctx.enter_context(tc.tile_pool(name="opool", bufs=2))
-        dpsum = ctx.enter_context(tc.psum_pool(name="dpsum", bufs=3))
-        accps = ctx.enter_context(tc.psum_pool(name="accps", bufs=3))
+        dpsum = ctx.enter_context(tc.psum_pool(name="dpsum", bufs=2))
+        accps = ctx.enter_context(tc.psum_pool(name="accps", bufs=4))
         misc = ctx.enter_context(tc.psum_pool(name="misc", bufs=1))
 
         ident = const.tile([P, P], F32, name="ident")
         make_identity(nc, ident[:])
         neghalf = const.tile([P, 4], F32, name="neghalf")
         nc.gpsimd.memset(neghalf[:], -0.5)
-        rs_s = const.tile([P, NB, 3, 4], F32, name="rs_s")
-        rs_v = const.tile([P, NB, 3, 4], F32, name="rs_v")
+        rs_s = const.tile([P, NB, 4, 4], F32, name="rs_s")
+        rs_v = const.tile([P, NB, 4, 4], F32, name="rs_v")
         dinv = const.tile([P, NB, 4], F32, name="dinv")
         sup_codes = const.tile([P, NB, F2], U32, name="sup_codes", align_bytes=64)
         sup_scales = const.tile([P, NB, F2], U8, name="sup_scales", align_bytes=64)
@@ -58,14 +63,10 @@ def tile_gcnresnet_pa_t_kernel(tc, x_pre, A, W_gc2, out):
 
         a_tiles = {}
 
-        def load_a(c, g):
-            b0, nb = GROUPS[g]
-            if nb == 3:
-                t = apool.tile([P, 4, nb * BLK], BF16, name="a12")
-            else:
-                t = a8pool.tile([P, 4, nb * BLK], BF16, name="a8")
-            nc.sync.dma_start(out=t[:], in_=a_view[c][:, :, b0 * BLK : (b0 + nb) * BLK])
-            a_tiles[(c, g)] = t
+        def load_a(c, q):
+            t = apool.tile([P, 4, QW], BF16, name="aq")
+            nc.sync.dma_start(out=t[:], in_=a_view[c][:, :, q * QW : (q + 1) * QW])
+            a_tiles[(c, q)] = t
 
         def load_w():
             w_raw = const.tile([P, 4, F2], BF16, name="w_raw")
@@ -91,7 +92,7 @@ def tile_gcnresnet_pa_t_kernel(tc, x_pre, A, W_gc2, out):
 
         def support(c):
             x_words = x_tiles[c][:].bitcast(F32)
-            x_grp = xpool.tile([P, BLK, 4], BF16, name="x_grp", align_bytes=64)
+            x_grp = x1pool.tile([P, BLK, 4], BF16, name="x_grp", align_bytes=64)
             x_grp_w = x_grp[:].bitcast(F32)
             for half in range(2):
                 tp = misc.tile([P, 2, 2, P], F32, name="tp", tag="tp")
@@ -105,12 +106,11 @@ def tile_gcnresnet_pa_t_kernel(tc, x_pre, A, W_gc2, out):
                     in_=tp[:].rearrange("q t u p -> q t p u"),
                 )
             x_flat = x_grp[:].rearrange("q n s -> q (n s)")
-            y = xpool.tile([P, 4 * BLK], BF16, name="y")
-            nc.vector.tensor_scalar(out=y[:], in0=x_flat, scalar1=SLOPE, scalar2=None, op0=ALU.mult)
             h_grp = xpool.tile([P, 4 * BLK], BF16, name="h_grp", align_bytes=64)
-            nc.vector.tensor_tensor(out=h_grp[:], in0=x_flat, in1=y[:], op=ALU.max)
-            h_codes = xpool.tile([P, BLK], U32, name="h_codes", align_bytes=64)
-            h_scales = xpool.tile([P, BLK], U8, name="h_scales", align_bytes=64)
+            nc.vector.tensor_scalar(out=h_grp[:], in0=x_flat, scalar1=SLOPE, scalar2=None, op0=ALU.mult)
+            nc.vector.tensor_tensor(out=h_grp[:], in0=x_flat, in1=h_grp[:], op=ALU.max)
+            h_codes = x1pool.tile([P, BLK], U32, name="h_codes", align_bytes=64)
+            h_scales = x1pool.tile([P, BLK], U8, name="h_scales", align_bytes=64)
             nc.vector.quantize_mx(out=h_codes[:].bitcast(FP8X4), scales=h_scales[:], in_=h_grp[:])
             sp = misc.tile([P, 4, F2], F32, name="sp", tag="sp")
             for t in range(4):
@@ -123,7 +123,7 @@ def tile_gcnresnet_pa_t_kernel(tc, x_pre, A, W_gc2, out):
                     start=True,
                     stop=True,
                 )
-            s_grp = xpool.tile([P, F2, 4], BF16, name="s_grp", align_bytes=64)
+            s_grp = x1pool.tile([P, F2, 4], BF16, name="s_grp", align_bytes=64)
             nc.scalar.copy(out=s_grp[:], in_=sp[:].rearrange("p t f -> p f t"))
             nc.vector.quantize_mx(
                 out=sup_codes[:, c, :].bitcast(FP8X4),
@@ -131,10 +131,10 @@ def tile_gcnresnet_pa_t_kernel(tc, x_pre, A, W_gc2, out):
                 in_=s_grp[:].rearrange("p f t -> p (f t)"),
             )
 
-        def row_sums(c, g):
-            t_a = a_tiles[(c, g)]
+        def row_sums(c, q):
+            t_a = a_tiles[(c, q)]
             for t in range(4):
-                if (c, g) in V_SUMS:
+                if (c, q) in V_SUMS:
                     nc.vector.tensor_scalar(
                         out=t_a[:, t, :],
                         in0=t_a[:, t, :],
@@ -142,143 +142,169 @@ def tile_gcnresnet_pa_t_kernel(tc, x_pre, A, W_gc2, out):
                         scalar2=None,
                         op0=ALU.mult,
                         op1=ALU.add,
-                        accum_out=rs_v[:, c, g, t : t + 1],
+                        accum_out=rs_v[:, c, q, t : t + 1],
                     )
                 else:
                     nc.scalar.activation(
-                        out=t_a[:, t, :], in_=t_a[:, t, :], func=ACT.Copy, accum_out=rs_s[:, c, g, t : t + 1]
+                        out=t_a[:, t, :], in_=t_a[:, t, :], func=ACT.Copy, accum_out=rs_s[:, c, q, t : t + 1]
                     )
 
-        def part(c, g):
-            return rs_v[:, c, g, :] if (c, g) in V_SUMS else rs_s[:, c, g, :]
+        def part(c, q):
+            return rs_v[:, c, q, :] if (c, q) in V_SUMS else rs_s[:, c, q, :]
 
         def chain(c):
-            s1 = small.tile([P, 4], F32, name="s1")
-            nc.gpsimd.tensor_tensor(out=s1[:], in0=part(c, 0), in1=part(c, 1), op=ALU.add)
-            s2 = small.tile([P, 4], F32, name="s2")
-            nc.gpsimd.tensor_tensor(out=s2[:], in0=s1[:], in1=part(c, 2), op=ALU.add)
-            nc.gpsimd.tensor_tensor(out=dinv[:, c, :], in0=s2[:], in1=neghalf[:], op=ALU.pow)
+            s01 = small.tile([P, 4], F32, name="s01")
+            nc.gpsimd.tensor_tensor(out=s01[:], in0=part(c, 0), in1=part(c, 1), op=ALU.add)
+            s23 = small.tile([P, 4], F32, name="s23")
+            nc.gpsimd.tensor_tensor(out=s23[:], in0=part(c, 2), in1=part(c, 3), op=ALU.add)
+            s_all = small.tile([P, 4], F32, name="s_all")
+            nc.gpsimd.tensor_tensor(out=s_all[:], in0=s01[:], in1=s23[:], op=ALU.add)
+            nc.gpsimd.tensor_tensor(out=dinv[:, c, :], in0=s_all[:], in1=neghalf[:], op=ALU.pow)
 
-        dbc = {}
-
-        def spread(b):
-            t_d = dpsum.tile([P, BLK], F32, name="dbc")
+        def spread(t_d, b):
             for t in range(4):
                 nc.tensor.transpose(
                     t_d[:].rearrange("m (q t) -> m t q", t=4)[:, t, :],
                     dinv[:, b, t : t + 1].to_broadcast([P, P]),
                     ident[:],
                 )
-            dbc[b] = t_d
+
+        dbc_sb = {}
+
+        def spread_sbuf(b):
+            tq = misc.tile([P, BLK], F32, name="td", tag="tp")
+            spread(tq, b)
+            dbc_sb[b] = const.tile([P, BLK], F32, name="dbc_sb%d" % b)
+            nc.scalar.copy(out=dbc_sb[b][:], in_=tq[:])
 
         t1_tiles = {}
 
-        def scale_rows(c, g, engines, per_block):
-            b0, nb = GROUPS[g]
-            t_a = a_tiles[(c, g)]
-            t1 = t1pool.tile([P, 4, 3 * BLK], F32, name="t1")
-            pieces = [(k * BLK, BLK) for k in range(nb)] if per_block else [(0, nb * BLK)]
-            for lo, w in pieces:
-                for t in range(4):
-                    if engines[t] == "V":
-                        nc.vector.tensor_scalar(
-                            out=t1[:, t, lo : lo + w],
-                            in0=t_a[:, t, lo : lo + w],
-                            scalar1=dinv[:, c, t : t + 1],
-                            scalar2=None,
-                            op0=ALU.mult,
-                        )
-                    elif engines[t] == "G":
-                        nc.gpsimd.tensor_scalar(
-                            out=t1[:, t, lo : lo + w],
-                            in0=t_a[:, t, lo : lo + w],
-                            scalar1=dinv[:, c, t : t + 1],
-                            scalar2=0.0,
-                            op0=ALU.mult,
-                            op1=ALU.add,
-                        )
-                    else:
-                        nc.scalar.activation(
-                            out=t1[:, t, lo : lo + w],
-                            in_=t_a[:, t, lo : lo + w],
-                            func=ACT.Copy,
-                            scale=dinv[:, c, t : t + 1],
-                        )
-            t1_tiles[(c, g)] = t1
+        def scale_rows(c, q, engines):
+            t_a = a_tiles[(c, q)]
+            t1 = t1pool.tile([P, 4, QW], F32, name="t1")
+            for t in range(4):
+                if engines[t] == "V":
+                    nc.vector.tensor_scalar(
+                        out=t1[:, t, :], in0=t_a[:, t, :], scalar1=dinv[:, c, t : t + 1], scalar2=None, op0=ALU.mult
+                    )
+                elif engines[t] == "G":
+                    nc.gpsimd.tensor_scalar(
+                        out=t1[:, t, :],
+                        in0=t_a[:, t, :],
+                        scalar1=dinv[:, c, t : t + 1],
+                        scalar2=0.0,
+                        op0=ALU.mult,
+                        op1=ALU.add,
+                    )
+                else:
+                    nc.scalar.activation(
+                        out=t1[:, t, :], in_=t_a[:, t, :], func=ACT.Copy, scale=dinv[:, c, t : t + 1]
+                    )
+            t1_tiles[(c, q)] = t1
 
         acc = {}
         done = {}
 
-        def block(c, g, b):
-            b0, nb = GROUPS[g]
-            lo = (b - b0) * BLK
-            t1 = t1_tiles[(c, g)]
-            grp = gpool.tile([P, BLK, 4], BF16, name="grp", align_bytes=64)
-            nc.vector.tensor_tensor(
-                out=grp[:].rearrange("p (c i) t -> p c t i", i=4),
-                in0=t1[:, :, lo : lo + BLK].rearrange("p t (c i) -> p c t i", i=4),
-                in1=dbc[b][:].rearrange("p (c i) -> p c i", i=4).unsqueeze(2).to_broadcast([P, BLK // 4, 4, 4]),
-                op=ALU.mult,
-            )
-            codes = cpool.tile([P, BLK], U32, name="codes", align_bytes=64)
-            scales = cpool.tile([P, BLK], U8, name="scales", align_bytes=64)
+        def unit(c, q, t1_engines, s_engines):
+            scale_rows(c, q, t1_engines)
+            t1 = t1_tiles[(c, q)]
+            grp = gpool.tile([P, 2 * BLK, 4], BF16, name="grp", align_bytes=64)
+            for k in range(2):
+                b = 2 * q + k
+                lo = k * BLK
+                if s_engines[k] == "V":
+                    t_d = dpsum.tile([P, BLK], F32, name="dbc")
+                    spread(t_d, b)
+                    nc.vector.tensor_tensor(
+                        out=grp[:, lo : lo + BLK, :].rearrange("p (c i) t -> p c t i", i=4),
+                        in0=t1[:, :, lo : lo + BLK].rearrange("p t (c i) -> p c t i", i=4),
+                        in1=t_d[:].rearrange("p (c i) -> p c i", i=4).unsqueeze(2).to_broadcast([P, BLK // 4, 4, 4]),
+                        op=ALU.mult,
+                    )
+                else:
+                    for z in range(4):
+                        nc.gpsimd.tensor_tensor(
+                            out=grp[:, lo + P * z : lo + P * z + P, :],
+                            in0=t1[:, :, lo + P * z : lo + P * z + P].rearrange("p t i -> p i t"),
+                            in1=dbc_sb[b][:, P * z : P * z + P].unsqueeze(2).to_broadcast([P, P, 4]),
+                            op=ALU.mult,
+                        )
+            codes = cpool.tile([P, 2 * BLK], U32, name="codes", align_bytes=64)
+            scales = cpool.tile([P, 2 * BLK], U8, name="scales", align_bytes=64)
             nc.vector.quantize_mx(
                 out=codes[:].bitcast(FP8X4), scales=scales[:], in_=grp[:].rearrange("p i t -> p (i t)")
             )
-            if b not in acc:
-                acc[b] = accps.tile([P, BLK], F32, name="acc")
-                done[b] = 0
-            nc.tensor.matmul_mx(
-                out=acc[b][:],
-                lhsT=sup_codes[:, c, :].bitcast(FP8X4),
-                lhsT_scale=sup_scales[:, c, :],
-                rhs=codes[:].bitcast(FP8X4),
-                rhs_scale=scales[:],
-                start=(done[b] == 0),
-                stop=(done[b] == NB - 1),
-            )
-            done[b] += 1
+            for k in range(2):
+                b = 2 * q + k
+                if b not in acc:
+                    acc[b] = accps.tile([P, BLK], F32, name="acc")
+                    done[b] = 0
+                nc.tensor.matmul_mx(
+                    out=acc[b][:],
+                    lhsT=sup_codes[:, c, :].bitcast(FP8X4),
+                    lhsT_scale=sup_scales[:, c, :],
+                    rhs=codes[:, k * BLK : (k + 1) * BLK].bitcast(FP8X4),
+                    rhs_scale=scales[:, k * BLK : (k + 1) * BLK],
+                    start=(done[b] == 0),
+                    stop=(done[b] == NB - 1),
+                )
+                done[b] += 1
 
-        def close(b):
+        def close(b, engine):
             o_t = opool.tile([P, BLK], F32, name="o_t")
-            nc.scalar.copy(out=o_t[:], in_=acc[b][:])
-            tq = misc.tile([P, 4, F2], F32, name="tq", tag="tp")
+            if engine == "V":
+                nc.vector.tensor_copy(out=o_t[:], in_=acc[b][:])
+            else:
+                nc.scalar.copy(out=o_t[:], in_=acc[b][:])
+            tq = misc.tile([P, 4, F2], F32, name="tq", tag="sp" if engine == "V" else "tp")
             for u in range(4):
                 nc.tensor.transpose(tq[:, u, :], o_t[:, P * u : P * u + P], ident[:])
             o_s = opool.tile([P, 4, F2], F32, name="o_s")
-            nc.scalar.copy(out=o_s[:], in_=tq[:])
+            if engine == "V":
+                nc.vector.tensor_copy(out=o_s[:], in_=tq[:])
+            else:
+                nc.scalar.copy(out=o_s[:], in_=tq[:])
             nc.sync.dma_start(out=out_view[b], in_=o_s[:])
 
-        for g in range(3):
-            load_a(0, g)
         load_w()
         load_x(0)
+        for q in (0, 2, 1, 3):
+            load_a(0, q)
         for c in range(NB):
             if c + 1 < NB:
                 load_x(c + 1)
-                for g in range(3):
-                    load_a(c + 1, g)
-            for g in range(3):
-                row_sums(c, g)
+                for q in (0, 2, 1, 3):
+                    load_a(c + 1, q)
+            for q in (0, 2, 1, 3):
+                row_sums(c, q)
             support(c)
-            chain(c)
-            if c < 3:
-                spread(c)
-                for r in range(c):
-                    block(r, 0, c)
-            scale_rows(c, 0, "VVVV", c < 3)
-            for b in range(min(c + 1, 3)):
-                block(c, 0, b)
-        for b in range(3):
-            close(b)
-        for g in (1, 2):
-            b0, nb = GROUPS[g]
-            for b in range(b0, b0 + nb):
-                spread(b)
-            for c in range(NB):
-                load_a(c, g)
-                scale_rows(c, g, "SSSS", False)
-                for b in range(b0, b0 + nb):
-                    block(c, g, b)
-            for b in range(b0, b0 + nb):
-                close(b)
+            with tc.high_priority():
+                chain(c)
+            for b in range(4):
+                if S_ROUND0[b] == "G" and c == b:
+                    spread_sbuf(b)
+            if c == 1:
+                unit(0, 0, T1_ROUND0, S_ROUND0[0:2])
+                unit(1, 0, T1_ROUND0, S_ROUND0[0:2])
+            elif c == 2:
+                unit(2, 0, T1_ROUND0, S_ROUND0[0:2])
+            elif c == 3:
+                unit(3, 0, T1_ROUND0, S_ROUND0[0:2])
+                for r in range(4):
+                    unit(r, 1, T1_ROUND0, S_ROUND0[2:4])
+            elif c > 3:
+                unit(c, 0, T1_ROUND0, S_ROUND0[0:2])
+                unit(c, 1, T1_ROUND0, S_ROUND0[2:4])
+        for b in range(4):
+            if S_ROUND1[b] == "G":
+                spread_sbuf(4 + b)
+        for b in range(4):
+            close(b, "S")
+        for c in range(NB):
+            for q in (2, 3):
+                load_a(c, q)
+                unit(c, q, T1_ROUND1, S_ROUND1[2 * q - 4 : 2 * q - 2])
+        close(4, "S")
+        close(5, "S")
+        close(6, "S")
+        close(7, "V")

@@ -21,9 +21,9 @@ QW = 1024
 SLOPE = 0.2
 FLOPS = 2 * C * F1 * F2 + 2 * C * C * F2
 
-V_SUMS = {(0, 2), (0, 3), (1, 2), (1, 3), (2, 3), (3, 3), (4, 3), (5, 3)}
-T1_ROUND0 = "GGGG"
-T1_ROUND1 = "SSSS"
+V_SUMS = {(0, 3), (0, 2), (1, 3), (1, 2), (1, 1), (1, 0), (2, 3), (3, 3), (4, 3), (4, 2)}
+T1_ROUND0 = "GGSGGGGG"
+T1_ROUND1 = "SSSSGSSS"
 S_ROUND0 = "VVVV"
 S_ROUND1 = "VVVG"
 A_BUFS = 13
@@ -32,7 +32,7 @@ A_BUFS = 13
 def tile_gcnresnet_pa_t_kernel(tc, x_pre, A, W_gc2, out):
     nc = tc.nc
     a_view = A.rearrange("(c p t) i -> c p t i", p=P, t=4)
-    x_view = x_pre.rearrange("(c p t) k -> c p t k", p=P, t=4)
+    x_view = x_pre.rearrange("(cc h p t) k -> cc p h t k", h=2, p=P, t=4)
     out_view = out.rearrange("(b u p) f -> b p u f", u=4, p=P)
 
     with ExitStack() as ctx:
@@ -64,7 +64,7 @@ def tile_gcnresnet_pa_t_kernel(tc, x_pre, A, W_gc2, out):
         a_tiles = {}
 
         def load_a(c, q):
-            t = apool.tile([P, 4, QW], BF16, name="aq")
+            t = apool.tile([P, 4, QW], BF16, name="aq", tag="aq")
             nc.sync.dma_start(out=t[:], in_=a_view[c][:, :, q * QW : (q + 1) * QW])
             a_tiles[(c, q)] = t
 
@@ -85,17 +85,18 @@ def tile_gcnresnet_pa_t_kernel(tc, x_pre, A, W_gc2, out):
 
         x_tiles = {}
 
-        def load_x(c):
-            x_raw = xpool.tile([P, 4, F1], BF16, name="x_raw")
-            nc.sync.dma_start(out=x_raw[:], in_=x_view[c])
-            x_tiles[c] = x_raw
+        def load_x(cc):
+            x_raw = apool.tile([P, 2, 4, F1], BF16, name="x_raw", tag="aq")
+            nc.sync.dma_start(out=x_raw[:], in_=x_view[cc])
+            x_tiles[2 * cc] = x_raw[:, 0]
+            x_tiles[2 * cc + 1] = x_raw[:, 1]
 
         def support(c):
-            x_words = x_tiles[c][:].bitcast(F32)
-            x_grp = x1pool.tile([P, BLK, 4], BF16, name="x_grp", align_bytes=64)
+            x_words = x_tiles[c].bitcast(F32)
+            x_grp = xpool.tile([P, BLK, 4], BF16, name="x_grp", align_bytes=64)
             x_grp_w = x_grp[:].bitcast(F32)
             for half in range(2):
-                tp = misc.tile([P, 2, 2, P], F32, name="tp", tag="tp")
+                tp = dpsum.tile([P, 2, 2, P], F32, name="tp", tag="dbc")
                 for tt in range(2):
                     for u in range(2):
                         nc.tensor.transpose(
@@ -109,8 +110,8 @@ def tile_gcnresnet_pa_t_kernel(tc, x_pre, A, W_gc2, out):
             h_grp = xpool.tile([P, 4 * BLK], BF16, name="h_grp", align_bytes=64)
             nc.vector.tensor_scalar(out=h_grp[:], in0=x_flat, scalar1=SLOPE, scalar2=None, op0=ALU.mult)
             nc.vector.tensor_tensor(out=h_grp[:], in0=x_flat, in1=h_grp[:], op=ALU.max)
-            h_codes = x1pool.tile([P, BLK], U32, name="h_codes", align_bytes=64)
-            h_scales = x1pool.tile([P, BLK], U8, name="h_scales", align_bytes=64)
+            h_codes = xpool.tile([P, BLK], U32, name="h_codes", align_bytes=64)
+            h_scales = xpool.tile([P, BLK], U8, name="h_scales", align_bytes=64)
             nc.vector.quantize_mx(out=h_codes[:].bitcast(FP8X4), scales=h_scales[:], in_=h_grp[:])
             sp = misc.tile([P, 4, F2], F32, name="sp", tag="sp")
             for t in range(4):
@@ -213,7 +214,7 @@ def tile_gcnresnet_pa_t_kernel(tc, x_pre, A, W_gc2, out):
                 b = 2 * q + k
                 lo = k * BLK
                 if s_engines[k] == "V":
-                    t_d = dpsum.tile([P, BLK], F32, name="dbc")
+                    t_d = dpsum.tile([P, BLK], F32, name="dbc", tag="dbc")
                     spread(t_d, b)
                     nc.vector.tensor_tensor(
                         out=grp[:, lo : lo + BLK, :].rearrange("p (c i) t -> p c t i", i=4),
@@ -267,43 +268,47 @@ def tile_gcnresnet_pa_t_kernel(tc, x_pre, A, W_gc2, out):
             nc.sync.dma_start(out=out_view[b], in_=o_s[:])
 
         load_w()
-        load_x(0)
+        for cc in range(4):
+            load_x(cc)
         for q in (0, 2, 1, 3):
             load_a(0, q)
         for c in range(NB):
+            support(c)
+
+        def unit0(r, q):
+            unit(r, q, T1_ROUND0[4 * q : 4 * q + 4], S_ROUND0[2 * q : 2 * q + 2])
+
+        for c in range(NB):
             if c + 1 < NB:
-                load_x(c + 1)
                 for q in (0, 2, 1, 3):
                     load_a(c + 1, q)
             for q in (0, 2, 1, 3):
                 row_sums(c, q)
-            support(c)
             with tc.high_priority():
                 chain(c)
-            for b in range(4):
-                if S_ROUND0[b] == "G" and c == b:
-                    spread_sbuf(b)
+                if c < 4 and S_ROUND0[c] == "G":
+                    spread_sbuf(c)
+            if c >= 4 and S_ROUND1[c - 4] == "G":
+                spread_sbuf(c)
             if c == 1:
-                unit(0, 0, T1_ROUND0, S_ROUND0[0:2])
-                unit(1, 0, T1_ROUND0, S_ROUND0[0:2])
+                unit0(0, 0)
+                unit0(1, 0)
             elif c == 2:
-                unit(2, 0, T1_ROUND0, S_ROUND0[0:2])
+                unit0(2, 0)
             elif c == 3:
-                unit(3, 0, T1_ROUND0, S_ROUND0[0:2])
+                unit0(3, 0)
                 for r in range(4):
-                    unit(r, 1, T1_ROUND0, S_ROUND0[2:4])
+                    unit0(r, 1)
             elif c > 3:
-                unit(c, 0, T1_ROUND0, S_ROUND0[0:2])
-                unit(c, 1, T1_ROUND0, S_ROUND0[2:4])
-        for b in range(4):
-            if S_ROUND1[b] == "G":
-                spread_sbuf(4 + b)
+                unit0(c, 0)
+                unit0(c, 1)
         for b in range(4):
             close(b, "S")
         for c in range(NB):
             for q in (2, 3):
                 load_a(c, q)
-                unit(c, q, T1_ROUND1, S_ROUND1[2 * q - 4 : 2 * q - 2])
+            for q in (2, 3):
+                unit(c, q, T1_ROUND1[4 * q - 8 : 4 * q - 4], S_ROUND1[2 * q - 4 : 2 * q - 2])
         close(4, "S")
         close(5, "S")
         close(6, "S")

@@ -12,304 +12,276 @@ ALU = mybir.AluOpType
 ACT = mybir.ActivationFunctionType
 
 P = 128
-C = 4096
-F1 = 512
-F2 = 128
-NB = 8
-BLK = 512
-QW = 1024
+PACK = 4
+NODES = 4096
+FEAT_IN = 512
+FEAT_OUT = 128
 SLOPE = 0.2
-FLOPS = 2 * C * F1 * F2 + 2 * C * C * F2
+BLOCK = P * PACK
+N_BLOCKS = NODES // BLOCK
+QUARTER = 2 * BLOCK
+N_QUARTERS = NODES // QUARTER
+ROUND_QUARTERS = 2
+RUN = 4
+FLOPS = 2 * NODES * FEAT_IN * FEAT_OUT + 2 * NODES * NODES * FEAT_OUT
 
-V_SUMS = {(0, 3), (0, 2), (1, 3), (1, 2), (1, 1), (1, 0), (2, 3), (3, 3), (4, 3), (4, 2)}
-T1_ROUND0 = "GGSGGGGG"
-T1_ROUND1 = "SSSSGSSS"
-S_ROUND0 = "VVVV"
-S_ROUND1 = "VVVG"
-A_BUFS = 13
+VECTOR_SUM_ROW_BLOCKS = 4
+VECTOR_SUM_QUARTERS = (2, 3)
+GPSIMD_COLUMN_BLOCK = N_BLOCKS - 1
+A_TILES = 13
 
 
 def tile_gcnresnet_pa_t_kernel(tc, x_pre, A, W_gc2, out):
     nc = tc.nc
-    a_view = A.rearrange("(c p t) i -> c p t i", p=P, t=4)
-    x_view = x_pre.rearrange("(cc h p t) k -> cc p h t k", h=2, p=P, t=4)
-    out_view = out.rearrange("(b u p) f -> b p u f", u=4, p=P)
+    a_view = A.rearrange("(c p t) i -> c p t i", p=P, t=PACK)
+    x_view = x_pre.rearrange("(m h p t) k -> m p h t k", h=2, p=P, t=PACK)
+    out_view = out.rearrange("(b u p) f -> b p u f", u=BLOCK // P, p=P)
 
     with ExitStack() as ctx:
-        const = ctx.enter_context(tc.tile_pool(name="const", bufs=1))
-        apool = ctx.enter_context(tc.tile_pool(name="apool", bufs=A_BUFS))
-        t1pool = ctx.enter_context(tc.tile_pool(name="t1pool", bufs=3))
-        gpool = ctx.enter_context(tc.tile_pool(name="gpool", bufs=2))
-        cpool = ctx.enter_context(tc.tile_pool(name="cpool", bufs=3))
-        xpool = ctx.enter_context(tc.tile_pool(name="xpool", bufs=2))
-        x1pool = ctx.enter_context(tc.tile_pool(name="x1pool", bufs=1))
-        small = ctx.enter_context(tc.tile_pool(name="small", bufs=2))
-        opool = ctx.enter_context(tc.tile_pool(name="opool", bufs=2))
-        dpsum = ctx.enter_context(tc.psum_pool(name="dpsum", bufs=2))
-        accps = ctx.enter_context(tc.psum_pool(name="accps", bufs=4))
-        misc = ctx.enter_context(tc.psum_pool(name="misc", bufs=1))
+        keep = ctx.enter_context(tc.tile_pool(name="keep", bufs=1))
+        a_pool = ctx.enter_context(tc.tile_pool(name="a_pool", bufs=A_TILES))
+        scaled_pool = ctx.enter_context(tc.tile_pool(name="scaled_pool", bufs=3))
+        grouped_pool = ctx.enter_context(tc.tile_pool(name="grouped_pool", bufs=2))
+        codes_pool = ctx.enter_context(tc.tile_pool(name="codes_pool", bufs=3))
+        first_pool = ctx.enter_context(tc.tile_pool(name="first_pool", bufs=2))
+        sums_pool = ctx.enter_context(tc.tile_pool(name="sums_pool", bufs=2))
+        out_pool = ctx.enter_context(tc.tile_pool(name="out_pool", bufs=2))
+        spread_psum = ctx.enter_context(tc.psum_pool(name="spread_psum", bufs=2))
+        acc_psum = ctx.enter_context(tc.psum_pool(name="acc_psum", bufs=ROUND_QUARTERS * 2))
+        misc_psum = ctx.enter_context(tc.psum_pool(name="misc_psum", bufs=1))
 
-        ident = const.tile([P, P], F32, name="ident")
-        make_identity(nc, ident[:])
-        neghalf = const.tile([P, 4], F32, name="neghalf")
-        nc.gpsimd.memset(neghalf[:], -0.5)
-        rs_s = const.tile([P, NB, 4, 4], F32, name="rs_s")
-        rs_v = const.tile([P, NB, 4, 4], F32, name="rs_v")
-        dinv = const.tile([P, NB, 4], F32, name="dinv")
-        sup_codes = const.tile([P, NB, F2], U32, name="sup_codes", align_bytes=64)
-        sup_scales = const.tile([P, NB, F2], U8, name="sup_scales", align_bytes=64)
-        w_codes = const.tile([P, F2], U32, name="w_codes", align_bytes=64)
-        w_scales = const.tile([P, F2], U8, name="w_scales", align_bytes=64)
+        identity = keep.tile([P, P], F32, name="identity")
+        make_identity(nc, identity[:])
+        minus_half = keep.tile([P, PACK], F32, name="minus_half")
+        nc.gpsimd.memset(minus_half[:], -0.5)
+        sums_scalar = keep.tile([P, N_BLOCKS, N_QUARTERS, PACK], F32, name="sums_scalar")
+        sums_vector = keep.tile([P, N_BLOCKS, N_QUARTERS, PACK], F32, name="sums_vector")
+        d = keep.tile([P, N_BLOCKS, PACK], F32, name="d")
+        d_gpsimd = keep.tile([P, BLOCK], F32, name="d_gpsimd")
+        support_codes = keep.tile([P, N_BLOCKS, FEAT_OUT], U32, name="support_codes", align_bytes=64)
+        support_scales = keep.tile([P, N_BLOCKS, FEAT_OUT], U8, name="support_scales", align_bytes=64)
+        w_codes = keep.tile([P, FEAT_OUT], U32, name="w_codes", align_bytes=64)
+        w_scales = keep.tile([P, FEAT_OUT], U8, name="w_scales", align_bytes=64)
 
-        a_tiles = {}
+        def load_quarter(c, q):
+            tile = a_pool.tile([P, PACK, QUARTER], BF16, name="a_quarter", tag="a")
+            nc.sync.dma_start(out=tile[:], in_=a_view[c][:, :, q * QUARTER : (q + 1) * QUARTER])
+            return tile
 
-        def load_a(c, q):
-            t = apool.tile([P, 4, QW], BF16, name="aq", tag="aq")
-            nc.sync.dma_start(out=t[:], in_=a_view[c][:, :, q * QW : (q + 1) * QW])
-            a_tiles[(c, q)] = t
 
-        def load_w():
-            w_raw = const.tile([P, 4, F2], BF16, name="w_raw")
+        def quantise_w():
+            w_rows = keep.tile([P, PACK, FEAT_OUT], BF16, name="w_rows")
             for u in range(2):
                 nc.sync.dma_start(
-                    out=w_raw[:, 2 * u : 2 * u + 2, :],
+                    out=w_rows[:, 2 * u : 2 * u + 2, :],
                     in_=W_gc2[256 * u : 256 * u + 256, :].rearrange("(q e) f -> q e f", e=2),
                 )
-            w_grp = const.tile([P, F2, 4], BF16, name="w_grp", align_bytes=64)
-            nc.vector.tensor_copy(out=w_grp[:], in_=w_raw[:].rearrange("q s f -> q f s"))
+            w_grouped = keep.tile([P, FEAT_OUT, PACK], BF16, name="w_grouped", align_bytes=64)
+            nc.vector.tensor_copy(out=w_grouped[:], in_=w_rows[:].rearrange("q s f -> q f s"))
             nc.vector.quantize_mx(
                 out=w_codes[:].bitcast(FP8X4),
                 scales=w_scales[:],
-                in_=w_grp[:].rearrange("q f s -> q (f s)"),
+                in_=w_grouped[:].rearrange("q f s -> q (f s)"),
             )
 
-        x_tiles = {}
-
-        def load_x(cc):
-            x_raw = apool.tile([P, 2, 4, F1], BF16, name="x_raw", tag="aq")
-            nc.sync.dma_start(out=x_raw[:], in_=x_view[cc])
-            x_tiles[2 * cc] = x_raw[:, 0]
-            x_tiles[2 * cc + 1] = x_raw[:, 1]
-
-        def support(c):
-            x_words = x_tiles[c].bitcast(F32)
-            x_grp = xpool.tile([P, BLK, 4], BF16, name="x_grp", align_bytes=64)
-            x_grp_w = x_grp[:].bitcast(F32)
+        def support_of_row_block(c, x_rows):
+            x_words = x_rows.bitcast(F32)
+            x_grouped = first_pool.tile([P, BLOCK, PACK], BF16, name="x_grouped", align_bytes=64)
+            x_grouped_words = x_grouped[:].bitcast(F32)
             for half in range(2):
-                tp = dpsum.tile([P, 2, 2, P], F32, name="tp", tag="dbc")
-                for tt in range(2):
+                turned = spread_psum.tile([P, 2, 2, P], F32, name="turned", tag="spread")
+                for t in range(2):
                     for u in range(2):
                         nc.tensor.transpose(
-                            tp[:, tt, u, :], x_words[:, 2 * half + tt, P * u : P * u + P], ident[:]
+                            turned[:, t, u, :], x_words[:, 2 * half + t, P * u : P * u + P], identity[:]
                         )
                 nc.scalar.copy(
-                    out=x_grp_w[:, 256 * half : 256 * half + 256, :].rearrange("q (t p) u -> q t p u", t=2),
-                    in_=tp[:].rearrange("q t u p -> q t p u"),
+                    out=x_grouped_words[:, 2 * P * half : 2 * P * (half + 1), :].rearrange(
+                        "q (t p) u -> q t p u", t=2
+                    ),
+                    in_=turned[:].rearrange("q t u p -> q t p u"),
                 )
-            x_flat = x_grp[:].rearrange("q n s -> q (n s)")
-            h_grp = xpool.tile([P, 4 * BLK], BF16, name="h_grp", align_bytes=64)
-            nc.vector.tensor_scalar(out=h_grp[:], in0=x_flat, scalar1=SLOPE, scalar2=None, op0=ALU.mult)
-            nc.vector.tensor_tensor(out=h_grp[:], in0=x_flat, in1=h_grp[:], op=ALU.max)
-            h_codes = xpool.tile([P, BLK], U32, name="h_codes", align_bytes=64)
-            h_scales = xpool.tile([P, BLK], U8, name="h_scales", align_bytes=64)
-            nc.vector.quantize_mx(out=h_codes[:].bitcast(FP8X4), scales=h_scales[:], in_=h_grp[:])
-            sp = misc.tile([P, 4, F2], F32, name="sp", tag="sp")
-            for t in range(4):
+            x_flat = x_grouped[:].rearrange("q n s -> q (n s)")
+            h_grouped = first_pool.tile([P, BLOCK * PACK], BF16, name="h_grouped", align_bytes=64)
+            nc.vector.tensor_scalar(out=h_grouped[:], in0=x_flat, scalar1=SLOPE, scalar2=None, op0=ALU.mult)
+            nc.vector.tensor_tensor(out=h_grouped[:], in0=x_flat, in1=h_grouped[:], op=ALU.max)
+            h_codes = first_pool.tile([P, BLOCK], U32, name="h_codes", align_bytes=64)
+            h_scales = first_pool.tile([P, BLOCK], U8, name="h_scales", align_bytes=64)
+            nc.vector.quantize_mx(out=h_codes[:].bitcast(FP8X4), scales=h_scales[:], in_=h_grouped[:])
+            product = misc_psum.tile([P, PACK, FEAT_OUT], F32, name="product", tag="product")
+            for t in range(PACK):
                 nc.tensor.matmul_mx(
-                    out=sp[:, t, :],
-                    lhsT=h_codes[:, P * t : P * t + P].bitcast(FP8X4),
-                    lhsT_scale=h_scales[:, P * t : P * t + P],
+                    out=product[:, t, :],
+                    lhsT=h_codes[:, P * t : P * (t + 1)].bitcast(FP8X4),
+                    lhsT_scale=h_scales[:, P * t : P * (t + 1)],
                     rhs=w_codes[:].bitcast(FP8X4),
                     rhs_scale=w_scales[:],
                     start=True,
                     stop=True,
                 )
-            s_grp = x1pool.tile([P, F2, 4], BF16, name="s_grp", align_bytes=64)
-            nc.scalar.copy(out=s_grp[:], in_=sp[:].rearrange("p t f -> p f t"))
+            s_grouped = first_pool.tile([P, FEAT_OUT, PACK], BF16, name="s_grouped", align_bytes=64)
+            nc.scalar.copy(out=s_grouped[:], in_=product[:].rearrange("p t f -> p f t"))
             nc.vector.quantize_mx(
-                out=sup_codes[:, c, :].bitcast(FP8X4),
-                scales=sup_scales[:, c, :],
-                in_=s_grp[:].rearrange("p f t -> p (f t)"),
+                out=support_codes[:, c, :].bitcast(FP8X4),
+                scales=support_scales[:, c, :],
+                in_=s_grouped[:].rearrange("p f t -> p (f t)"),
             )
 
-        def row_sums(c, q):
-            t_a = a_tiles[(c, q)]
-            for t in range(4):
-                if (c, q) in V_SUMS:
+
+        def vector_sums(c, q):
+            return c < VECTOR_SUM_ROW_BLOCKS and q in VECTOR_SUM_QUARTERS
+
+        def sum_rows(c, q, a_quarter):
+            for t in range(PACK):
+                row = a_quarter[:, t, :]
+                if vector_sums(c, q):
                     nc.vector.tensor_scalar(
-                        out=t_a[:, t, :],
-                        in0=t_a[:, t, :],
+                        out=row,
+                        in0=row,
                         scalar1=1.0,
                         scalar2=None,
                         op0=ALU.mult,
                         op1=ALU.add,
-                        accum_out=rs_v[:, c, q, t : t + 1],
+                        accum_out=sums_vector[:, c, q, t : t + 1],
                     )
                 else:
-                    nc.scalar.activation(
-                        out=t_a[:, t, :], in_=t_a[:, t, :], func=ACT.Copy, accum_out=rs_s[:, c, q, t : t + 1]
-                    )
+                    nc.scalar.activation(out=row, in_=row, func=ACT.Copy, accum_out=sums_scalar[:, c, q, t : t + 1])
 
-        def part(c, q):
-            return rs_v[:, c, q, :] if (c, q) in V_SUMS else rs_s[:, c, q, :]
+        def quarter_sum(c, q):
+            return sums_vector[:, c, q, :] if vector_sums(c, q) else sums_scalar[:, c, q, :]
 
-        def chain(c):
-            s01 = small.tile([P, 4], F32, name="s01")
-            nc.gpsimd.tensor_tensor(out=s01[:], in0=part(c, 0), in1=part(c, 1), op=ALU.add)
-            s23 = small.tile([P, 4], F32, name="s23")
-            nc.gpsimd.tensor_tensor(out=s23[:], in0=part(c, 2), in1=part(c, 3), op=ALU.add)
-            s_all = small.tile([P, 4], F32, name="s_all")
-            nc.gpsimd.tensor_tensor(out=s_all[:], in0=s01[:], in1=s23[:], op=ALU.add)
-            nc.gpsimd.tensor_tensor(out=dinv[:, c, :], in0=s_all[:], in1=neghalf[:], op=ALU.pow)
+        def inverse_root_of_row_sums(c):
+            left = sums_pool.tile([P, PACK], F32, name="left")
+            nc.gpsimd.tensor_tensor(out=left[:], in0=quarter_sum(c, 0), in1=quarter_sum(c, 1), op=ALU.add)
+            right = sums_pool.tile([P, PACK], F32, name="right")
+            nc.gpsimd.tensor_tensor(out=right[:], in0=quarter_sum(c, 2), in1=quarter_sum(c, 3), op=ALU.add)
+            whole = sums_pool.tile([P, PACK], F32, name="whole")
+            nc.gpsimd.tensor_tensor(out=whole[:], in0=left[:], in1=right[:], op=ALU.add)
+            nc.gpsimd.tensor_tensor(out=d[:, c, :], in0=whole[:], in1=minus_half[:], op=ALU.pow)
 
-        def spread(t_d, b):
-            for t in range(4):
+        def spread_d(bank, b):
+            for t in range(PACK):
                 nc.tensor.transpose(
-                    t_d[:].rearrange("m (q t) -> m t q", t=4)[:, t, :],
-                    dinv[:, b, t : t + 1].to_broadcast([P, P]),
-                    ident[:],
+                    bank[:].rearrange("m (q t) -> m t q", t=PACK)[:, t, :],
+                    d[:, b, t : t + 1].to_broadcast([P, P]),
+                    identity[:],
                 )
 
-        dbc_sb = {}
 
-        def spread_sbuf(b):
-            tq = misc.tile([P, BLK], F32, name="td", tag="tp")
-            spread(tq, b)
-            dbc_sb[b] = const.tile([P, BLK], F32, name="dbc_sb%d" % b)
-            nc.scalar.copy(out=dbc_sb[b][:], in_=tq[:])
+        acc = {}
+        passes = {}
 
-        t1_tiles = {}
-
-        def scale_rows(c, q, engines):
-            t_a = a_tiles[(c, q)]
-            t1 = t1pool.tile([P, 4, QW], F32, name="t1")
-            for t in range(4):
-                if engines[t] == "V":
-                    nc.vector.tensor_scalar(
-                        out=t1[:, t, :], in0=t_a[:, t, :], scalar1=dinv[:, c, t : t + 1], scalar2=None, op0=ALU.mult
-                    )
-                elif engines[t] == "G":
+        def unit(c, q, a_quarter, scale_on_gpsimd):
+            scaled = scaled_pool.tile([P, PACK, QUARTER], F32, name="scaled")
+            for t in range(PACK):
+                if scale_on_gpsimd:
                     nc.gpsimd.tensor_scalar(
-                        out=t1[:, t, :],
-                        in0=t_a[:, t, :],
-                        scalar1=dinv[:, c, t : t + 1],
+                        out=scaled[:, t, :],
+                        in0=a_quarter[:, t, :],
+                        scalar1=d[:, c, t : t + 1],
                         scalar2=0.0,
                         op0=ALU.mult,
                         op1=ALU.add,
                     )
                 else:
                     nc.scalar.activation(
-                        out=t1[:, t, :], in_=t_a[:, t, :], func=ACT.Copy, scale=dinv[:, c, t : t + 1]
+                        out=scaled[:, t, :], in_=a_quarter[:, t, :], func=ACT.Copy, scale=d[:, c, t : t + 1]
                     )
-            t1_tiles[(c, q)] = t1
-
-        acc = {}
-        done = {}
-
-        def unit(c, q, t1_engines, s_engines):
-            scale_rows(c, q, t1_engines)
-            t1 = t1_tiles[(c, q)]
-            grp = gpool.tile([P, 2 * BLK, 4], BF16, name="grp", align_bytes=64)
+            grouped = grouped_pool.tile([P, QUARTER, PACK], BF16, name="grouped", align_bytes=64)
             for k in range(2):
                 b = 2 * q + k
-                lo = k * BLK
-                if s_engines[k] == "V":
-                    t_d = dpsum.tile([P, BLK], F32, name="dbc", tag="dbc")
-                    spread(t_d, b)
-                    nc.vector.tensor_tensor(
-                        out=grp[:, lo : lo + BLK, :].rearrange("p (c i) t -> p c t i", i=4),
-                        in0=t1[:, :, lo : lo + BLK].rearrange("p t (c i) -> p c t i", i=4),
-                        in1=t_d[:].rearrange("p (c i) -> p c i", i=4).unsqueeze(2).to_broadcast([P, BLK // 4, 4, 4]),
-                        op=ALU.mult,
-                    )
-                else:
-                    for z in range(4):
+                lo = k * BLOCK
+                if b == GPSIMD_COLUMN_BLOCK:
+                    for i0 in range(lo, lo + BLOCK, P):
                         nc.gpsimd.tensor_tensor(
-                            out=grp[:, lo + P * z : lo + P * z + P, :],
-                            in0=t1[:, :, lo + P * z : lo + P * z + P].rearrange("p t i -> p i t"),
-                            in1=dbc_sb[b][:, P * z : P * z + P].unsqueeze(2).to_broadcast([P, P, 4]),
+                            out=grouped[:, i0 : i0 + P, :],
+                            in0=scaled[:, :, i0 : i0 + P].rearrange("p t i -> p i t"),
+                            in1=d_gpsimd[:, i0 - lo : i0 - lo + P].unsqueeze(2).to_broadcast([P, P, PACK]),
                             op=ALU.mult,
                         )
-            codes = cpool.tile([P, 2 * BLK], U32, name="codes", align_bytes=64)
-            scales = cpool.tile([P, 2 * BLK], U8, name="scales", align_bytes=64)
+                else:
+                    d_bank = spread_psum.tile([P, BLOCK], F32, name="d_bank", tag="spread")
+                    spread_d(d_bank, b)
+                    nc.vector.tensor_tensor(
+                        out=grouped[:, lo : lo + BLOCK, :].rearrange("p (n i) t -> p n t i", i=RUN),
+                        in0=scaled[:, :, lo : lo + BLOCK].rearrange("p t (n i) -> p n t i", i=RUN),
+                        in1=d_bank[:]
+                        .rearrange("p (n i) -> p n i", i=RUN)
+                        .unsqueeze(2)
+                        .to_broadcast([P, BLOCK // RUN, PACK, RUN]),
+                        op=ALU.mult,
+                    )
+            codes = codes_pool.tile([P, QUARTER], U32, name="codes", align_bytes=64)
+            scales = codes_pool.tile([P, QUARTER], U8, name="scales", align_bytes=64)
             nc.vector.quantize_mx(
-                out=codes[:].bitcast(FP8X4), scales=scales[:], in_=grp[:].rearrange("p i t -> p (i t)")
+                out=codes[:].bitcast(FP8X4), scales=scales[:], in_=grouped[:].rearrange("p i t -> p (i t)")
             )
             for k in range(2):
                 b = 2 * q + k
                 if b not in acc:
-                    acc[b] = accps.tile([P, BLK], F32, name="acc")
-                    done[b] = 0
+                    acc[b] = acc_psum.tile([P, BLOCK], F32, name="acc")
+                    passes[b] = 0
                 nc.tensor.matmul_mx(
                     out=acc[b][:],
-                    lhsT=sup_codes[:, c, :].bitcast(FP8X4),
-                    lhsT_scale=sup_scales[:, c, :],
-                    rhs=codes[:, k * BLK : (k + 1) * BLK].bitcast(FP8X4),
-                    rhs_scale=scales[:, k * BLK : (k + 1) * BLK],
-                    start=(done[b] == 0),
-                    stop=(done[b] == NB - 1),
+                    lhsT=support_codes[:, c, :].bitcast(FP8X4),
+                    lhsT_scale=support_scales[:, c, :],
+                    rhs=codes[:, k * BLOCK : (k + 1) * BLOCK].bitcast(FP8X4),
+                    rhs_scale=scales[:, k * BLOCK : (k + 1) * BLOCK],
+                    start=(passes[b] == 0),
+                    stop=(passes[b] == N_BLOCKS - 1),
                 )
-                done[b] += 1
+                passes[b] += 1
 
-        def close(b, engine):
-            o_t = opool.tile([P, BLK], F32, name="o_t")
-            if engine == "V":
-                nc.vector.tensor_copy(out=o_t[:], in_=acc[b][:])
-            else:
-                nc.scalar.copy(out=o_t[:], in_=acc[b][:])
-            tq = misc.tile([P, 4, F2], F32, name="tq", tag="sp" if engine == "V" else "tp")
-            for u in range(4):
-                nc.tensor.transpose(tq[:, u, :], o_t[:, P * u : P * u + P], ident[:])
-            o_s = opool.tile([P, 4, F2], F32, name="o_s")
-            if engine == "V":
-                nc.vector.tensor_copy(out=o_s[:], in_=tq[:])
-            else:
-                nc.scalar.copy(out=o_s[:], in_=tq[:])
-            nc.sync.dma_start(out=out_view[b], in_=o_s[:])
+        def store_column_block(b, copy, tag):
+            out_t = out_pool.tile([P, BLOCK], F32, name="out_t")
+            copy(out=out_t[:], in_=acc[b][:])
+            rows_psum = misc_psum.tile([P, BLOCK // P, FEAT_OUT], F32, name="rows_psum", tag=tag)
+            for u in range(BLOCK // P):
+                nc.tensor.transpose(rows_psum[:, u, :], out_t[:, P * u : P * (u + 1)], identity[:])
+            rows = out_pool.tile([P, BLOCK // P, FEAT_OUT], F32, name="rows")
+            copy(out=rows[:], in_=rows_psum[:])
+            nc.sync.dma_start(out=out_view[b], in_=rows[:])
 
-        load_w()
-        for cc in range(4):
-            load_x(cc)
-        for q in (0, 2, 1, 3):
-            load_a(0, q)
-        for c in range(NB):
-            support(c)
 
-        def unit0(r, q):
-            unit(r, q, T1_ROUND0[4 * q : 4 * q + 4], S_ROUND0[2 * q : 2 * q + 2])
+        quantise_w()
+        x_tiles = []
+        for m in range(N_BLOCKS // 2):
+            x_pair = a_pool.tile([P, 2, PACK, FEAT_IN], BF16, name="x_pair", tag="a")
+            nc.sync.dma_start(out=x_pair[:], in_=x_view[m])
+            x_tiles.append(x_pair)
+        load_order = (0, 2, 1, 3)
+        a_tiles = {}
+        for q in load_order:
+            a_tiles[(0, q)] = load_quarter(0, q)
+        for c in range(N_BLOCKS):
+            support_of_row_block(c, x_tiles[c // 2][:, c % 2])
 
-        for c in range(NB):
-            if c + 1 < NB:
-                for q in (0, 2, 1, 3):
-                    load_a(c + 1, q)
-            for q in (0, 2, 1, 3):
-                row_sums(c, q)
+        for c in range(N_BLOCKS):
+            if c + 1 < N_BLOCKS:
+                for q in load_order:
+                    a_tiles[(c + 1, q)] = load_quarter(c + 1, q)
+            for q in load_order:
+                sum_rows(c, q, a_tiles[(c, q)])
             with tc.high_priority():
-                chain(c)
-                if c < 4 and S_ROUND0[c] == "G":
-                    spread_sbuf(c)
-            if c >= 4 and S_ROUND1[c - 4] == "G":
-                spread_sbuf(c)
-            if c == 1:
-                unit0(0, 0)
-                unit0(1, 0)
-            elif c == 2:
-                unit0(2, 0)
-            elif c == 3:
-                unit0(3, 0)
-                for r in range(4):
-                    unit0(r, 1)
-            elif c > 3:
-                unit0(c, 0)
-                unit0(c, 1)
-        for b in range(4):
-            close(b, "S")
-        for c in range(NB):
-            for q in (2, 3):
-                load_a(c, q)
-            for q in (2, 3):
-                unit(c, q, T1_ROUND1[4 * q - 8 : 4 * q - 4], S_ROUND1[2 * q - 4 : 2 * q - 2])
-        close(4, "S")
-        close(5, "S")
-        close(6, "S")
-        close(7, "V")
+                inverse_root_of_row_sums(c)
+            if c == GPSIMD_COLUMN_BLOCK:
+                d_turned = misc_psum.tile([P, BLOCK], F32, name="d_turned", tag="rows")
+                spread_d(d_turned, c)
+                nc.scalar.copy(out=d_gpsimd[:], in_=d_turned[:])
+            for q in range(ROUND_QUARTERS):
+                last_needed = 2 * q + 1
+                if c >= last_needed:
+                    first_ready = 0 if c == last_needed else c
+                    for r in range(first_ready, c + 1):
+                        unit(r, q, a_tiles[(r, q)], scale_on_gpsimd=True)
+        for b in range(2 * ROUND_QUARTERS):
+            store_column_block(b, nc.scalar.copy, "rows")
+
+        for c in range(N_BLOCKS):
+            for q in range(ROUND_QUARTERS, N_QUARTERS):
+                a_tiles[(c, q)] = load_quarter(c, q)
+            for q in range(ROUND_QUARTERS, N_QUARTERS):
+                unit(c, q, a_tiles[(c, q)], scale_on_gpsimd=False)
+        for b in range(2 * ROUND_QUARTERS, N_BLOCKS - 1):
+            store_column_block(b, nc.scalar.copy, "rows")
+        store_column_block(N_BLOCKS - 1, nc.vector.tensor_copy, "product")

@@ -29,6 +29,9 @@ VECTOR_SUM_ROW_BLOCKS = 4
 VECTOR_SUM_QUARTERS = (2, 3)
 GPSIMD_COLUMN_BLOCK = N_BLOCKS - 1
 A_TILES = 13
+FOLDED_ROW_BLOCKS = (4, 5, 6)
+FOLDED_ROW = PACK - 1
+SCALAR_SCALE_ROW_BLOCKS = 4
 
 
 def tile_gcnresnet_pa_t_kernel(tc, x_pre, A, W_gc2, out):
@@ -52,10 +55,15 @@ def tile_gcnresnet_pa_t_kernel(tc, x_pre, A, W_gc2, out):
 
         identity = keep.tile([P, P], F32, name="identity")
         make_identity(nc, identity[:])
+        identity_bf16 = keep.tile([P, P], BF16, name="identity_bf16")
+        make_identity(nc, identity_bf16[:])
+        folds = {}
         minus_half = keep.tile([P, PACK], F32, name="minus_half")
         nc.gpsimd.memset(minus_half[:], -0.5)
+        load_order = (0, 2, 1, 3)
         sums_scalar = keep.tile([P, N_BLOCKS, N_QUARTERS, PACK], F32, name="sums_scalar")
         sums_vector = keep.tile([P, N_BLOCKS, N_QUARTERS, PACK], F32, name="sums_vector")
+        nc.gpsimd.memset(sums_scalar[:], 0.0)
         d = keep.tile([P, N_BLOCKS, PACK], F32, name="d")
         d_gpsimd = keep.tile([P, BLOCK], F32, name="d_gpsimd")
         support_codes = keep.tile([P, N_BLOCKS, FEAT_OUT], U32, name="support_codes", align_bytes=64)
@@ -131,9 +139,31 @@ def tile_gcnresnet_pa_t_kernel(tc, x_pre, A, W_gc2, out):
         def vector_sums(c, q):
             return c < VECTOR_SUM_ROW_BLOCKS and q in VECTOR_SUM_QUARTERS
 
+        def folded(c, t):
+            return c in FOLDED_ROW_BLOCKS and t == FOLDED_ROW
+
         def sum_rows(c, q, a_quarter):
             for t in range(PACK):
+                if folded(c, t):
+                    if q == load_order[0]:
+                        folds[(c, t)] = misc_psum.tile([P, BLOCK], F32, name="fold", tag="product")
+                    for k in range(2):
+                        nc.tensor.matmul(
+                            folds[(c, t)][:],
+                            lhsT=identity_bf16[:],
+                            rhs=a_quarter[:, t, k * BLOCK : (k + 1) * BLOCK],
+                            start=(q == load_order[0] and k == 0),
+                            stop=(q == load_order[-1] and k == 1),
+                        )
+                    if q == load_order[-1]:
+                        junk = sums_pool.tile([P, BLOCK], F32, name="junk")
+                        nc.scalar.activation(
+                            out=junk[:], in_=folds[(c, t)][:], func=ACT.Copy, accum_out=sums_scalar[:, c, 0, t : t + 1]
+                        )
+            for t in range(PACK):
                 row = a_quarter[:, t, :]
+                if folded(c, t):
+                    continue
                 if vector_sums(c, q):
                     nc.vector.tensor_scalar(
                         out=row,
@@ -170,11 +200,16 @@ def tile_gcnresnet_pa_t_kernel(tc, x_pre, A, W_gc2, out):
 
         acc = {}
         passes = {}
+        waiting = []
 
         def unit(c, q, a_quarter, scale_on_gpsimd):
             scaled = scaled_pool.tile([P, PACK, QUARTER], F32, name="scaled")
             for t in range(PACK):
-                if scale_on_gpsimd:
+                if scale_on_gpsimd and t == 0 and c >= SCALAR_SCALE_ROW_BLOCKS:
+                    nc.vector.tensor_scalar(
+                        out=scaled[:, t, :], in0=a_quarter[:, t, :], scalar1=d[:, c, t : t + 1], scalar2=None, op0=ALU.mult
+                    )
+                elif scale_on_gpsimd and t > 0:
                     nc.gpsimd.tensor_scalar(
                         out=scaled[:, t, :],
                         in0=a_quarter[:, t, :],
@@ -211,6 +246,12 @@ def tile_gcnresnet_pa_t_kernel(tc, x_pre, A, W_gc2, out):
                         .to_broadcast([P, BLOCK // RUN, PACK, RUN]),
                         op=ALU.mult,
                     )
+            if waiting:
+                finish()
+            waiting.append((c, q, grouped))
+
+        def finish():
+            c, q, grouped = waiting.pop(0)
             codes = codes_pool.tile([P, QUARTER], U32, name="codes", align_bytes=64)
             scales = codes_pool.tile([P, QUARTER], U8, name="scales", align_bytes=64)
             nc.vector.quantize_mx(
@@ -249,7 +290,6 @@ def tile_gcnresnet_pa_t_kernel(tc, x_pre, A, W_gc2, out):
             x_pair = a_pool.tile([P, 2, PACK, FEAT_IN], BF16, name="x_pair", tag="a")
             nc.sync.dma_start(out=x_pair[:], in_=x_view[m])
             x_tiles.append(x_pair)
-        load_order = (0, 2, 1, 3)
         a_tiles = {}
         for q in load_order:
             a_tiles[(0, q)] = load_quarter(0, q)
@@ -274,6 +314,7 @@ def tile_gcnresnet_pa_t_kernel(tc, x_pre, A, W_gc2, out):
                     first_ready = 0 if c == last_needed else c
                     for r in range(first_ready, c + 1):
                         unit(r, q, a_tiles[(r, q)], scale_on_gpsimd=True)
+        finish()
         for b in range(2 * ROUND_QUARTERS):
             store_column_block(b, nc.scalar.copy, "rows")
 
@@ -282,6 +323,7 @@ def tile_gcnresnet_pa_t_kernel(tc, x_pre, A, W_gc2, out):
                 a_tiles[(c, q)] = load_quarter(c, q)
             for q in range(ROUND_QUARTERS, N_QUARTERS):
                 unit(c, q, a_tiles[(c, q)], scale_on_gpsimd=False)
+        finish()
         for b in range(2 * ROUND_QUARTERS, N_BLOCKS - 1):
             store_column_block(b, nc.scalar.copy, "rows")
         store_column_block(N_BLOCKS - 1, nc.vector.tensor_copy, "product")

@@ -25,13 +25,18 @@ ROUND_QUARTERS = 2
 RUN = 4
 FLOPS = 2 * NODES * FEAT_IN * FEAT_OUT + 2 * NODES * NODES * FEAT_OUT
 
-VECTOR_SUM_ROW_BLOCKS = 4
+TENSOR_SUM_ROW_BLOCKS = (2,3,5,7)
+PIECE = 512
+PIECES = NODES // PIECE
+ROWS_ABREAST = P // PIECES
+SUM_ROWS = 8 * ROWS_ABREAST
+SUM_TILES = 4
+VECTOR_SUM_ROW_BLOCKS = (0, 1)
 VECTOR_SUM_QUARTERS = (2, 3)
-GPSIMD_COLUMN_BLOCK = N_BLOCKS - 1
-A_TILES = 13
-FOLDED_ROW_BLOCKS = (4, 5, 6)
-FOLDED_ROW = PACK - 1
-SCALAR_SCALE_ROW_BLOCKS = 4
+GPSIMD_COLUMNS = (0, 0, 256, 256)
+A_TILES = 10
+X_AT = (-1,1,2,3)
+SCALAR_SCALE_ROWS = 1
 
 
 def tile_gcnresnet_pa_t_kernel(tc, x_pre, A, W_gc2, out):
@@ -39,10 +44,14 @@ def tile_gcnresnet_pa_t_kernel(tc, x_pre, A, W_gc2, out):
     a_view = A.rearrange("(c p t) i -> c p t i", p=P, t=PACK)
     x_view = x_pre.rearrange("(m h p t) k -> m p h t k", h=2, p=P, t=PACK)
     out_view = out.rearrange("(b u p) f -> b p u f", u=BLOCK // P, p=P)
+    sum_view = A.rearrange("n i -> (n i)").rearrange(
+        "(b r q w) -> b q r w", r=SUM_ROWS // ROWS_ABREAST, q=P, w=PIECE
+    )
 
     with ExitStack() as ctx:
         keep = ctx.enter_context(tc.tile_pool(name="keep", bufs=1))
         a_pool = ctx.enter_context(tc.tile_pool(name="a_pool", bufs=A_TILES))
+        sum_pool = ctx.enter_context(tc.tile_pool(name="sum_pool", bufs=SUM_TILES))
         scaled_pool = ctx.enter_context(tc.tile_pool(name="scaled_pool", bufs=3))
         grouped_pool = ctx.enter_context(tc.tile_pool(name="grouped_pool", bufs=2))
         codes_pool = ctx.enter_context(tc.tile_pool(name="codes_pool", bufs=3))
@@ -55,9 +64,16 @@ def tile_gcnresnet_pa_t_kernel(tc, x_pre, A, W_gc2, out):
 
         identity = keep.tile([P, P], F32, name="identity")
         make_identity(nc, identity[:])
-        identity_bf16 = keep.tile([P, P], BF16, name="identity_bf16")
-        make_identity(nc, identity_bf16[:])
-        folds = {}
+        pick_f32 = keep.tile([P, ROWS_ABREAST], F32, name="pick_f32")
+        nc.vector.reduce_sum(
+            out=pick_f32[:],
+            in_=identity[:].rearrange("q (g c) -> q g c", c=PIECES),
+            axis=mybir.AxisListType.X,
+        )
+        pick = keep.tile([P, ROWS_ABREAST], BF16, name="pick")
+        nc.vector.tensor_copy(out=pick[:], in_=pick_f32[:])
+        one = keep.tile([P, 1], F32, name="one")
+        nc.gpsimd.memset(one[:], 1.0)
         minus_half = keep.tile([P, PACK], F32, name="minus_half")
         nc.gpsimd.memset(minus_half[:], -0.5)
         load_order = (0, 2, 1, 3)
@@ -65,7 +81,11 @@ def tile_gcnresnet_pa_t_kernel(tc, x_pre, A, W_gc2, out):
         sums_vector = keep.tile([P, N_BLOCKS, N_QUARTERS, PACK], F32, name="sums_vector")
         nc.gpsimd.memset(sums_scalar[:], 0.0)
         d = keep.tile([P, N_BLOCKS, PACK], F32, name="d")
-        d_gpsimd = keep.tile([P, BLOCK], F32, name="d_gpsimd")
+        d_gpsimd = {
+            q: keep.tile([P, GPSIMD_COLUMNS[q]], F32, name="d_gpsimd%d" % q)
+            for q in range(N_QUARTERS)
+            if GPSIMD_COLUMNS[q] > 0
+        }
         support_codes = keep.tile([P, N_BLOCKS, FEAT_OUT], U32, name="support_codes", align_bytes=64)
         support_scales = keep.tile([P, N_BLOCKS, FEAT_OUT], U8, name="support_scales", align_bytes=64)
         w_codes = keep.tile([P, FEAT_OUT], U32, name="w_codes", align_bytes=64)
@@ -75,6 +95,14 @@ def tile_gcnresnet_pa_t_kernel(tc, x_pre, A, W_gc2, out):
             tile = a_pool.tile([P, PACK, QUARTER], BF16, name="a_quarter", tag="a")
             nc.sync.dma_start(out=tile[:], in_=a_view[c][:, :, q * QUARTER : (q + 1) * QUARTER])
             return tile
+
+        def load_sum_tiles(c):
+            tiles = []
+            for n in range(BLOCK // SUM_ROWS):
+                tile = sum_pool.tile([P, SUM_ROWS // ROWS_ABREAST, PIECE], BF16, name="a_sum", tag="a_sum")
+                nc.sync.dma_start(out=tile[:], in_=sum_view[c * (BLOCK // SUM_ROWS) + n])
+                tiles.append(tile)
+            return tiles
 
 
         def quantise_w():
@@ -137,33 +165,11 @@ def tile_gcnresnet_pa_t_kernel(tc, x_pre, A, W_gc2, out):
 
 
         def vector_sums(c, q):
-            return c < VECTOR_SUM_ROW_BLOCKS and q in VECTOR_SUM_QUARTERS
-
-        def folded(c, t):
-            return c in FOLDED_ROW_BLOCKS and t == FOLDED_ROW
+            return c in VECTOR_SUM_ROW_BLOCKS and q in VECTOR_SUM_QUARTERS
 
         def sum_rows(c, q, a_quarter):
             for t in range(PACK):
-                if folded(c, t):
-                    if q == load_order[0]:
-                        folds[(c, t)] = misc_psum.tile([P, BLOCK], F32, name="fold", tag="product")
-                    for k in range(2):
-                        nc.tensor.matmul(
-                            folds[(c, t)][:],
-                            lhsT=identity_bf16[:],
-                            rhs=a_quarter[:, t, k * BLOCK : (k + 1) * BLOCK],
-                            start=(q == load_order[0] and k == 0),
-                            stop=(q == load_order[-1] and k == 1),
-                        )
-                    if q == load_order[-1]:
-                        junk = sums_pool.tile([P, BLOCK], F32, name="junk")
-                        nc.scalar.activation(
-                            out=junk[:], in_=folds[(c, t)][:], func=ACT.Copy, accum_out=sums_scalar[:, c, 0, t : t + 1]
-                        )
-            for t in range(PACK):
                 row = a_quarter[:, t, :]
-                if folded(c, t):
-                    continue
                 if vector_sums(c, q):
                     nc.vector.tensor_scalar(
                         out=row,
@@ -180,13 +186,39 @@ def tile_gcnresnet_pa_t_kernel(tc, x_pre, A, W_gc2, out):
         def quarter_sum(c, q):
             return sums_vector[:, c, q, :] if vector_sums(c, q) else sums_scalar[:, c, q, :]
 
-        def inverse_root_of_row_sums(c):
+        def add_quarter_sums(c):
             left = sums_pool.tile([P, PACK], F32, name="left")
             nc.gpsimd.tensor_tensor(out=left[:], in0=quarter_sum(c, 0), in1=quarter_sum(c, 1), op=ALU.add)
             right = sums_pool.tile([P, PACK], F32, name="right")
             nc.gpsimd.tensor_tensor(out=right[:], in0=quarter_sum(c, 2), in1=quarter_sum(c, 3), op=ALU.add)
             whole = sums_pool.tile([P, PACK], F32, name="whole")
             nc.gpsimd.tensor_tensor(out=whole[:], in0=left[:], in1=right[:], op=ALU.add)
+            return whole
+
+        def tensor_row_sums(tiles):
+            folded = misc_psum.tile([P, BLOCK], F32, name="folded", tag="rows")
+            j0 = 0
+            for tile in tiles:
+                for r in range(SUM_ROWS // ROWS_ABREAST):
+                    for m in range(PIECE // P):
+                        nc.tensor.matmul(
+                            folded[:, j0 : j0 + ROWS_ABREAST],
+                            lhsT=tile[:, r, m * P : (m + 1) * P],
+                            rhs=pick[:],
+                            start=(m == 0),
+                            stop=(m == PIECE // P - 1),
+                        )
+                    j0 += ROWS_ABREAST
+            by_row = sums_pool.tile([P, PACK, P], F32, name="by_row")
+            nc.scalar.copy(out=by_row[:], in_=folded[:].rearrange("m (p t) -> m t p", t=PACK))
+            totals = misc_psum.tile([P, PACK], F32, name="totals", tag="product")
+            for t in range(PACK):
+                nc.tensor.matmul(totals[:, t : t + 1], lhsT=by_row[:, t, :], rhs=one[:], start=True, stop=True)
+            whole = sums_pool.tile([P, PACK], F32, name="whole")
+            nc.scalar.copy(out=whole[:], in_=totals[:])
+            return whole
+
+        def inverse_root(c, whole):
             nc.gpsimd.tensor_tensor(out=d[:, c, :], in0=whole[:], in1=minus_half[:], op=ALU.pow)
 
         def spread_d(bank, b):
@@ -205,11 +237,7 @@ def tile_gcnresnet_pa_t_kernel(tc, x_pre, A, W_gc2, out):
         def unit(c, q, a_quarter, scale_on_gpsimd):
             scaled = scaled_pool.tile([P, PACK, QUARTER], F32, name="scaled")
             for t in range(PACK):
-                if scale_on_gpsimd and t == 0 and c >= SCALAR_SCALE_ROW_BLOCKS:
-                    nc.vector.tensor_scalar(
-                        out=scaled[:, t, :], in0=a_quarter[:, t, :], scalar1=d[:, c, t : t + 1], scalar2=None, op0=ALU.mult
-                    )
-                elif scale_on_gpsimd and t > 0:
+                if scale_on_gpsimd and t >= SCALAR_SCALE_ROWS:
                     nc.gpsimd.tensor_scalar(
                         out=scaled[:, t, :],
                         in0=a_quarter[:, t, :],
@@ -223,29 +251,29 @@ def tile_gcnresnet_pa_t_kernel(tc, x_pre, A, W_gc2, out):
                         out=scaled[:, t, :], in_=a_quarter[:, t, :], func=ACT.Copy, scale=d[:, c, t : t + 1]
                     )
             grouped = grouped_pool.tile([P, QUARTER, PACK], BF16, name="grouped", align_bytes=64)
+            vector_columns = QUARTER - GPSIMD_COLUMNS[q]
+            for i0 in range(vector_columns, QUARTER, P):
+                j0 = i0 - vector_columns
+                nc.gpsimd.tensor_tensor(
+                    out=grouped[:, i0 : i0 + P, :],
+                    in0=scaled[:, :, i0 : i0 + P].rearrange("p t i -> p i t"),
+                    in1=d_gpsimd[q][:, j0 : j0 + P].unsqueeze(2).to_broadcast([P, P, PACK]),
+                    op=ALU.mult,
+                )
             for k in range(2):
-                b = 2 * q + k
                 lo = k * BLOCK
-                if b == GPSIMD_COLUMN_BLOCK:
-                    for i0 in range(lo, lo + BLOCK, P):
-                        nc.gpsimd.tensor_tensor(
-                            out=grouped[:, i0 : i0 + P, :],
-                            in0=scaled[:, :, i0 : i0 + P].rearrange("p t i -> p i t"),
-                            in1=d_gpsimd[:, i0 - lo : i0 - lo + P].unsqueeze(2).to_broadcast([P, P, PACK]),
-                            op=ALU.mult,
-                        )
-                else:
-                    d_bank = spread_psum.tile([P, BLOCK], F32, name="d_bank", tag="spread")
-                    spread_d(d_bank, b)
-                    nc.vector.tensor_tensor(
-                        out=grouped[:, lo : lo + BLOCK, :].rearrange("p (n i) t -> p n t i", i=RUN),
-                        in0=scaled[:, :, lo : lo + BLOCK].rearrange("p t (n i) -> p n t i", i=RUN),
-                        in1=d_bank[:]
-                        .rearrange("p (n i) -> p n i", i=RUN)
-                        .unsqueeze(2)
-                        .to_broadcast([P, BLOCK // RUN, PACK, RUN]),
-                        op=ALU.mult,
-                    )
+                columns = min(BLOCK, vector_columns - lo)
+                d_bank = spread_psum.tile([P, BLOCK], F32, name="d_bank", tag="spread")
+                spread_d(d_bank, 2 * q + k)
+                nc.vector.tensor_tensor(
+                    out=grouped[:, lo : lo + columns, :].rearrange("p (n i) t -> p n t i", i=RUN),
+                    in0=scaled[:, :, lo : lo + columns].rearrange("p t (n i) -> p n t i", i=RUN),
+                    in1=d_bank[:, :columns]
+                    .rearrange("p (n i) -> p n i", i=RUN)
+                    .unsqueeze(2)
+                    .to_broadcast([P, columns // RUN, PACK, RUN]),
+                    op=ALU.mult,
+                )
             if waiting:
                 finish()
             waiting.append((c, q, grouped))
@@ -285,29 +313,56 @@ def tile_gcnresnet_pa_t_kernel(tc, x_pre, A, W_gc2, out):
 
 
         quantise_w()
-        x_tiles = []
-        for m in range(N_BLOCKS // 2):
-            x_pair = a_pool.tile([P, 2, PACK, FEAT_IN], BF16, name="x_pair", tag="a")
-            nc.sync.dma_start(out=x_pair[:], in_=x_view[m])
-            x_tiles.append(x_pair)
+        x_tiles = {}
+
+        def load_x(c):
+            for m in range(N_BLOCKS // 2):
+                if X_AT[m] == c:
+                    x_pair = a_pool.tile([P, 2, PACK, FEAT_IN], BF16, name="x_pair", tag="a")
+                    nc.sync.dma_start(out=x_pair[:], in_=x_view[m])
+                    x_tiles[m] = x_pair
+
+        def support(c):
+            for m in range(N_BLOCKS // 2):
+                if X_AT[m] == c:
+                    for h in range(2):
+                        support_of_row_block(2 * m + h, x_tiles[m][:, h])
+
         a_tiles = {}
-        for q in load_order:
-            a_tiles[(0, q)] = load_quarter(0, q)
-        for c in range(N_BLOCKS):
-            support_of_row_block(c, x_tiles[c // 2][:, c % 2])
+        sum_tiles = {}
+
+        def load_row_block(c):
+            if c in TENSOR_SUM_ROW_BLOCKS:
+                sum_tiles[c] = load_sum_tiles(c)
+                wanted = [(r, q) for q in range(ROUND_QUARTERS) if c > 2 * q for r in range(c + 1)]
+            else:
+                wanted = [(c, q) for q in load_order]
+            for key in wanted:
+                if key not in a_tiles:
+                    a_tiles[key] = load_quarter(key[0], key[1])
+            load_x(c)
+
+        load_x(-1)
+        load_row_block(0)
+        support(-1)
 
         for c in range(N_BLOCKS):
             if c + 1 < N_BLOCKS:
+                load_row_block(c + 1)
+            if c in TENSOR_SUM_ROW_BLOCKS:
+                with tc.high_priority():
+                    inverse_root(c, tensor_row_sums(sum_tiles[c]))
+            else:
                 for q in load_order:
-                    a_tiles[(c + 1, q)] = load_quarter(c + 1, q)
-            for q in load_order:
-                sum_rows(c, q, a_tiles[(c, q)])
-            with tc.high_priority():
-                inverse_root_of_row_sums(c)
-            if c == GPSIMD_COLUMN_BLOCK:
+                    sum_rows(c, q, a_tiles[(c, q)])
+                with tc.high_priority():
+                    inverse_root(c, add_quarter_sums(c))
+            if c % 2 == 1 and GPSIMD_COLUMNS[c // 2] > 0:
+                columns = GPSIMD_COLUMNS[c // 2]
                 d_turned = misc_psum.tile([P, BLOCK], F32, name="d_turned", tag="rows")
                 spread_d(d_turned, c)
-                nc.scalar.copy(out=d_gpsimd[:], in_=d_turned[:])
+                nc.scalar.copy(out=d_gpsimd[c // 2][:], in_=d_turned[:, BLOCK - columns :])
+            support(c)
             for q in range(ROUND_QUARTERS):
                 last_needed = 2 * q + 1
                 if c >= last_needed:
@@ -318,12 +373,13 @@ def tile_gcnresnet_pa_t_kernel(tc, x_pre, A, W_gc2, out):
         for b in range(2 * ROUND_QUARTERS):
             store_column_block(b, nc.scalar.copy, "rows")
 
-        for c in range(N_BLOCKS):
-            for q in range(ROUND_QUARTERS, N_QUARTERS):
+        for q in range(ROUND_QUARTERS, N_QUARTERS):
+            for c in range(N_BLOCKS):
                 a_tiles[(c, q)] = load_quarter(c, q)
-            for q in range(ROUND_QUARTERS, N_QUARTERS):
                 unit(c, q, a_tiles[(c, q)], scale_on_gpsimd=False)
+                if q == ROUND_QUARTERS + 1 and c == 0:
+                    for b in (2 * ROUND_QUARTERS, 2 * ROUND_QUARTERS + 1):
+                        store_column_block(b, nc.scalar.copy, "rows")
         finish()
-        for b in range(2 * ROUND_QUARTERS, N_BLOCKS - 1):
-            store_column_block(b, nc.scalar.copy, "rows")
+        store_column_block(N_BLOCKS - 2, nc.scalar.copy, "rows")
         store_column_block(N_BLOCKS - 1, nc.vector.tensor_copy, "product")

@@ -25,18 +25,33 @@ ROUND_QUARTERS = 2
 RUN = 4
 FLOPS = 2 * NODES * FEAT_IN * FEAT_OUT + 2 * NODES * NODES * FEAT_OUT
 
-TENSOR_SUM_ROW_BLOCKS = (2,3,5,7)
+TENSOR_SUM_ROW_BLOCKS = (1, 3, 5, 7)
 PIECE = 512
 PIECES = NODES // PIECE
 ROWS_ABREAST = P // PIECES
-SUM_ROWS = 8 * ROWS_ABREAST
+SUM_STEPS = 4096 // PIECE
+SUM_ROWS = SUM_STEPS * ROWS_ABREAST
 SUM_TILES = 4
-VECTOR_SUM_ROW_BLOCKS = (0, 1)
-VECTOR_SUM_QUARTERS = (2, 3)
-GPSIMD_COLUMNS = (0, 0, 256, 256)
+VECTOR_SUMS = ((0, 2), (0, 3), (2, 2), (2, 3))
+GPSIMD_COLUMNS = 256
+GC0 = 0
+GC0B = 128
+S_FREE = 2
+FOLD_PER = 2
+ENDOFF = 2
 A_TILES = 10
-X_AT = (-1,1,2,3)
 SCALAR_SCALE_ROWS = 1
+G1 = 3
+SCALED = 2
+GROUPED = 3
+MXLAG = 2
+V0 = 3
+S0 = 3
+LAG = 3
+FOLD_AT = 5
+AHEAD = 2
+AHEAD_S = 3
+AHEAD_U = 4
 
 
 def tile_gcnresnet_pa_t_kernel(tc, x_pre, A, W_gc2, out):
@@ -45,15 +60,15 @@ def tile_gcnresnet_pa_t_kernel(tc, x_pre, A, W_gc2, out):
     x_view = x_pre.rearrange("(m h p t) k -> m p h t k", h=2, p=P, t=PACK)
     out_view = out.rearrange("(b u p) f -> b p u f", u=BLOCK // P, p=P)
     sum_view = A.rearrange("n i -> (n i)").rearrange(
-        "(b r q w) -> b q r w", r=SUM_ROWS // ROWS_ABREAST, q=P, w=PIECE
+        "(b r q w) -> b q r w", r=SUM_STEPS, q=P, w=PIECE
     )
 
     with ExitStack() as ctx:
         keep = ctx.enter_context(tc.tile_pool(name="keep", bufs=1))
         a_pool = ctx.enter_context(tc.tile_pool(name="a_pool", bufs=A_TILES))
         sum_pool = ctx.enter_context(tc.tile_pool(name="sum_pool", bufs=SUM_TILES))
-        scaled_pool = ctx.enter_context(tc.tile_pool(name="scaled_pool", bufs=3))
-        grouped_pool = ctx.enter_context(tc.tile_pool(name="grouped_pool", bufs=2))
+        scaled_pool = ctx.enter_context(tc.tile_pool(name="scaled_pool", bufs=SCALED))
+        grouped_pool = ctx.enter_context(tc.tile_pool(name="grouped_pool", bufs=GROUPED))
         codes_pool = ctx.enter_context(tc.tile_pool(name="codes_pool", bufs=3))
         first_pool = ctx.enter_context(tc.tile_pool(name="first_pool", bufs=2))
         sums_pool = ctx.enter_context(tc.tile_pool(name="sums_pool", bufs=2))
@@ -61,6 +76,7 @@ def tile_gcnresnet_pa_t_kernel(tc, x_pre, A, W_gc2, out):
         spread_psum = ctx.enter_context(tc.psum_pool(name="spread_psum", bufs=2))
         acc_psum = ctx.enter_context(tc.psum_pool(name="acc_psum", bufs=ROUND_QUARTERS * 2))
         misc_psum = ctx.enter_context(tc.psum_pool(name="misc_psum", bufs=1))
+        ctx.enter_context(tc.manual_schedule())
 
         identity = keep.tile([P, P], F32, name="identity")
         make_identity(nc, identity[:])
@@ -81,11 +97,12 @@ def tile_gcnresnet_pa_t_kernel(tc, x_pre, A, W_gc2, out):
         sums_vector = keep.tile([P, N_BLOCKS, N_QUARTERS, PACK], F32, name="sums_vector")
         nc.gpsimd.memset(sums_scalar[:], 0.0)
         d = keep.tile([P, N_BLOCKS, PACK], F32, name="d")
-        d_gpsimd = {
-            q: keep.tile([P, GPSIMD_COLUMNS[q]], F32, name="d_gpsimd%d" % q)
-            for q in range(N_QUARTERS)
-            if GPSIMD_COLUMNS[q] > 0
-        }
+        d_gpsimd = {}
+        for q in range(N_QUARTERS):
+            width = max(GC0, GC0B) if q < ROUND_QUARTERS else GPSIMD_COLUMNS
+            if width:
+                d_gpsimd[q] = keep.tile([P, width], F32, name="d_gpsimd%d" % q)
+        spread_quarters = set()
         support_codes = keep.tile([P, N_BLOCKS, FEAT_OUT], U32, name="support_codes", align_bytes=64)
         support_scales = keep.tile([P, N_BLOCKS, FEAT_OUT], U8, name="support_scales", align_bytes=64)
         w_codes = keep.tile([P, FEAT_OUT], U32, name="w_codes", align_bytes=64)
@@ -99,7 +116,7 @@ def tile_gcnresnet_pa_t_kernel(tc, x_pre, A, W_gc2, out):
         def load_sum_tiles(c):
             tiles = []
             for n in range(BLOCK // SUM_ROWS):
-                tile = sum_pool.tile([P, SUM_ROWS // ROWS_ABREAST, PIECE], BF16, name="a_sum", tag="a_sum")
+                tile = sum_pool.tile([P, SUM_STEPS, PIECE], BF16, name="a_sum", tag="a_sum")
                 nc.sync.dma_start(out=tile[:], in_=sum_view[c * (BLOCK // SUM_ROWS) + n])
                 tiles.append(tile)
             return tiles
@@ -120,7 +137,10 @@ def tile_gcnresnet_pa_t_kernel(tc, x_pre, A, W_gc2, out):
                 in_=w_grouped[:].rearrange("q f s -> q (f s)"),
             )
 
-        def support_of_row_block(c, x_rows):
+        x_grouped_tiles = {}
+        h_tiles = {}
+
+        def turn_x(c, x_rows):
             x_words = x_rows.bitcast(F32)
             x_grouped = first_pool.tile([P, BLOCK, PACK], BF16, name="x_grouped", align_bytes=64)
             x_grouped_words = x_grouped[:].bitcast(F32)
@@ -137,14 +157,21 @@ def tile_gcnresnet_pa_t_kernel(tc, x_pre, A, W_gc2, out):
                     ),
                     in_=turned[:].rearrange("q t u p -> q t p u"),
                 )
-            x_flat = x_grouped[:].rearrange("q n s -> q (n s)")
+            x_grouped_tiles[c] = x_grouped
+
+        def quantise_h(c, fillers):
+            x_flat = x_grouped_tiles[c][:].rearrange("q n s -> q (n s)")
             h_grouped = first_pool.tile([P, BLOCK * PACK], BF16, name="h_grouped", align_bytes=64)
             nc.vector.tensor_scalar(out=h_grouped[:], in0=x_flat, scalar1=SLOPE, scalar2=None, op0=ALU.mult)
+            for f in fillers[:1]:
+                f()
             nc.vector.tensor_tensor(out=h_grouped[:], in0=x_flat, in1=h_grouped[:], op=ALU.max)
+            for f in fillers[1:]:
+                f()
             h_codes = first_pool.tile([P, BLOCK], U32, name="h_codes", align_bytes=64)
             h_scales = first_pool.tile([P, BLOCK], U8, name="h_scales", align_bytes=64)
             nc.vector.quantize_mx(out=h_codes[:].bitcast(FP8X4), scales=h_scales[:], in_=h_grouped[:])
-            product = misc_psum.tile([P, PACK, FEAT_OUT], F32, name="product", tag="product")
+            product = acc_psum.tile([P, PACK, FEAT_OUT], F32, name="product", tag="acc")
             for t in range(PACK):
                 nc.tensor.matmul_mx(
                     out=product[:, t, :],
@@ -155,8 +182,11 @@ def tile_gcnresnet_pa_t_kernel(tc, x_pre, A, W_gc2, out):
                     start=True,
                     stop=True,
                 )
+            h_tiles[c] = product
+
+        def quantise_support(c):
             s_grouped = first_pool.tile([P, FEAT_OUT, PACK], BF16, name="s_grouped", align_bytes=64)
-            nc.scalar.copy(out=s_grouped[:], in_=product[:].rearrange("p t f -> p f t"))
+            nc.scalar.copy(out=s_grouped[:], in_=h_tiles[c][:].rearrange("p t f -> p f t"))
             nc.vector.quantize_mx(
                 out=support_codes[:, c, :].bitcast(FP8X4),
                 scales=support_scales[:, c, :],
@@ -165,10 +195,10 @@ def tile_gcnresnet_pa_t_kernel(tc, x_pre, A, W_gc2, out):
 
 
         def vector_sums(c, q):
-            return c in VECTOR_SUM_ROW_BLOCKS and q in VECTOR_SUM_QUARTERS
+            return (c, q) in VECTOR_SUMS
 
-        def sum_rows(c, q, a_quarter):
-            for t in range(PACK):
+        def sum_rows(c, q, a_quarter, rows=range(PACK)):
+            for t in rows:
                 row = a_quarter[:, t, :]
                 if vector_sums(c, q):
                     nc.vector.tensor_scalar(
@@ -195,28 +225,32 @@ def tile_gcnresnet_pa_t_kernel(tc, x_pre, A, W_gc2, out):
             nc.gpsimd.tensor_tensor(out=whole[:], in0=left[:], in1=right[:], op=ALU.add)
             return whole
 
-        def tensor_row_sums(tiles):
-            folded = misc_psum.tile([P, BLOCK], F32, name="folded", tag="rows")
-            j0 = 0
-            for tile in tiles:
-                for r in range(SUM_ROWS // ROWS_ABREAST):
-                    for m in range(PIECE // P):
-                        nc.tensor.matmul(
-                            folded[:, j0 : j0 + ROWS_ABREAST],
-                            lhsT=tile[:, r, m * P : (m + 1) * P],
-                            rhs=pick[:],
-                            start=(m == 0),
-                            stop=(m == PIECE // P - 1),
-                        )
-                    j0 += ROWS_ABREAST
+        folded = {}
+
+        def fold_sum_tile(c, n):
+            if n == 0:
+                folded[c] = misc_psum.tile([P, BLOCK], F32, name="folded", tag="rows")
+            tile = sum_tiles[c][n]
+            for r in range(SUM_STEPS):
+                j0 = n * SUM_ROWS + r * ROWS_ABREAST
+                for m in range(PIECE // P):
+                    nc.tensor.matmul(
+                        folded[c][:, j0 : j0 + ROWS_ABREAST],
+                        lhsT=tile[:, r, m * P : (m + 1) * P],
+                        rhs=pick[:],
+                        start=(m == 0),
+                        stop=(m == PIECE // P - 1),
+                    )
+
+        def total_folded(c):
             by_row = sums_pool.tile([P, PACK, P], F32, name="by_row")
-            nc.scalar.copy(out=by_row[:], in_=folded[:].rearrange("m (p t) -> m t p", t=PACK))
+            nc.scalar.copy(out=by_row[:], in_=folded[c][:].rearrange("m (p t) -> m t p", t=PACK))
             totals = misc_psum.tile([P, PACK], F32, name="totals", tag="product")
             for t in range(PACK):
                 nc.tensor.matmul(totals[:, t : t + 1], lhsT=by_row[:, t, :], rhs=one[:], start=True, stop=True)
             whole = sums_pool.tile([P, PACK], F32, name="whole")
             nc.scalar.copy(out=whole[:], in_=totals[:])
-            return whole
+            inverse_root(c, whole)
 
         def inverse_root(c, whole):
             nc.gpsimd.tensor_tensor(out=d[:, c, :], in0=whole[:], in1=minus_half[:], op=ALU.pow)
@@ -229,15 +263,36 @@ def tile_gcnresnet_pa_t_kernel(tc, x_pre, A, W_gc2, out):
                     identity[:],
                 )
 
-
         acc = {}
         passes = {}
-        waiting = []
+        a_tiles = {}
+        sum_tiles = {}
+        scaled_tiles = {}
+        grouped_tiles = {}
+        code_tiles = {}
+        d_banks = [None, None]
 
-        def unit(c, q, a_quarter, scale_on_gpsimd):
+        order = [(0, 0), (1, 0), (2, 0), (3, 0), (0, 1), (1, 1), (2, 1), (3, 1), (4, 1), (4, 0), (5, 0), (5, 1), (6, 1), (6, 0), (7, 0), (7, 1)]
+        order = order + [(c, q) for q in (2, 3) for c in range(N_BLOCKS)]
+
+        def scalar_rows(s):
+            return SCALAR_SCALE_ROWS if busy_scalar[s] else S_FREE
+
+        def gpsimd_columns(s):
+            if order[s][1] >= ROUND_QUARTERS:
+                return GPSIMD_COLUMNS
+            return GC0 if scalar_rows(s) == SCALAR_SCALE_ROWS else GC0B
+
+        def scale(s):
+            c, q = order[s]
+            a_quarter = a_tiles[(c, q)]
             scaled = scaled_pool.tile([P, PACK, QUARTER], F32, name="scaled")
-            for t in range(PACK):
-                if scale_on_gpsimd and t >= SCALAR_SCALE_ROWS:
+            if q < ROUND_QUARTERS:
+                gs = range(scalar_rows(s), PACK)
+            else:
+                gs = range(PACK - 1, PACK) if G1 and s % G1 == 0 else ()
+            for t in list(gs) + [t for t in range(PACK) if t not in gs]:
+                if t in gs:
                     nc.gpsimd.tensor_scalar(
                         out=scaled[:, t, :],
                         in0=a_quarter[:, t, :],
@@ -250,45 +305,61 @@ def tile_gcnresnet_pa_t_kernel(tc, x_pre, A, W_gc2, out):
                     nc.scalar.activation(
                         out=scaled[:, t, :], in_=a_quarter[:, t, :], func=ACT.Copy, scale=d[:, c, t : t + 1]
                     )
+            scaled_tiles[s] = scaled
+
+        def spread(s):
+            c, q = order[s]
+            for k in range(2):
+                d_banks[k] = spread_psum.tile([P, BLOCK], F32, name="d_bank", tag="spread")
+                spread_d(d_banks[k], 2 * q + k)
+            if q < ROUND_QUARTERS and (GC0 or GC0B) and q not in spread_quarters:
+                spread_quarters.add(q)
+                nc.scalar.copy(out=d_gpsimd[q][:], in_=d_banks[1][:, BLOCK - max(GC0, GC0B) :])
+
+        def multiply(s):
+            c, q = order[s]
+            scaled = scaled_tiles[s]
             grouped = grouped_pool.tile([P, QUARTER, PACK], BF16, name="grouped", align_bytes=64)
-            vector_columns = QUARTER - GPSIMD_COLUMNS[q]
+            grouped_tiles[s] = grouped
+            vector_columns = QUARTER - gpsimd_columns(s)
+            width = max(GC0, GC0B) if q < ROUND_QUARTERS else GPSIMD_COLUMNS
             for i0 in range(vector_columns, QUARTER, P):
-                j0 = i0 - vector_columns
+                n = min(P, QUARTER - i0)
+                j0 = i0 - (QUARTER - width)
                 nc.gpsimd.tensor_tensor(
-                    out=grouped[:, i0 : i0 + P, :],
-                    in0=scaled[:, :, i0 : i0 + P].rearrange("p t i -> p i t"),
-                    in1=d_gpsimd[q][:, j0 : j0 + P].unsqueeze(2).to_broadcast([P, P, PACK]),
+                    out=grouped[:, i0 : i0 + n, :],
+                    in0=scaled[:, :, i0 : i0 + n].rearrange("p t i -> p i t"),
+                    in1=d_gpsimd[q][:, j0 : j0 + n].unsqueeze(2).to_broadcast([P, n, PACK]),
                     op=ALU.mult,
                 )
             for k in range(2):
                 lo = k * BLOCK
                 columns = min(BLOCK, vector_columns - lo)
-                d_bank = spread_psum.tile([P, BLOCK], F32, name="d_bank", tag="spread")
-                spread_d(d_bank, 2 * q + k)
                 nc.vector.tensor_tensor(
                     out=grouped[:, lo : lo + columns, :].rearrange("p (n i) t -> p n t i", i=RUN),
                     in0=scaled[:, :, lo : lo + columns].rearrange("p t (n i) -> p n t i", i=RUN),
-                    in1=d_bank[:, :columns]
+                    in1=d_banks[k][:, :columns]
                     .rearrange("p (n i) -> p n i", i=RUN)
                     .unsqueeze(2)
                     .to_broadcast([P, columns // RUN, PACK, RUN]),
                     op=ALU.mult,
                 )
-            if waiting:
-                finish()
-            waiting.append((c, q, grouped))
 
-        def finish():
-            c, q, grouped = waiting.pop(0)
+        def quantise(s):
             codes = codes_pool.tile([P, QUARTER], U32, name="codes", align_bytes=64)
             scales = codes_pool.tile([P, QUARTER], U8, name="scales", align_bytes=64)
             nc.vector.quantize_mx(
-                out=codes[:].bitcast(FP8X4), scales=scales[:], in_=grouped[:].rearrange("p i t -> p (i t)")
+                out=codes[:].bitcast(FP8X4), scales=scales[:], in_=grouped_tiles[s][:].rearrange("p i t -> p (i t)")
             )
+            code_tiles[s] = (codes, scales)
+
+        def accumulate(s):
+            c, q = order[s]
+            codes, scales = code_tiles[s]
             for k in range(2):
                 b = 2 * q + k
                 if b not in acc:
-                    acc[b] = acc_psum.tile([P, BLOCK], F32, name="acc")
+                    acc[b] = acc_psum.tile([P, BLOCK], F32, name="acc", tag="acc")
                     passes[b] = 0
                 nc.tensor.matmul_mx(
                     out=acc[b][:],
@@ -301,85 +372,141 @@ def tile_gcnresnet_pa_t_kernel(tc, x_pre, A, W_gc2, out):
                 )
                 passes[b] += 1
 
-        def store_column_block(b, copy, tag):
+        out_tiles = {}
+
+        def empty_bank(b, copy, tag):
             out_t = out_pool.tile([P, BLOCK], F32, name="out_t")
             copy(out=out_t[:], in_=acc[b][:])
             rows_psum = misc_psum.tile([P, BLOCK // P, FEAT_OUT], F32, name="rows_psum", tag=tag)
             for u in range(BLOCK // P):
                 nc.tensor.transpose(rows_psum[:, u, :], out_t[:, P * u : P * (u + 1)], identity[:])
+            out_tiles[b] = rows_psum
+
+        def store_rows(b, copy, queue):
             rows = out_pool.tile([P, BLOCK // P, FEAT_OUT], F32, name="rows")
-            copy(out=rows[:], in_=rows_psum[:])
-            nc.sync.dma_start(out=out_view[b], in_=rows[:])
+            copy(out=rows[:], in_=out_tiles[b][:])
+            queue.dma_start(out=out_view[b], in_=rows[:])
 
-
-        quantise_w()
-        x_tiles = {}
-
-        def load_x(c):
-            for m in range(N_BLOCKS // 2):
-                if X_AT[m] == c:
-                    x_pair = a_pool.tile([P, 2, PACK, FEAT_IN], BF16, name="x_pair", tag="a")
-                    nc.sync.dma_start(out=x_pair[:], in_=x_view[m])
-                    x_tiles[m] = x_pair
-
-        def support(c):
-            for m in range(N_BLOCKS // 2):
-                if X_AT[m] == c:
-                    for h in range(2):
-                        support_of_row_block(2 * m + h, x_tiles[m][:, h])
-
-        a_tiles = {}
-        sum_tiles = {}
-
-        def load_row_block(c):
-            if c in TENSOR_SUM_ROW_BLOCKS:
-                sum_tiles[c] = load_sum_tiles(c)
-                wanted = [(r, q) for q in range(ROUND_QUARTERS) if c > 2 * q for r in range(c + 1)]
-            else:
-                wanted = [(c, q) for q in load_order]
-            for key in wanted:
-                if key not in a_tiles:
-                    a_tiles[key] = load_quarter(key[0], key[1])
-            load_x(c)
-
-        load_x(-1)
-        load_row_block(0)
-        support(-1)
-
-        for c in range(N_BLOCKS):
-            if c + 1 < N_BLOCKS:
-                load_row_block(c + 1)
-            if c in TENSOR_SUM_ROW_BLOCKS:
-                with tc.high_priority():
-                    inverse_root(c, tensor_row_sums(sum_tiles[c]))
-            else:
-                for q in load_order:
-                    sum_rows(c, q, a_tiles[(c, q)])
-                with tc.high_priority():
-                    inverse_root(c, add_quarter_sums(c))
-            if c % 2 == 1 and GPSIMD_COLUMNS[c // 2] > 0:
-                columns = GPSIMD_COLUMNS[c // 2]
-                d_turned = misc_psum.tile([P, BLOCK], F32, name="d_turned", tag="rows")
-                spread_d(d_turned, c)
-                nc.scalar.copy(out=d_gpsimd[c // 2][:], in_=d_turned[:, BLOCK - columns :])
-            support(c)
-            for q in range(ROUND_QUARTERS):
-                last_needed = 2 * q + 1
-                if c >= last_needed:
-                    first_ready = 0 if c == last_needed else c
-                    for r in range(first_ready, c + 1):
-                        unit(r, q, a_tiles[(r, q)], scale_on_gpsimd=True)
-        finish()
-        for b in range(2 * ROUND_QUARTERS):
-            store_column_block(b, nc.scalar.copy, "rows")
-
-        for q in range(ROUND_QUARTERS, N_QUARTERS):
-            for c in range(N_BLOCKS):
+        def load(*keys):
+            for c, q in keys:
                 a_tiles[(c, q)] = load_quarter(c, q)
-                unit(c, q, a_tiles[(c, q)], scale_on_gpsimd=False)
-                if q == ROUND_QUARTERS + 1 and c == 0:
-                    for b in (2 * ROUND_QUARTERS, 2 * ROUND_QUARTERS + 1):
-                        store_column_block(b, nc.scalar.copy, "rows")
-        finish()
-        store_column_block(N_BLOCKS - 2, nc.scalar.copy, "rows")
-        store_column_block(N_BLOCKS - 1, nc.vector.tensor_copy, "product")
+
+        def load_block(c):
+            load(*[(c, q) for q in load_order])
+
+        x_tiles = []
+        for m in range(N_BLOCKS // 2):
+            x_pair = a_pool.tile([P, 2, PACK, FEAT_IN], BF16, name="x_pair", tag="a")
+            nc.sync.dma_start(out=x_pair[:], in_=x_view[m])
+            x_tiles.append(x_pair)
+            if m == 0:
+                quantise_w()
+        load_block(0)
+        sum_tiles[1] = load_sum_tiles(1)
+        load((1, 0))
+        if 2 in TENSOR_SUM_ROW_BLOCKS:
+            pass
+        else:
+            load_block(2)
+
+        for c in range(N_BLOCKS + LAG):
+            if c < N_BLOCKS:
+                turn_x(c, x_tiles[c // 2][:, c % 2])
+            if 0 < c <= N_BLOCKS:
+                n = c - 1 - V0
+                fillers = [
+                    lambda q=(2, 3)[m // PACK], t=m % PACK: sum_rows(0, q, a_tiles[(0, q)], (t,))
+                    for m in range(2 * n, 2 * n + 2)
+                    if 0 <= m < 2 * PACK
+                ]
+                quantise_h(c - 1, fillers)
+            if LAG <= c:
+                quantise_support(c - LAG)
+            if S0 <= c < S0 + 4:
+                q = (0, 1)[(c - S0) // 2]
+                sum_rows(0, q, a_tiles[(0, q)], range(2 * ((c - S0) % 2), 2 * ((c - S0) % 2) + 2))
+            if c == max(V0 + 5, S0 + 4):
+                inverse_root(0, add_quarter_sums(0))
+            if FOLD_AT <= c < FOLD_AT + 4:
+                fold_sum_tile(1, c - FOLD_AT)
+        total_folded(1)
+
+        def sums(c, *qs):
+            for q in qs:
+                sum_rows(c, q, a_tiles[(c, q)])
+
+        def d_scalar(c):
+            inverse_root(c, add_quarter_sums(c))
+
+        def load_sum(c):
+            sum_tiles[c] = load_sum_tiles(c)
+
+        busy_scalar = [False] * (len(order) + 1)
+        first_use = {c: min(s for s in range(len(order)) if order[s][0] == c or order[s][1] == c // 2) for c in range(N_BLOCKS)}
+        first_use = {c: min(s for s in range(len(order)) if order[s][0] == c) for c in range(N_BLOCKS)}
+        jobs = {}
+        loads = {}
+
+        def add(table, s, f):
+            table.setdefault(max(s, 0), []).append(f)
+
+        queue = []
+        for c in range(2, N_BLOCKS):
+            end = max(first_use[c] - ENDOFF, 0)
+            if c in TENSOR_SUM_ROW_BLOCKS:
+                for n in range(4):
+                    add(jobs, end - (3 - n) // FOLD_PER, lambda c=c, n=n: fold_sum_tile(c, n))
+                add(jobs, end, lambda c=c: total_folded(c))
+                queue.append((end - 3 // FOLD_PER - AHEAD_S, lambda c=c: load_sum(c)))
+            else:
+                for n, q in enumerate(load_order):
+                    s = max(end - 3 + n, 0)
+                    add(jobs, s, lambda c=c, q=q: sums(c, q))
+                    if not vector_sums(c, q):
+                        busy_scalar[s + 1] = True
+                add(jobs, end, lambda c=c: d_scalar(c))
+                if c > 2:
+                    queue.append((end - 3 - AHEAD, lambda c=c: load_block(c)))
+            if c in TENSOR_SUM_ROW_BLOCKS:
+                wanted = [(c, q) for q in range(ROUND_QUARTERS)]
+                for s in range(len(order)):
+                    if order[s] in wanted:
+                        queue.append((s - AHEAD_U, lambda k=order[s]: load(k)))
+        for s in range(len(order)):
+            c, q = order[s]
+            if (q < ROUND_QUARTERS and c == 1 and q == 1) or q >= ROUND_QUARTERS:
+                queue.append((s - AHEAD_U, lambda k=(c, q): load(k)))
+        for s, f in sorted(queue, key=lambda e: e[0]):
+            add(loads, s, f)
+        steps = len(order)
+        scale(0)
+        for s in range(steps + MXLAG + 3):
+            for f in loads.get(s, ()):
+                f()
+            if s + 1 < steps:
+                scale(s + 1)
+            if s < steps and (s == 0 or order[s][1] != order[s - 1][1]):
+                spread(s)
+            if s < steps:
+                multiply(s)
+            if 1 <= s <= steps:
+                quantise(s - 1)
+            if MXLAG <= s < steps + MXLAG:
+                accumulate(s - MXLAG)
+            for f in jobs.get(s, ()):
+                f()
+            if s in (13, 14):
+                j = s - 13
+                d_turned = misc_psum.tile([P, BLOCK], F32, name="d_turned", tag="rows")
+                spread_d(d_turned, 2 * (j + ROUND_QUARTERS) + 1)
+                nc.scalar.copy(out=d_gpsimd[j + ROUND_QUARTERS][:], in_=d_turned[:, BLOCK - GPSIMD_COLUMNS :])
+            for s0, b in ((16, 0), (17, 1), (18, 2), (19, 3), (25, 4), (26, 5)):
+                if s == s0 + 1:
+                    store_rows(b, nc.scalar.copy, nc.scalar)
+            for s0, b in ((16, 0), (17, 1), (18, 2), (19, 3), (25, 4), (26, 5)):
+                if s == s0:
+                    empty_bank(b, nc.scalar.copy, "rows")
+        empty_bank(N_BLOCKS - 2, nc.scalar.copy, "rows")
+        empty_bank(N_BLOCKS - 1, nc.vector.tensor_copy, "product")
+        store_rows(N_BLOCKS - 2, nc.scalar.copy, nc.sync)
+        store_rows(N_BLOCKS - 1, nc.vector.tensor_copy, nc.sync)

@@ -26,19 +26,19 @@ RUN = 4
 FLOPS = 2 * NODES * FEAT_IN * FEAT_OUT + 2 * NODES * NODES * FEAT_OUT
 
 TENSOR_SUM_ROW_BLOCKS = (1, 3, 5, 7)
-PIECE = 512
-PIECES = NODES // PIECE
-ROWS_ABREAST = P // PIECES
-SUM_STEPS = 4096 // PIECE
-SUM_ROWS = SUM_STEPS * ROWS_ABREAST
+SUM_ROWS = P
+WIDE = (1, 3, 5)
+ROW_TILES = (4, 6)
 SUM_TILES = 4
 VECTOR_SUMS = ((0, 2), (0, 3), (2, 2), (2, 3))
 GPSIMD_COLUMNS = 256
 GC0 = 0
-GC0B = 128
+GC0B = 0
 S_FREE = 2
-FOLD_PER = 2
-ENDOFF = 2
+FOLD_PER = 4
+END_S = 2
+END_T = 2
+TOT_AT = 9
 A_TILES = 10
 SCALAR_SCALE_ROWS = 1
 G1 = 3
@@ -46,8 +46,8 @@ SCALED = 2
 GROUPED = 3
 MXLAG = 2
 V0 = 3
-S0 = 3
-LAG = 3
+S0 = 4
+LAG = 4
 FOLD_AT = 5
 AHEAD = 2
 AHEAD_S = 3
@@ -59,9 +59,13 @@ def tile_gcnresnet_pa_t_kernel(tc, x_pre, A, W_gc2, out):
     a_view = A.rearrange("(c p t) i -> c p t i", p=P, t=PACK)
     x_view = x_pre.rearrange("(m h p t) k -> m p h t k", h=2, p=P, t=PACK)
     out_view = out.rearrange("(b u p) f -> b p u f", u=BLOCK // P, p=P)
-    sum_view = A.rearrange("n i -> (n i)").rearrange(
-        "(b r q w) -> b q r w", r=SUM_STEPS, q=P, w=PIECE
-    )
+    def piece(c):
+        return 1024 if c in WIDE else 512
+
+    sum_views = {
+        w: A.rearrange("n i -> (n i)").rearrange("(b r q w) -> b q r w", r=NODES // w, q=P, w=w)
+        for w in {piece(c) for c in TENSOR_SUM_ROW_BLOCKS}
+    }
 
     with ExitStack() as ctx:
         keep = ctx.enter_context(tc.tile_pool(name="keep", bufs=1))
@@ -80,14 +84,16 @@ def tile_gcnresnet_pa_t_kernel(tc, x_pre, A, W_gc2, out):
 
         identity = keep.tile([P, P], F32, name="identity")
         make_identity(nc, identity[:])
-        pick_f32 = keep.tile([P, ROWS_ABREAST], F32, name="pick_f32")
-        nc.vector.reduce_sum(
-            out=pick_f32[:],
-            in_=identity[:].rearrange("q (g c) -> q g c", c=PIECES),
-            axis=mybir.AxisListType.X,
-        )
-        pick = keep.tile([P, ROWS_ABREAST], BF16, name="pick")
-        nc.vector.tensor_copy(out=pick[:], in_=pick_f32[:])
+        picks = {}
+        for w in sum_views:
+            pick_f32 = keep.tile([P, P * w // NODES], F32, name="pick_f32_%d" % w)
+            nc.vector.reduce_sum(
+                out=pick_f32[:],
+                in_=identity[:].rearrange("q (g c) -> q g c", c=NODES // w),
+                axis=mybir.AxisListType.X,
+            )
+            picks[w] = keep.tile([P, P * w // NODES], BF16, name="pick_%d" % w)
+            nc.vector.tensor_copy(out=picks[w][:], in_=pick_f32[:])
         one = keep.tile([P, 1], F32, name="one")
         nc.gpsimd.memset(one[:], 1.0)
         minus_half = keep.tile([P, PACK], F32, name="minus_half")
@@ -116,8 +122,9 @@ def tile_gcnresnet_pa_t_kernel(tc, x_pre, A, W_gc2, out):
         def load_sum_tiles(c):
             tiles = []
             for n in range(BLOCK // SUM_ROWS):
-                tile = sum_pool.tile([P, SUM_STEPS, PIECE], BF16, name="a_sum", tag="a_sum")
-                nc.sync.dma_start(out=tile[:], in_=sum_view[c * (BLOCK // SUM_ROWS) + n])
+                w = piece(c)
+                tile = sum_pool.tile([P, NODES // w, w], BF16, name="a_sum", tag="a_sum")
+                nc.sync.dma_start(out=tile[:], in_=sum_views[w][c * (BLOCK // SUM_ROWS) + n])
                 tiles.append(tile)
             return tiles
 
@@ -226,34 +233,39 @@ def tile_gcnresnet_pa_t_kernel(tc, x_pre, A, W_gc2, out):
             return whole
 
         folded = {}
+        totals = {}
 
         def fold_sum_tile(c, n):
             if n == 0:
                 folded[c] = misc_psum.tile([P, BLOCK], F32, name="folded", tag="rows")
             tile = sum_tiles[c][n]
-            for r in range(SUM_STEPS):
-                j0 = n * SUM_ROWS + r * ROWS_ABREAST
-                for m in range(PIECE // P):
+            w = piece(c)
+            abreast = P * w // NODES
+            for r in range(NODES // w):
+                j0 = n * SUM_ROWS + r * abreast
+                for m in range(w // P):
                     nc.tensor.matmul(
-                        folded[c][:, j0 : j0 + ROWS_ABREAST],
+                        folded[c][:, j0 : j0 + abreast],
                         lhsT=tile[:, r, m * P : (m + 1) * P],
-                        rhs=pick[:],
+                        rhs=picks[w][:],
                         start=(m == 0),
-                        stop=(m == PIECE // P - 1),
+                        stop=(m == w // P - 1),
                     )
 
         def total_folded(c):
             by_row = sums_pool.tile([P, PACK, P], F32, name="by_row")
             nc.scalar.copy(out=by_row[:], in_=folded[c][:].rearrange("m (p t) -> m t p", t=PACK))
-            totals = misc_psum.tile([P, PACK], F32, name="totals", tag="product")
+            totals[c] = misc_psum.tile([P, PACK], F32, name="totals", tag="product")
             for t in range(PACK):
-                nc.tensor.matmul(totals[:, t : t + 1], lhsT=by_row[:, t, :], rhs=one[:], start=True, stop=True)
+                nc.tensor.matmul(totals[c][:, t : t + 1], lhsT=by_row[:, t, :], rhs=one[:], start=True, stop=True)
+
+        def d_tensor(c):
             whole = sums_pool.tile([P, PACK], F32, name="whole")
-            nc.scalar.copy(out=whole[:], in_=totals[:])
-            inverse_root(c, whole)
+            nc.scalar.copy(out=whole[:], in_=totals[c][:])
+            inverse_root(c, whole[:])
 
         def inverse_root(c, whole):
-            nc.gpsimd.tensor_tensor(out=d[:, c, :], in0=whole[:], in1=minus_half[:], op=ALU.pow)
+            nc.gpsimd.tensor_tensor(out=d[:, c, :], in0=whole, in1=minus_half[:], op=ALU.pow)
 
         def spread_d(bank, b):
             for t in range(PACK):
@@ -267,6 +279,7 @@ def tile_gcnresnet_pa_t_kernel(tc, x_pre, A, W_gc2, out):
         passes = {}
         a_tiles = {}
         sum_tiles = {}
+        a_row_tiles = {}
         scaled_tiles = {}
         grouped_tiles = {}
         code_tiles = {}
@@ -285,7 +298,10 @@ def tile_gcnresnet_pa_t_kernel(tc, x_pre, A, W_gc2, out):
 
         def scale(s):
             c, q = order[s]
-            a_quarter = a_tiles[(c, q)]
+            if c in ROW_TILES and q < ROUND_QUARTERS:
+                a_rows = [a_row_tiles[(c, t)][:, q * QUARTER : (q + 1) * QUARTER] for t in range(PACK)]
+            else:
+                a_rows = [a_tiles[(c, q)][:, t, :] for t in range(PACK)]
             scaled = scaled_pool.tile([P, PACK, QUARTER], F32, name="scaled")
             if q < ROUND_QUARTERS:
                 gs = range(scalar_rows(s), PACK)
@@ -295,7 +311,7 @@ def tile_gcnresnet_pa_t_kernel(tc, x_pre, A, W_gc2, out):
                 if t in gs:
                     nc.gpsimd.tensor_scalar(
                         out=scaled[:, t, :],
-                        in0=a_quarter[:, t, :],
+                        in0=a_rows[t],
                         scalar1=d[:, c, t : t + 1],
                         scalar2=0.0,
                         op0=ALU.mult,
@@ -303,7 +319,7 @@ def tile_gcnresnet_pa_t_kernel(tc, x_pre, A, W_gc2, out):
                     )
                 else:
                     nc.scalar.activation(
-                        out=scaled[:, t, :], in_=a_quarter[:, t, :], func=ACT.Copy, scale=d[:, c, t : t + 1]
+                        out=scaled[:, t, :], in_=a_rows[t], func=ACT.Copy, scale=d[:, c, t : t + 1]
                     )
             scaled_tiles[s] = scaled
 
@@ -392,7 +408,16 @@ def tile_gcnresnet_pa_t_kernel(tc, x_pre, A, W_gc2, out):
                 a_tiles[(c, q)] = load_quarter(c, q)
 
         def load_block(c):
-            load(*[(c, q) for q in load_order])
+            if c not in ROW_TILES:
+                load(*[(c, q) for q in load_order])
+                return
+            for t in range(PACK):
+                a_row_tiles[(c, t)] = a_pool.tile([P, NODES], BF16, name="a_row", tag="a")
+                nc.sync.dma_start(out=a_row_tiles[(c, t)][:], in_=a_view[c][:, t, :])
+
+        def sum_row(c, t):
+            row = a_row_tiles[(c, t)][:]
+            nc.scalar.activation(out=row, in_=row, func=ACT.Copy, accum_out=sums_scalar[:, c, 0, t : t + 1])
 
         x_tiles = []
         for m in range(N_BLOCKS // 2):
@@ -405,10 +430,65 @@ def tile_gcnresnet_pa_t_kernel(tc, x_pre, A, W_gc2, out):
         sum_tiles[1] = load_sum_tiles(1)
         load((1, 0))
         if 2 in TENSOR_SUM_ROW_BLOCKS:
-            pass
+            sum_tiles[2] = load_sum_tiles(2)
+            load((2, 0))
         else:
             load_block(2)
 
+        def sums(c, *qs):
+            for q in qs:
+                sum_rows(c, q, a_tiles[(c, q)])
+
+        def d_scalar(c):
+            inverse_root(c, sums_scalar[:, c, 0, :] if c in ROW_TILES else add_quarter_sums(c)[:])
+
+        def load_sum(c):
+            sum_tiles[c] = load_sum_tiles(c)
+
+        busy_scalar = [False] * (len(order) + 1)
+        first_use = {c: min(s for s in range(len(order)) if order[s][0] == c or order[s][1] == c // 2) for c in range(N_BLOCKS)}
+        first_use = {c: min(s for s in range(len(order)) if order[s][0] == c) for c in range(N_BLOCKS)}
+        jobs = {}
+        loads = {}
+
+        pre_jobs = {}
+
+        def add(table, s, f, least=0):
+            table.setdefault(max(s, least), []).append(f)
+
+        queue = []
+        for c in range(2, N_BLOCKS):
+            end = max(first_use[c] - (END_T if c in TENSOR_SUM_ROW_BLOCKS else END_S), 0)
+            if c in TENSOR_SUM_ROW_BLOCKS:
+                for n in range(4):
+                    add(jobs, end - 1 - (3 - n) // FOLD_PER, lambda c=c, n=n: fold_sum_tile(c, n), -1)
+                add(pre_jobs, end, lambda c=c: total_folded(c))
+                add(jobs, end, lambda c=c: d_tensor(c))
+                if c > 2:
+                    queue.append((end - 1 - 3 // FOLD_PER - AHEAD_S, lambda c=c: load_sum(c)))
+            else:
+                for n, q in enumerate(load_order):
+                    s = max(end - 3 + n, 0)
+                    if c in ROW_TILES:
+                        add(jobs, s, lambda c=c, n=n: sum_row(c, n))
+                    else:
+                        add(jobs, s, lambda c=c, q=q: sums(c, q))
+                    if not vector_sums(c, q):
+                        busy_scalar[s + 1] = True
+                add(jobs, end, lambda c=c: d_scalar(c))
+                if c > 2:
+                    queue.append((end - 3 - AHEAD, lambda c=c: load_block(c)))
+            if c in TENSOR_SUM_ROW_BLOCKS:
+                wanted = [(c, q) for q in range(ROUND_QUARTERS)]
+                for s in range(len(order)):
+                    if order[s] in wanted and order[s] != (2, 0):
+                        queue.append((s - AHEAD_U, lambda k=order[s]: load(k)))
+        for s in range(len(order)):
+            c, q = order[s]
+            if (q < ROUND_QUARTERS and c == 1 and q == 1) or q >= ROUND_QUARTERS:
+                queue.append((s - AHEAD_U, lambda k=(c, q): load(k)))
+        for s, f in sorted(queue, key=lambda e: e[0]):
+            add(loads, s, f, -1)
         for c in range(N_BLOCKS + LAG):
             if c < N_BLOCKS:
                 turn_x(c, x_tiles[c // 2][:, c % 2])
@@ -426,62 +506,22 @@ def tile_gcnresnet_pa_t_kernel(tc, x_pre, A, W_gc2, out):
                 q = (0, 1)[(c - S0) // 2]
                 sum_rows(0, q, a_tiles[(0, q)], range(2 * ((c - S0) % 2), 2 * ((c - S0) % 2) + 2))
             if c == max(V0 + 5, S0 + 4):
-                inverse_root(0, add_quarter_sums(0))
+                inverse_root(0, add_quarter_sums(0)[:])
             if FOLD_AT <= c < FOLD_AT + 4:
                 fold_sum_tile(1, c - FOLD_AT)
-        total_folded(1)
+            if c == TOT_AT:
+                total_folded(1)
+            if c == TOT_AT + 1:
+                scale(0)
+                d_tensor(1)
 
-        def sums(c, *qs):
-            for q in qs:
-                sum_rows(c, q, a_tiles[(c, q)])
-
-        def d_scalar(c):
-            inverse_root(c, add_quarter_sums(c))
-
-        def load_sum(c):
-            sum_tiles[c] = load_sum_tiles(c)
-
-        busy_scalar = [False] * (len(order) + 1)
-        first_use = {c: min(s for s in range(len(order)) if order[s][0] == c or order[s][1] == c // 2) for c in range(N_BLOCKS)}
-        first_use = {c: min(s for s in range(len(order)) if order[s][0] == c) for c in range(N_BLOCKS)}
-        jobs = {}
-        loads = {}
-
-        def add(table, s, f):
-            table.setdefault(max(s, 0), []).append(f)
-
-        queue = []
-        for c in range(2, N_BLOCKS):
-            end = max(first_use[c] - ENDOFF, 0)
-            if c in TENSOR_SUM_ROW_BLOCKS:
-                for n in range(4):
-                    add(jobs, end - (3 - n) // FOLD_PER, lambda c=c, n=n: fold_sum_tile(c, n))
-                add(jobs, end, lambda c=c: total_folded(c))
-                queue.append((end - 3 // FOLD_PER - AHEAD_S, lambda c=c: load_sum(c)))
-            else:
-                for n, q in enumerate(load_order):
-                    s = max(end - 3 + n, 0)
-                    add(jobs, s, lambda c=c, q=q: sums(c, q))
-                    if not vector_sums(c, q):
-                        busy_scalar[s + 1] = True
-                add(jobs, end, lambda c=c: d_scalar(c))
-                if c > 2:
-                    queue.append((end - 3 - AHEAD, lambda c=c: load_block(c)))
-            if c in TENSOR_SUM_ROW_BLOCKS:
-                wanted = [(c, q) for q in range(ROUND_QUARTERS)]
-                for s in range(len(order)):
-                    if order[s] in wanted:
-                        queue.append((s - AHEAD_U, lambda k=order[s]: load(k)))
-        for s in range(len(order)):
-            c, q = order[s]
-            if (q < ROUND_QUARTERS and c == 1 and q == 1) or q >= ROUND_QUARTERS:
-                queue.append((s - AHEAD_U, lambda k=(c, q): load(k)))
-        for s, f in sorted(queue, key=lambda e: e[0]):
-            add(loads, s, f)
         steps = len(order)
-        scale(0)
+        for f in loads.get(-1, []) + jobs.get(-1, []):
+            f()
         for s in range(steps + MXLAG + 3):
             for f in loads.get(s, ()):
+                f()
+            for f in pre_jobs.get(s, ()):
                 f()
             if s + 1 < steps:
                 scale(s + 1)

@@ -33,22 +33,32 @@ SUM_TILES = 4
 VECTOR_SUMS = ((0, 2), (0, 3), (2, 2), (2, 3))
 GPSIMD_COLUMNS = 256
 GC0 = 0
-GC0B = 0
-S_FREE = 2
+GC0B = 128
+S_FREE = 3
 FOLD_PER = 4
 END_S = 2
 END_T = 2
 TOT_AT = 9
+SC_AT = 9
+FOLD_C = (6,7,7,7)
+D1_AT = 9
+D0_AT = 8
+GFIRST = 0
 A_TILES = 10
 SCALAR_SCALE_ROWS = 1
 G1 = 3
 SCALED = 2
 GROUPED = 3
 MXLAG = 2
-V0 = 3
+EARLY_SPREAD = 0
+TOT_FIRST = 1
+D1_FIRST = 1
+QUICK = (1,3)
+S_FIRST = (3,)
+V_ROWS_AT = (4,5,6,7)
 S0 = 4
-LAG = 4
-FOLD_AT = 5
+LAG = 2
+FOLD_AT = 6
 AHEAD = 2
 AHEAD_S = 3
 AHEAD_U = 4
@@ -166,15 +176,21 @@ def tile_gcnresnet_pa_t_kernel(tc, x_pre, A, W_gc2, out):
                 )
             x_grouped_tiles[c] = x_grouped
 
-        def quantise_h(c, fillers):
+        h_grouped_tiles = {}
+
+        def slope_times_x(c):
             x_flat = x_grouped_tiles[c][:].rearrange("q n s -> q (n s)")
             h_grouped = first_pool.tile([P, BLOCK * PACK], BF16, name="h_grouped", align_bytes=64)
             nc.vector.tensor_scalar(out=h_grouped[:], in0=x_flat, scalar1=SLOPE, scalar2=None, op0=ALU.mult)
-            for f in fillers[:1]:
-                f()
+            h_grouped_tiles[c] = h_grouped
+
+        def leaky_relu(c):
+            x_flat = x_grouped_tiles[c][:].rearrange("q n s -> q (n s)")
+            h_grouped = h_grouped_tiles[c]
             nc.vector.tensor_tensor(out=h_grouped[:], in0=x_flat, in1=h_grouped[:], op=ALU.max)
-            for f in fillers[1:]:
-                f()
+
+        def quantise_h(c):
+            h_grouped = h_grouped_tiles[c]
             h_codes = first_pool.tile([P, BLOCK], U32, name="h_codes", align_bytes=64)
             h_scales = first_pool.tile([P, BLOCK], U8, name="h_scales", align_bytes=64)
             nc.vector.quantize_mx(out=h_codes[:].bitcast(FP8X4), scales=h_scales[:], in_=h_grouped[:])
@@ -255,13 +271,23 @@ def tile_gcnresnet_pa_t_kernel(tc, x_pre, A, W_gc2, out):
         def total_folded(c):
             by_row = sums_pool.tile([P, PACK, P], F32, name="by_row")
             nc.scalar.copy(out=by_row[:], in_=folded[c][:].rearrange("m (p t) -> m t p", t=PACK))
-            totals[c] = misc_psum.tile([P, PACK], F32, name="totals", tag="product")
+            totals[c] = misc_psum.tile([P, PACK, P], F32, name="totals", tag="product")
             for t in range(PACK):
-                nc.tensor.matmul(totals[c][:, t : t + 1], lhsT=by_row[:, t, :], rhs=one[:], start=True, stop=True)
+                if c in QUICK:
+                    nc.tensor.transpose(totals[c][:, t, :], by_row[:, t, :], identity[:])
+                else:
+                    nc.tensor.matmul(totals[c][:, 0, t : t + 1], lhsT=by_row[:, t, :], rhs=one[:], start=True, stop=True)
 
         def d_tensor(c):
             whole = sums_pool.tile([P, PACK], F32, name="whole")
-            nc.scalar.copy(out=whole[:], in_=totals[c][:])
+            if c in QUICK:
+                for t in range(PACK):
+                    junk = sums_pool.tile([P, P], BF16, name="junk")
+                    nc.scalar.activation(
+                        out=junk[:], in_=totals[c][:, t, :], func=ACT.Copy, accum_out=whole[:, t : t + 1]
+                    )
+            else:
+                nc.scalar.copy(out=whole[:], in_=totals[c][:, 0, :PACK])
             inverse_root(c, whole[:])
 
         def inverse_root(c, whole):
@@ -289,11 +315,15 @@ def tile_gcnresnet_pa_t_kernel(tc, x_pre, A, W_gc2, out):
         order = order + [(c, q) for q in (2, 3) for c in range(N_BLOCKS)]
 
         def scalar_rows(s):
+            if s < len(S_FIRST):
+                return S_FIRST[s]
             return SCALAR_SCALE_ROWS if busy_scalar[s] else S_FREE
 
         def gpsimd_columns(s):
             if order[s][1] >= ROUND_QUARTERS:
                 return GPSIMD_COLUMNS
+            if s < len(S_FIRST):
+                return 0
             return GC0 if scalar_rows(s) == SCALAR_SCALE_ROWS else GC0B
 
         def scale(s):
@@ -323,11 +353,16 @@ def tile_gcnresnet_pa_t_kernel(tc, x_pre, A, W_gc2, out):
                     )
             scaled_tiles[s] = scaled
 
+        def spread_half(s, k):
+            c, q = order[s]
+            d_banks[k] = spread_psum.tile([P, BLOCK], F32, name="d_bank", tag="spread")
+            spread_d(d_banks[k], 2 * q + k)
+
         def spread(s):
             c, q = order[s]
             for k in range(2):
-                d_banks[k] = spread_psum.tile([P, BLOCK], F32, name="d_bank", tag="spread")
-                spread_d(d_banks[k], 2 * q + k)
+                if s > 0 or k == 1 or not EARLY_SPREAD:
+                    spread_half(s, k)
             if q < ROUND_QUARTERS and (GC0 or GC0B) and q not in spread_quarters:
                 spread_quarters.add(q)
                 nc.scalar.copy(out=d_gpsimd[q][:], in_=d_banks[1][:, BLOCK - max(GC0, GC0B) :])
@@ -335,19 +370,8 @@ def tile_gcnresnet_pa_t_kernel(tc, x_pre, A, W_gc2, out):
         def multiply(s):
             c, q = order[s]
             scaled = scaled_tiles[s]
-            grouped = grouped_pool.tile([P, QUARTER, PACK], BF16, name="grouped", align_bytes=64)
-            grouped_tiles[s] = grouped
+            grouped = grouped_tiles[s]
             vector_columns = QUARTER - gpsimd_columns(s)
-            width = max(GC0, GC0B) if q < ROUND_QUARTERS else GPSIMD_COLUMNS
-            for i0 in range(vector_columns, QUARTER, P):
-                n = min(P, QUARTER - i0)
-                j0 = i0 - (QUARTER - width)
-                nc.gpsimd.tensor_tensor(
-                    out=grouped[:, i0 : i0 + n, :],
-                    in0=scaled[:, :, i0 : i0 + n].rearrange("p t i -> p i t"),
-                    in1=d_gpsimd[q][:, j0 : j0 + n].unsqueeze(2).to_broadcast([P, n, PACK]),
-                    op=ALU.mult,
-                )
             for k in range(2):
                 lo = k * BLOCK
                 columns = min(BLOCK, vector_columns - lo)
@@ -358,6 +382,22 @@ def tile_gcnresnet_pa_t_kernel(tc, x_pre, A, W_gc2, out):
                     .rearrange("p (n i) -> p n i", i=RUN)
                     .unsqueeze(2)
                     .to_broadcast([P, columns // RUN, PACK, RUN]),
+                    op=ALU.mult,
+                )
+
+        def multiply_gpsimd(s):
+            c, q = order[s]
+            scaled = scaled_tiles[s]
+            grouped = grouped_tiles[s]
+            vector_columns = QUARTER - gpsimd_columns(s)
+            width = max(GC0, GC0B) if q < ROUND_QUARTERS else GPSIMD_COLUMNS
+            for i0 in range(vector_columns, QUARTER, P):
+                n = min(P, QUARTER - i0)
+                j0 = i0 - (QUARTER - width)
+                nc.gpsimd.tensor_tensor(
+                    out=grouped[:, i0 : i0 + n, :],
+                    in0=scaled[:, :, i0 : i0 + n].rearrange("p t i -> p i t"),
+                    in1=d_gpsimd[q][:, j0 : j0 + n].unsqueeze(2).to_broadcast([P, n, PACK]),
                     op=ALU.mult,
                 )
 
@@ -462,7 +502,7 @@ def tile_gcnresnet_pa_t_kernel(tc, x_pre, A, W_gc2, out):
             if c in TENSOR_SUM_ROW_BLOCKS:
                 for n in range(4):
                     add(jobs, end - 1 - (3 - n) // FOLD_PER, lambda c=c, n=n: fold_sum_tile(c, n), -1)
-                add(pre_jobs, end, lambda c=c: total_folded(c))
+                add(jobs if c in QUICK else pre_jobs, end, lambda c=c: total_folded(c))
                 add(jobs, end, lambda c=c: d_tensor(c))
                 if c > 2:
                     queue.append((end - 1 - 3 // FOLD_PER - AHEAD_S, lambda c=c: load_sum(c)))
@@ -489,44 +529,59 @@ def tile_gcnresnet_pa_t_kernel(tc, x_pre, A, W_gc2, out):
                 queue.append((s - AHEAD_U, lambda k=(c, q): load(k)))
         for s, f in sorted(queue, key=lambda e: e[0]):
             add(loads, s, f, -1)
-        for c in range(N_BLOCKS + LAG):
+        for c in range(N_BLOCKS + 1):
             if c < N_BLOCKS:
                 turn_x(c, x_tiles[c // 2][:, c % 2])
-            if 0 < c <= N_BLOCKS:
-                n = c - 1 - V0
-                fillers = [
-                    lambda q=(2, 3)[m // PACK], t=m % PACK: sum_rows(0, q, a_tiles[(0, q)], (t,))
-                    for m in range(2 * n, 2 * n + 2)
-                    if 0 <= m < 2 * PACK
-                ]
-                quantise_h(c - 1, fillers)
-            if LAG <= c:
+                slope_times_x(c)
+            if c > 0:
+                quantise_h(c - 1)
+            if c < N_BLOCKS:
+                leaky_relu(c)
+            if c >= LAG:
                 quantise_support(c - LAG)
+            for n in range(2 * PACK):
+                if V_ROWS_AT[n // 2] == c:
+                    q, t = (2, 3)[n // PACK], n % PACK
+                    sum_rows(0, q, a_tiles[(0, q)], (t,))
             if S0 <= c < S0 + 4:
                 q = (0, 1)[(c - S0) // 2]
                 sum_rows(0, q, a_tiles[(0, q)], range(2 * ((c - S0) % 2), 2 * ((c - S0) % 2) + 2))
-            if c == max(V0 + 5, S0 + 4):
-                inverse_root(0, add_quarter_sums(0)[:])
-            if FOLD_AT <= c < FOLD_AT + 4:
-                fold_sum_tile(1, c - FOLD_AT)
-            if c == TOT_AT:
-                total_folded(1)
-            if c == TOT_AT + 1:
-                scale(0)
-                d_tensor(1)
-
+            for n in range(4):
+                if FOLD_C[n] == c:
+                    fold_sum_tile(1, n)
+        if TOT_FIRST:
+            total_folded(1)
+        for c in range(N_BLOCKS + 1 - LAG, N_BLOCKS):
+            quantise_support(c)
+        inverse_root(0, add_quarter_sums(0)[:])
+        if EARLY_SPREAD:
+            spread_half(0, 0)
+        if not TOT_FIRST:
+            total_folded(1)
+        if D1_FIRST:
+            d_tensor(1)
+        scale(0)
+        if not D1_FIRST:
+            d_tensor(1)
         steps = len(order)
         for f in loads.get(-1, []) + jobs.get(-1, []):
             f()
         for s in range(steps + MXLAG + 3):
             for f in loads.get(s, ()):
                 f()
-            for f in pre_jobs.get(s, ()):
-                f()
-            if s + 1 < steps:
-                scale(s + 1)
             if s < steps and (s == 0 or order[s][1] != order[s - 1][1]):
                 spread(s)
+            for f in pre_jobs.get(s, ()):
+                f()
+            if s < steps:
+                grouped = grouped_pool.tile([P, QUARTER, PACK], BF16, name="grouped", align_bytes=64)
+                grouped_tiles[s] = grouped
+            if GFIRST and s < steps:
+                multiply_gpsimd(s)
+            if s + 1 < steps:
+                scale(s + 1)
+            if not GFIRST and s < steps:
+                multiply_gpsimd(s)
             if s < steps:
                 multiply(s)
             if 1 <= s <= steps:

@@ -54,7 +54,7 @@ EARLY_SPREAD = 0
 TOT_FIRST = 1
 D1_FIRST = 1
 QUICK = (1,3)
-S_FIRST = (3,)
+S_FIRST = (2,)
 V_ROWS_AT = (4,5,6,7)
 S0 = 4
 LAG = 2
@@ -530,8 +530,11 @@ def tile_gcnresnet_pa_t_kernel(tc, x_pre, A, W_gc2, out):
         for s, f in sorted(queue, key=lambda e: e[0]):
             add(loads, s, f, -1)
         for c in range(N_BLOCKS + 1):
+            if c == 0:
+                turn_x(0, x_tiles[0][:, 0])
+            if c + 1 < N_BLOCKS:
+                turn_x(c + 1, x_tiles[(c + 1) // 2][:, (c + 1) % 2])
             if c < N_BLOCKS:
-                turn_x(c, x_tiles[c // 2][:, c % 2])
                 slope_times_x(c)
             if c > 0:
                 quantise_h(c - 1)

@@ -46,11 +46,15 @@ D0_AT = 8
 GFIRST = 0
 A_TILES = 10
 SCALAR_SCALE_ROWS = 1
-G1 = 3
+G1 = 4
 SCALED = 2
-GROUPED = 3
+GROUPED = 2
 MXLAG = 2
-EARLY_SPREAD = 0
+SPLIT_LAST = 1
+STORES = ((16, "e", 0), (17, "e", 1), (18, "r", 0), (19, "r", 1), (20, "e", 2), (21, "e", 3), (22, "r", 2), (23, "r", 3), (25, "e", 4), (26, "e", 5), (27, "r", 4), (28, "r", 5))
+HALF1 = 0
+V1_AT = (7, 8)
+XU = 0
 TOT_FIRST = 1
 D1_FIRST = 1
 QUICK = (1,3)
@@ -59,9 +63,9 @@ V_ROWS_AT = (4,5,6,7)
 S0 = 4
 LAG = 2
 FOLD_AT = 6
-AHEAD = 2
-AHEAD_S = 3
-AHEAD_U = 4
+AHEAD = 1
+AHEAD_S = 2
+AHEAD_U = 5
 
 
 def tile_gcnresnet_pa_t_kernel(tc, x_pre, A, W_gc2, out):
@@ -72,6 +76,7 @@ def tile_gcnresnet_pa_t_kernel(tc, x_pre, A, W_gc2, out):
     def piece(c):
         return 1024 if c in WIDE else 512
 
+    half_view = A.rearrange("(b r g) i -> b g r i", r=8, g=32)
     sum_views = {
         w: A.rearrange("n i -> (n i)").rearrange("(b r q w) -> b q r w", r=NODES // w, q=P, w=w)
         for w in {piece(c) for c in TENSOR_SUM_ROW_BLOCKS}
@@ -114,10 +119,10 @@ def tile_gcnresnet_pa_t_kernel(tc, x_pre, A, W_gc2, out):
         nc.gpsimd.memset(sums_scalar[:], 0.0)
         d = keep.tile([P, N_BLOCKS, PACK], F32, name="d")
         d_gpsimd = {}
-        for q in range(N_QUARTERS):
-            width = max(GC0, GC0B) if q < ROUND_QUARTERS else GPSIMD_COLUMNS
+        for b in range(1, N_BLOCKS, 2):
+            width = max(GC0, GC0B) if b < 2 * ROUND_QUARTERS else GPSIMD_COLUMNS
             if width:
-                d_gpsimd[q] = keep.tile([P, width], F32, name="d_gpsimd%d" % q)
+                d_gpsimd[b] = keep.tile([P, width], F32, name="d_gpsimd%d" % b)
         spread_quarters = set()
         support_codes = keep.tile([P, N_BLOCKS, FEAT_OUT], U32, name="support_codes", align_bytes=64)
         support_scales = keep.tile([P, N_BLOCKS, FEAT_OUT], U8, name="support_scales", align_bytes=64)
@@ -128,6 +133,18 @@ def tile_gcnresnet_pa_t_kernel(tc, x_pre, A, W_gc2, out):
             tile = a_pool.tile([P, PACK, QUARTER], BF16, name="a_quarter", tag="a")
             nc.sync.dma_start(out=tile[:], in_=a_view[c][:, :, q * QUARTER : (q + 1) * QUARTER])
             return tile
+
+        def load_half_sum_tiles(c):
+            tiles = []
+            for n in range(2):
+                tile = sum_pool.tile([P, 8, 512], BF16, name="a_sum", tag="a_sum")
+                for s in range(4):
+                    nc.sync.dma_start(
+                        out=tile[s:P:4, :, :],
+                        in_=half_view[c * 2 + n][:, :, NODES // 2 + s * 512 : NODES // 2 + (s + 1) * 512],
+                    )
+                tiles.append(tile)
+            return tiles
 
         def load_sum_tiles(c):
             tiles = []
@@ -218,7 +235,7 @@ def tile_gcnresnet_pa_t_kernel(tc, x_pre, A, W_gc2, out):
 
 
         def vector_sums(c, q):
-            return (c, q) in VECTOR_SUMS
+            return (c, q) in VECTOR_SUMS or (c == 1 and q < 2)
 
         def sum_rows(c, q, a_quarter, rows=range(PACK)):
             for t in rows:
@@ -257,15 +274,20 @@ def tile_gcnresnet_pa_t_kernel(tc, x_pre, A, W_gc2, out):
             tile = sum_tiles[c][n]
             w = piece(c)
             abreast = P * w // NODES
-            for r in range(NODES // w):
-                j0 = n * SUM_ROWS + r * abreast
-                for m in range(w // P):
+            steps_ = NODES // w
+            if HALF1 and c == 1:
+                steps_, abreast, wd = 8, 32, 512
+            else:
+                wd = w
+            for r in range(steps_):
+                j0 = (n * steps_ + r) * abreast
+                for m in range(wd // P):
                     nc.tensor.matmul(
                         folded[c][:, j0 : j0 + abreast],
                         lhsT=tile[:, r, m * P : (m + 1) * P],
-                        rhs=picks[w][:],
+                        rhs=picks[abreast * NODES // P][:],
                         start=(m == 0),
-                        stop=(m == w // P - 1),
+                        stop=(m == wd // P - 1),
                     )
 
         def total_folded(c):
@@ -288,6 +310,9 @@ def tile_gcnresnet_pa_t_kernel(tc, x_pre, A, W_gc2, out):
                     )
             else:
                 nc.scalar.copy(out=whole[:], in_=totals[c][:, 0, :PACK])
+            if HALF1 and c == 1:
+                for q in range(2):
+                    nc.gpsimd.tensor_tensor(out=whole[:], in0=whole[:], in1=sums_vector[:, 1, q, :], op=ALU.add)
             inverse_root(c, whole[:])
 
         def inverse_root(c, whole):
@@ -309,10 +334,23 @@ def tile_gcnresnet_pa_t_kernel(tc, x_pre, A, W_gc2, out):
         scaled_tiles = {}
         grouped_tiles = {}
         code_tiles = {}
-        d_banks = [None, None]
 
-        order = [(0, 0), (1, 0), (2, 0), (3, 0), (0, 1), (1, 1), (2, 1), (3, 1), (4, 1), (4, 0), (5, 0), (5, 1), (6, 1), (6, 0), (7, 0), (7, 1)]
-        order = order + [(c, q) for q in (2, 3) for c in range(N_BLOCKS)]
+        def whole(c, q):
+            return ((c, 2 * q), (c, 2 * q + 1))
+
+        order = [whole(0, 0), whole(1, 0), whole(2, 0)]
+        if XU:
+            order += [((0, 2), (1, 2)), whole(3, 0), ((2, 2), (3, 2)), ((0, 3), (1, 3)), ((2, 3), (3, 3))]
+        else:
+            order += [whole(3, 0), whole(0, 1), whole(1, 1), whole(2, 1), whole(3, 1)]
+        order += [whole(c, q) for c, q in ((4, 1), (4, 0), (5, 0), (5, 1), (6, 1), (6, 0), (7, 0), (7, 1))]
+        order += [whole(c, q) for q in (2, 3) for c in range(N_BLOCKS)]
+
+        def is_whole(s):
+            return order[s][0][0] == order[s][1][0]
+
+        def in_round_0(s):
+            return order[s][0][1] < 2 * ROUND_QUARTERS
 
         def scalar_rows(s):
             if s < len(S_FIRST):
@@ -320,65 +358,80 @@ def tile_gcnresnet_pa_t_kernel(tc, x_pre, A, W_gc2, out):
             return SCALAR_SCALE_ROWS if busy_scalar[s] else S_FREE
 
         def gpsimd_columns(s):
-            if order[s][1] >= ROUND_QUARTERS:
+            if not in_round_0(s):
                 return GPSIMD_COLUMNS
-            if s < len(S_FIRST):
+            if s < len(S_FIRST) or not is_whole(s):
                 return 0
             return GC0 if scalar_rows(s) == SCALAR_SCALE_ROWS else GC0B
 
-        def scale(s):
-            c, q = order[s]
+        def a_rows(c, b):
+            q = b // 2
+            lo = (b % 2) * BLOCK
             if c in ROW_TILES and q < ROUND_QUARTERS:
-                a_rows = [a_row_tiles[(c, t)][:, q * QUARTER : (q + 1) * QUARTER] for t in range(PACK)]
-            else:
-                a_rows = [a_tiles[(c, q)][:, t, :] for t in range(PACK)]
+                return [a_row_tiles[(c, t)][:, q * QUARTER + lo : (q + 1) * QUARTER] for t in range(PACK)]
+            return [a_tiles[(c, q)][:, t, lo:] for t in range(PACK)]
+
+        def scale(s):
             scaled = scaled_pool.tile([P, PACK, QUARTER], F32, name="scaled")
-            if q < ROUND_QUARTERS:
-                gs = range(scalar_rows(s), PACK)
+            if in_round_0(s):
+                gs = list(range(scalar_rows(s), PACK))
             else:
-                gs = range(PACK - 1, PACK) if G1 and s % G1 == 0 else ()
-            for t in list(gs) + [t for t in range(PACK) if t not in gs]:
-                if t in gs:
-                    nc.gpsimd.tensor_scalar(
-                        out=scaled[:, t, :],
-                        in0=a_rows[t],
-                        scalar1=d[:, c, t : t + 1],
-                        scalar2=0.0,
-                        op0=ALU.mult,
-                        op1=ALU.add,
-                    )
-                else:
-                    nc.scalar.activation(
-                        out=scaled[:, t, :], in_=a_rows[t], func=ACT.Copy, scale=d[:, c, t : t + 1]
-                    )
+                gs = [PACK - 1] if G1 and s % G1 == 0 else []
+            parts = [(order[s][0], 0, QUARTER)] if is_whole(s) else [(order[s][0], 0, BLOCK), (order[s][1], BLOCK, QUARTER)]
+            for t in gs + [t for t in range(PACK) if t not in gs]:
+                for (c, b), lo, hi in parts:
+                    row = a_rows(c, b)[t][:, : hi - lo]
+                    if t in gs:
+                        nc.gpsimd.tensor_scalar(
+                            out=scaled[:, t, lo:hi],
+                            in0=row,
+                            scalar1=d[:, c, t : t + 1],
+                            scalar2=0.0,
+                            op0=ALU.mult,
+                            op1=ALU.add,
+                        )
+                    else:
+                        nc.scalar.activation(
+                            out=scaled[:, t, lo:hi], in_=row, func=ACT.Copy, scale=d[:, c, t : t + 1]
+                        )
             scaled_tiles[s] = scaled
 
-        def spread_half(s, k):
-            c, q = order[s]
-            d_banks[k] = spread_psum.tile([P, BLOCK], F32, name="d_bank", tag="spread")
-            spread_d(d_banks[k], 2 * q + k)
+        d_banks = {}
+        recent = []
+        halves = {}
 
         def spread(s):
-            c, q = order[s]
-            for k in range(2):
-                if s > 0 or k == 1 or not EARLY_SPREAD:
-                    spread_half(s, k)
-            if q < ROUND_QUARTERS and (GC0 or GC0B) and q not in spread_quarters:
-                spread_quarters.add(q)
-                nc.scalar.copy(out=d_gpsimd[q][:], in_=d_banks[1][:, BLOCK - max(GC0, GC0B) :])
+            bs = [order[s][k][1] for k in range(2)]
+            halves[s] = sorted(range(2), key=lambda k: bs[k] not in d_banks)
+            for k in halves[s]:
+                b = bs[k]
+                if b in recent:
+                    recent.remove(b)
+                else:
+                    if len(recent) == 2:
+                        del_b = recent.pop(0)
+                        d_banks.pop(del_b)
+                    d_banks[b] = spread_psum.tile([P, BLOCK], F32, name="d_bank", tag="spread")
+                    spread_d(d_banks[b], b)
+                    if b in d_gpsimd and b < 2 * ROUND_QUARTERS and b not in spread_quarters:
+                        spread_quarters.add(b)
+                        nc.scalar.copy(out=d_gpsimd[b][:], in_=d_banks[b][:, BLOCK - max(GC0, GC0B) :])
+                recent.append(b)
+            bank_tiles[s] = [d_banks[b] for b in bs]
+
+        bank_tiles = {}
 
         def multiply(s):
-            c, q = order[s]
             scaled = scaled_tiles[s]
             grouped = grouped_tiles[s]
             vector_columns = QUARTER - gpsimd_columns(s)
-            for k in range(2):
+            for k in halves[s]:
                 lo = k * BLOCK
                 columns = min(BLOCK, vector_columns - lo)
                 nc.vector.tensor_tensor(
                     out=grouped[:, lo : lo + columns, :].rearrange("p (n i) t -> p n t i", i=RUN),
                     in0=scaled[:, :, lo : lo + columns].rearrange("p t (n i) -> p n t i", i=RUN),
-                    in1=d_banks[k][:, :columns]
+                    in1=bank_tiles[s][k][:, :columns]
                     .rearrange("p (n i) -> p n i", i=RUN)
                     .unsqueeze(2)
                     .to_broadcast([P, columns // RUN, PACK, RUN]),
@@ -386,18 +439,18 @@ def tile_gcnresnet_pa_t_kernel(tc, x_pre, A, W_gc2, out):
                 )
 
         def multiply_gpsimd(s):
-            c, q = order[s]
+            b = order[s][1][1]
             scaled = scaled_tiles[s]
             grouped = grouped_tiles[s]
             vector_columns = QUARTER - gpsimd_columns(s)
-            width = max(GC0, GC0B) if q < ROUND_QUARTERS else GPSIMD_COLUMNS
+            width = max(GC0, GC0B) if in_round_0(s) else GPSIMD_COLUMNS
             for i0 in range(vector_columns, QUARTER, P):
                 n = min(P, QUARTER - i0)
                 j0 = i0 - (QUARTER - width)
                 nc.gpsimd.tensor_tensor(
                     out=grouped[:, i0 : i0 + n, :],
                     in0=scaled[:, :, i0 : i0 + n].rearrange("p t i -> p i t"),
-                    in1=d_gpsimd[q][:, j0 : j0 + n].unsqueeze(2).to_broadcast([P, n, PACK]),
+                    in1=d_gpsimd[b][:, j0 : j0 + n].unsqueeze(2).to_broadcast([P, n, PACK]),
                     op=ALU.mult,
                 )
 
@@ -409,11 +462,10 @@ def tile_gcnresnet_pa_t_kernel(tc, x_pre, A, W_gc2, out):
             )
             code_tiles[s] = (codes, scales)
 
-        def accumulate(s):
-            c, q = order[s]
+        def accumulate(s, ks=(0, 1)):
             codes, scales = code_tiles[s]
-            for k in range(2):
-                b = 2 * q + k
+            for k in ks:
+                c, b = order[s][k]
                 if b not in acc:
                     acc[b] = acc_psum.tile([P, BLOCK], F32, name="acc", tag="acc")
                     passes[b] = 0
@@ -467,8 +519,13 @@ def tile_gcnresnet_pa_t_kernel(tc, x_pre, A, W_gc2, out):
             if m == 0:
                 quantise_w()
         load_block(0)
-        sum_tiles[1] = load_sum_tiles(1)
-        load((1, 0))
+        if HALF1:
+            load((1, 0))
+            sum_tiles[1] = load_half_sum_tiles(1)
+            load((1, 1))
+        else:
+            sum_tiles[1] = load_sum_tiles(1)
+            load((1, 0))
         if 2 in TENSOR_SUM_ROW_BLOCKS:
             sum_tiles[2] = load_sum_tiles(2)
             load((2, 0))
@@ -486,8 +543,7 @@ def tile_gcnresnet_pa_t_kernel(tc, x_pre, A, W_gc2, out):
             sum_tiles[c] = load_sum_tiles(c)
 
         busy_scalar = [False] * (len(order) + 1)
-        first_use = {c: min(s for s in range(len(order)) if order[s][0] == c or order[s][1] == c // 2) for c in range(N_BLOCKS)}
-        first_use = {c: min(s for s in range(len(order)) if order[s][0] == c) for c in range(N_BLOCKS)}
+        first_use = {c: min(s for s in range(len(order)) if c in (order[s][0][0], order[s][1][0])) for c in range(N_BLOCKS)}
         jobs = {}
         loads = {}
 
@@ -518,15 +574,12 @@ def tile_gcnresnet_pa_t_kernel(tc, x_pre, A, W_gc2, out):
                 add(jobs, end, lambda c=c: d_scalar(c))
                 if c > 2:
                     queue.append((end - 3 - AHEAD, lambda c=c: load_block(c)))
-            if c in TENSOR_SUM_ROW_BLOCKS:
-                wanted = [(c, q) for q in range(ROUND_QUARTERS)]
-                for s in range(len(order)):
-                    if order[s] in wanted and order[s] != (2, 0):
-                        queue.append((s - AHEAD_U, lambda k=order[s]: load(k)))
+        queued = {(1, 0), (2, 0)} | ({(1, 1)} if HALF1 else set()) | {(c, q) for c in range(N_BLOCKS) if c not in TENSOR_SUM_ROW_BLOCKS for q in range(ROUND_QUARTERS)}
         for s in range(len(order)):
-            c, q = order[s]
-            if (q < ROUND_QUARTERS and c == 1 and q == 1) or q >= ROUND_QUARTERS:
-                queue.append((s - AHEAD_U, lambda k=(c, q): load(k)))
+            for c, b in order[s]:
+                if (c, b // 2) not in queued:
+                    queued.add((c, b // 2))
+                    queue.append((s - AHEAD_U, lambda k=(c, b // 2): load(k)))
         for s, f in sorted(queue, key=lambda e: e[0]):
             add(loads, s, f, -1)
         for c in range(N_BLOCKS + 1):
@@ -549,16 +602,18 @@ def tile_gcnresnet_pa_t_kernel(tc, x_pre, A, W_gc2, out):
             if S0 <= c < S0 + 4:
                 q = (0, 1)[(c - S0) // 2]
                 sum_rows(0, q, a_tiles[(0, q)], range(2 * ((c - S0) % 2), 2 * ((c - S0) % 2) + 2))
-            for n in range(4):
+            for n in range(2 if HALF1 else 4):
                 if FOLD_C[n] == c:
                     fold_sum_tile(1, n)
+            if HALF1:
+                for n in range(2 * PACK):
+                    if V1_AT[n // 4] == c:
+                        sum_rows(1, n // PACK, a_tiles[(1, n // PACK)], (n % PACK,))
         if TOT_FIRST:
             total_folded(1)
         for c in range(N_BLOCKS + 1 - LAG, N_BLOCKS):
             quantise_support(c)
         inverse_root(0, add_quarter_sums(0)[:])
-        if EARLY_SPREAD:
-            spread_half(0, 0)
         if not TOT_FIRST:
             total_folded(1)
         if D1_FIRST:
@@ -572,7 +627,7 @@ def tile_gcnresnet_pa_t_kernel(tc, x_pre, A, W_gc2, out):
         for s in range(steps + MXLAG + 3):
             for f in loads.get(s, ()):
                 f()
-            if s < steps and (s == 0 or order[s][1] != order[s - 1][1]):
+            if s < steps:
                 spread(s)
             for f in pre_jobs.get(s, ()):
                 f()
@@ -587,24 +642,51 @@ def tile_gcnresnet_pa_t_kernel(tc, x_pre, A, W_gc2, out):
                 multiply_gpsimd(s)
             if s < steps:
                 multiply(s)
-            if 1 <= s <= steps:
+            if 1 <= s < steps or (s == steps and not SPLIT_LAST):
                 quantise(s - 1)
-            if MXLAG <= s < steps + MXLAG:
+            if MXLAG <= s < steps + MXLAG - (1 if SPLIT_LAST else 0):
                 accumulate(s - MXLAG)
+            if SPLIT_LAST and s == steps:
+                codes = codes_pool.tile([P, QUARTER], U32, name="codes", align_bytes=64)
+                scales = codes_pool.tile([P, QUARTER], U8, name="scales", align_bytes=64)
+                code_tiles[s - 1] = (codes, scales)
+                for k in range(2):
+                    half = slice(k * BLOCK, (k + 1) * BLOCK)
+                    nc.vector.quantize_mx(
+                        out=codes[:, half].bitcast(FP8X4),
+                        scales=scales[:, half],
+                        in_=grouped_tiles[s - 1][:, half, :].rearrange("p i t -> p (i t)"),
+                    )
+                    accumulate(s - 1, (k,))
             for f in jobs.get(s, ()):
                 f()
             if s in (13, 14):
                 j = s - 13
                 d_turned = misc_psum.tile([P, BLOCK], F32, name="d_turned", tag="rows")
                 spread_d(d_turned, 2 * (j + ROUND_QUARTERS) + 1)
-                nc.scalar.copy(out=d_gpsimd[j + ROUND_QUARTERS][:], in_=d_turned[:, BLOCK - GPSIMD_COLUMNS :])
-            for s0, b in ((16, 0), (17, 1), (18, 2), (19, 3), (25, 4), (26, 5)):
-                if s == s0 + 1:
+                nc.scalar.copy(out=d_gpsimd[2 * (j + ROUND_QUARTERS) + 1][:], in_=d_turned[:, BLOCK - GPSIMD_COLUMNS :])
+            for s0, kind, b in STORES:
+                if s == s0 and kind == "e":
+                    empty_bank(b, nc.scalar.copy, ("rows", "product")[b % 2])
+                elif s == s0:
                     store_rows(b, nc.scalar.copy, nc.scalar)
-            for s0, b in ((16, 0), (17, 1), (18, 2), (19, 3), (25, 4), (26, 5)):
-                if s == s0:
-                    empty_bank(b, nc.scalar.copy, "rows")
-        empty_bank(N_BLOCKS - 2, nc.scalar.copy, "rows")
-        empty_bank(N_BLOCKS - 1, nc.vector.tensor_copy, "product")
-        store_rows(N_BLOCKS - 2, nc.scalar.copy, nc.sync)
-        store_rows(N_BLOCKS - 1, nc.vector.tensor_copy, nc.sync)
+        if not SPLIT_LAST:
+            empty_bank(N_BLOCKS - 2, nc.scalar.copy, "rows")
+            empty_bank(N_BLOCKS - 1, nc.vector.tensor_copy, "product")
+            store_rows(N_BLOCKS - 2, nc.scalar.copy, nc.sync)
+            store_rows(N_BLOCKS - 1, nc.vector.tensor_copy, nc.sync)
+        else:
+            empty_bank(N_BLOCKS - 2, nc.scalar.copy, "rows")
+            b = N_BLOCKS - 1
+            out_t = out_pool.tile([P, BLOCK], F32, name="out_t")
+            rows_psum = misc_psum.tile([P, BLOCK // P, FEAT_OUT], F32, name="rows_psum", tag="product")
+            rows = out_pool.tile([P, BLOCK // P, FEAT_OUT], F32, name="rows")
+            engines = (nc.vector.tensor_copy, nc.scalar.copy)
+            for k in range(2):
+                engines[k](out=out_t[:, k * 256 : (k + 1) * 256], in_=acc[b][:, k * 256 : (k + 1) * 256])
+                for u in (2 * k, 2 * k + 1):
+                    nc.tensor.transpose(rows_psum[:, u, :], out_t[:, P * u : P * (u + 1)], identity[:])
+            store_rows(N_BLOCKS - 2, nc.scalar.copy, nc.sync)
+            for k in range(2):
+                engines[k](out=rows[:, 2 * k : 2 * k + 2, :], in_=rows_psum[:, 2 * k : 2 * k + 2, :])
+            nc.sync.dma_start(out=out_view[b], in_=rows[:])

@@ -20,52 +20,25 @@ SLOPE = 0.2
 BLOCK = P * PACK
 N_BLOCKS = NODES // BLOCK
 QUARTER = 2 * BLOCK
-N_QUARTERS = NODES // QUARTER
 ROUND_QUARTERS = 2
 RUN = 4
 FLOPS = 2 * NODES * FEAT_IN * FEAT_OUT + 2 * NODES * NODES * FEAT_OUT
 
 TENSOR_SUM_ROW_BLOCKS = (1, 3, 5, 7)
-SUM_ROWS = P
-WIDE = (1, 3, 5)
-ROW_TILES = (4, 6)
+PIECE = {1: 1024, 3: 1024, 5: 1024, 7: 512}
+SUM_TILE_ROWS = P
 SUM_TILES = 4
-VECTOR_SUMS = ((0, 2), (0, 3), (2, 2), (2, 3))
-GPSIMD_COLUMNS = 256
-GC0 = 0
-GC0B = 128
-S_FREE = 3
-FOLD_PER = 4
-END_S = 2
-END_T = 2
-TOT_AT = 9
-SC_AT = 9
-FOLD_C = (6,7,7,7)
-D1_AT = 9
-D0_AT = 8
-GFIRST = 0
+QUICK_SUM_ROW_BLOCKS = (1, 3)
+WHOLE_ROW_BLOCKS = (4, 6)
+LOAD_ORDER = (0, 2, 1, 3)
 A_TILES = 10
-SCALAR_SCALE_ROWS = 1
-G1 = 4
-SCALED = 2
-GROUPED = 2
-MXLAG = 2
-SPLIT_LAST = 1
-STORES = ((16, "e", 0), (17, "e", 1), (18, "r", 0), (19, "r", 1), (20, "e", 2), (21, "e", 3), (22, "r", 2), (23, "r", 3), (25, "e", 4), (26, "e", 5), (27, "r", 4), (28, "r", 5))
-HALF1 = 0
-V1_AT = (7, 8)
-XU = 0
-TOT_FIRST = 1
-D1_FIRST = 1
-QUICK = (1,3)
-S_FIRST = (2,)
-V_ROWS_AT = (4,5,6,7)
-S0 = 4
-LAG = 2
-FOLD_AT = 6
-AHEAD = 1
-AHEAD_S = 2
-AHEAD_U = 5
+LOAD_AHEAD = 5
+UNIT_0_SCALAR_ROWS = 2
+BUSY_SCALAR_ROWS = 1
+FREE_SCALAR_ROWS = 3
+GPSIMD_COLUMNS_0 = P
+GPSIMD_COLUMNS_1 = 2 * P
+GPSIMD_ROW_EVERY = 4
 
 
 def tile_gcnresnet_pa_t_kernel(tc, x_pre, A, W_gc2, out):
@@ -73,38 +46,34 @@ def tile_gcnresnet_pa_t_kernel(tc, x_pre, A, W_gc2, out):
     a_view = A.rearrange("(c p t) i -> c p t i", p=P, t=PACK)
     x_view = x_pre.rearrange("(m h p t) k -> m p h t k", h=2, p=P, t=PACK)
     out_view = out.rearrange("(b u p) f -> b p u f", u=BLOCK // P, p=P)
-    def piece(c):
-        return 1024 if c in WIDE else 512
-
-    half_view = A.rearrange("(b r g) i -> b g r i", r=8, g=32)
     sum_views = {
-        w: A.rearrange("n i -> (n i)").rearrange("(b r q w) -> b q r w", r=NODES // w, q=P, w=w)
-        for w in {piece(c) for c in TENSOR_SUM_ROW_BLOCKS}
+        w: A.rearrange("n i -> (n i)").rearrange("(n r q w) -> n q r w", r=NODES // w, q=P, w=w)
+        for w in (1024, 512)
     }
 
     with ExitStack() as ctx:
         keep = ctx.enter_context(tc.tile_pool(name="keep", bufs=1))
         a_pool = ctx.enter_context(tc.tile_pool(name="a_pool", bufs=A_TILES))
         sum_pool = ctx.enter_context(tc.tile_pool(name="sum_pool", bufs=SUM_TILES))
-        scaled_pool = ctx.enter_context(tc.tile_pool(name="scaled_pool", bufs=SCALED))
-        grouped_pool = ctx.enter_context(tc.tile_pool(name="grouped_pool", bufs=GROUPED))
+        scaled_pool = ctx.enter_context(tc.tile_pool(name="scaled_pool", bufs=2))
+        grouped_pool = ctx.enter_context(tc.tile_pool(name="grouped_pool", bufs=3))
         codes_pool = ctx.enter_context(tc.tile_pool(name="codes_pool", bufs=3))
         first_pool = ctx.enter_context(tc.tile_pool(name="first_pool", bufs=2))
         sums_pool = ctx.enter_context(tc.tile_pool(name="sums_pool", bufs=2))
         out_pool = ctx.enter_context(tc.tile_pool(name="out_pool", bufs=2))
         spread_psum = ctx.enter_context(tc.psum_pool(name="spread_psum", bufs=2))
         acc_psum = ctx.enter_context(tc.psum_pool(name="acc_psum", bufs=ROUND_QUARTERS * 2))
-        misc_psum = ctx.enter_context(tc.psum_pool(name="misc_psum", bufs=1))
+        side_psum = ctx.enter_context(tc.psum_pool(name="side_psum", bufs=1))
         ctx.enter_context(tc.manual_schedule())
 
         identity = keep.tile([P, P], F32, name="identity")
         make_identity(nc, identity[:])
         picks = {}
-        for w in sum_views:
+        for w in (1024, 512):
             pick_f32 = keep.tile([P, P * w // NODES], F32, name="pick_f32_%d" % w)
             nc.vector.reduce_sum(
                 out=pick_f32[:],
-                in_=identity[:].rearrange("q (g c) -> q g c", c=NODES // w),
+                in_=identity[:].rearrange("q (g e) -> q g e", e=NODES // w),
                 axis=mybir.AxisListType.X,
             )
             picks[w] = keep.tile([P, P * w // NODES], BF16, name="pick_%d" % w)
@@ -113,48 +82,52 @@ def tile_gcnresnet_pa_t_kernel(tc, x_pre, A, W_gc2, out):
         nc.gpsimd.memset(one[:], 1.0)
         minus_half = keep.tile([P, PACK], F32, name="minus_half")
         nc.gpsimd.memset(minus_half[:], -0.5)
-        load_order = (0, 2, 1, 3)
-        sums_scalar = keep.tile([P, N_BLOCKS, N_QUARTERS, PACK], F32, name="sums_scalar")
-        sums_vector = keep.tile([P, N_BLOCKS, N_QUARTERS, PACK], F32, name="sums_vector")
-        nc.gpsimd.memset(sums_scalar[:], 0.0)
+        sums_scalar = keep.tile([P, N_BLOCKS, 4, PACK], F32, name="sums_scalar")
+        sums_vector = keep.tile([P, N_BLOCKS, 4, PACK], F32, name="sums_vector")
         d = keep.tile([P, N_BLOCKS, PACK], F32, name="d")
-        d_gpsimd = {}
-        for b in range(1, N_BLOCKS, 2):
-            width = max(GC0, GC0B) if b < 2 * ROUND_QUARTERS else GPSIMD_COLUMNS
-            if width:
-                d_gpsimd[b] = keep.tile([P, width], F32, name="d_gpsimd%d" % b)
-        spread_quarters = set()
+        d_gpsimd = []
+        for q in range(2 * ROUND_QUARTERS):
+            width = GPSIMD_COLUMNS_0 if q < ROUND_QUARTERS else GPSIMD_COLUMNS_1
+            d_columns = keep.tile([P, width], F32, name="d_gpsimd_%d" % q)
+            d_gpsimd.append(d_columns)
         support_codes = keep.tile([P, N_BLOCKS, FEAT_OUT], U32, name="support_codes", align_bytes=64)
         support_scales = keep.tile([P, N_BLOCKS, FEAT_OUT], U8, name="support_scales", align_bytes=64)
         w_codes = keep.tile([P, FEAT_OUT], U32, name="w_codes", align_bytes=64)
         w_scales = keep.tile([P, FEAT_OUT], U8, name="w_scales", align_bytes=64)
 
+
+        x_pairs = []
+        a_tiles = {}
+        sum_tiles = {}
+
+        def load_x_pair(m):
+            x_pair = a_pool.tile([P, 2, PACK, FEAT_IN], BF16, name="x_pair", tag="a")
+            nc.sync.dma_start(out=x_pair[:], in_=x_view[m])
+            x_pairs.append(x_pair)
+
         def load_quarter(c, q):
             tile = a_pool.tile([P, PACK, QUARTER], BF16, name="a_quarter", tag="a")
             nc.sync.dma_start(out=tile[:], in_=a_view[c][:, :, q * QUARTER : (q + 1) * QUARTER])
-            return tile
+            a_tiles[(c, q)] = tile
 
-        def load_half_sum_tiles(c):
-            tiles = []
-            for n in range(2):
-                tile = sum_pool.tile([P, 8, 512], BF16, name="a_sum", tag="a_sum")
-                for s in range(4):
-                    nc.sync.dma_start(
-                        out=tile[s:P:4, :, :],
-                        in_=half_view[c * 2 + n][:, :, NODES // 2 + s * 512 : NODES // 2 + (s + 1) * 512],
-                    )
-                tiles.append(tile)
-            return tiles
+        def load_whole_rows(c):
+            for t in range(PACK):
+                tile = a_pool.tile([P, NODES], BF16, name="a_row", tag="a")
+                nc.sync.dma_start(out=tile[:], in_=a_view[c][:, t, :])
+                a_tiles[(c, "row", t)] = tile
 
-        def load_sum_tiles(c):
-            tiles = []
-            for n in range(BLOCK // SUM_ROWS):
-                w = piece(c)
+        def load_second_copy(c):
+            w = PIECE[c]
+            sum_tiles[c] = []
+            for n in range(SUM_TILES):
                 tile = sum_pool.tile([P, NODES // w, w], BF16, name="a_sum", tag="a_sum")
-                nc.sync.dma_start(out=tile[:], in_=sum_views[w][c * (BLOCK // SUM_ROWS) + n])
-                tiles.append(tile)
-            return tiles
+                nc.sync.dma_start(out=tile[:], in_=sum_views[w][c * SUM_TILES + n])
+                sum_tiles[c].append(tile)
 
+
+        x_grouped = {}
+        h_grouped = {}
+        products = {}
 
         def quantise_w():
             w_rows = keep.tile([P, PACK, FEAT_OUT], BF16, name="w_rows")
@@ -171,13 +144,10 @@ def tile_gcnresnet_pa_t_kernel(tc, x_pre, A, W_gc2, out):
                 in_=w_grouped[:].rearrange("q f s -> q (f s)"),
             )
 
-        x_grouped_tiles = {}
-        h_tiles = {}
-
-        def turn_x(c, x_rows):
-            x_words = x_rows.bitcast(F32)
-            x_grouped = first_pool.tile([P, BLOCK, PACK], BF16, name="x_grouped", align_bytes=64)
-            x_grouped_words = x_grouped[:].bitcast(F32)
+        def turn_x(c):
+            x_words = x_pairs[c // 2][:, c % 2].bitcast(F32)
+            grouped = first_pool.tile([P, BLOCK, PACK], BF16, name="x_grouped", align_bytes=64)
+            grouped_words = grouped[:].bitcast(F32)
             for half in range(2):
                 turned = spread_psum.tile([P, 2, 2, P], F32, name="turned", tag="spread")
                 for t in range(2):
@@ -186,35 +156,28 @@ def tile_gcnresnet_pa_t_kernel(tc, x_pre, A, W_gc2, out):
                             turned[:, t, u, :], x_words[:, 2 * half + t, P * u : P * u + P], identity[:]
                         )
                 nc.scalar.copy(
-                    out=x_grouped_words[:, 2 * P * half : 2 * P * (half + 1), :].rearrange(
-                        "q (t p) u -> q t p u", t=2
-                    ),
+                    out=grouped_words[:, 2 * P * half : 2 * P * (half + 1), :].rearrange("q (t p) u -> q t p u", t=2),
                     in_=turned[:].rearrange("q t u p -> q t p u"),
                 )
-            x_grouped_tiles[c] = x_grouped
-
-        h_grouped_tiles = {}
+            x_grouped[c] = grouped[:].rearrange("q n s -> q (n s)")
 
         def slope_times_x(c):
-            x_flat = x_grouped_tiles[c][:].rearrange("q n s -> q (n s)")
-            h_grouped = first_pool.tile([P, BLOCK * PACK], BF16, name="h_grouped", align_bytes=64)
-            nc.vector.tensor_scalar(out=h_grouped[:], in0=x_flat, scalar1=SLOPE, scalar2=None, op0=ALU.mult)
-            h_grouped_tiles[c] = h_grouped
+            h_grouped[c] = first_pool.tile([P, BLOCK * PACK], BF16, name="h_grouped", align_bytes=64)
+            nc.vector.tensor_scalar(
+                out=h_grouped[c][:], in0=x_grouped[c], scalar1=SLOPE, scalar2=None, op0=ALU.mult
+            )
 
         def leaky_relu(c):
-            x_flat = x_grouped_tiles[c][:].rearrange("q n s -> q (n s)")
-            h_grouped = h_grouped_tiles[c]
-            nc.vector.tensor_tensor(out=h_grouped[:], in0=x_flat, in1=h_grouped[:], op=ALU.max)
+            nc.vector.tensor_tensor(out=h_grouped[c][:], in0=x_grouped[c], in1=h_grouped[c][:], op=ALU.max)
 
-        def quantise_h(c):
-            h_grouped = h_grouped_tiles[c]
+        def multiply_h(c):
             h_codes = first_pool.tile([P, BLOCK], U32, name="h_codes", align_bytes=64)
             h_scales = first_pool.tile([P, BLOCK], U8, name="h_scales", align_bytes=64)
-            nc.vector.quantize_mx(out=h_codes[:].bitcast(FP8X4), scales=h_scales[:], in_=h_grouped[:])
-            product = acc_psum.tile([P, PACK, FEAT_OUT], F32, name="product", tag="acc")
+            nc.vector.quantize_mx(out=h_codes[:].bitcast(FP8X4), scales=h_scales[:], in_=h_grouped[c][:])
+            products[c] = acc_psum.tile([P, PACK, FEAT_OUT], F32, name="product", tag="acc")
             for t in range(PACK):
                 nc.tensor.matmul_mx(
-                    out=product[:, t, :],
+                    out=products[c][:, t, :],
                     lhsT=h_codes[:, P * t : P * (t + 1)].bitcast(FP8X4),
                     lhsT_scale=h_scales[:, P * t : P * (t + 1)],
                     rhs=w_codes[:].bitcast(FP8X4),
@@ -222,11 +185,10 @@ def tile_gcnresnet_pa_t_kernel(tc, x_pre, A, W_gc2, out):
                     start=True,
                     stop=True,
                 )
-            h_tiles[c] = product
 
         def quantise_support(c):
             s_grouped = first_pool.tile([P, FEAT_OUT, PACK], BF16, name="s_grouped", align_bytes=64)
-            nc.scalar.copy(out=s_grouped[:], in_=h_tiles[c][:].rearrange("p t f -> p f t"))
+            nc.scalar.copy(out=s_grouped[:], in_=products[c][:].rearrange("p t f -> p f t"))
             nc.vector.quantize_mx(
                 out=support_codes[:, c, :].bitcast(FP8X4),
                 scales=support_scales[:, c, :],
@@ -234,89 +196,82 @@ def tile_gcnresnet_pa_t_kernel(tc, x_pre, A, W_gc2, out):
             )
 
 
-        def vector_sums(c, q):
-            return (c, q) in VECTOR_SUMS or (c == 1 and q < 2)
+        def sum_on_scalar(row, total):
+            nc.scalar.activation(out=row, in_=row, func=ACT.Copy, accum_out=total)
 
-        def sum_rows(c, q, a_quarter, rows=range(PACK)):
+        def sum_on_vector(row, total):
+            nc.vector.tensor_scalar(
+                out=row, in0=row, scalar1=1.0, scalar2=None, op0=ALU.mult, op1=ALU.add, accum_out=total
+            )
+
+        def sum_quarter_rows(c, q, rows):
             for t in rows:
-                row = a_quarter[:, t, :]
-                if vector_sums(c, q):
-                    nc.vector.tensor_scalar(
-                        out=row,
-                        in0=row,
-                        scalar1=1.0,
-                        scalar2=None,
-                        op0=ALU.mult,
-                        op1=ALU.add,
-                        accum_out=sums_vector[:, c, q, t : t + 1],
-                    )
+                if q < ROUND_QUARTERS:
+                    sum_on_scalar(a_tiles[(c, q)][:, t, :], sums_scalar[:, c, q, t : t + 1])
                 else:
-                    nc.scalar.activation(out=row, in_=row, func=ACT.Copy, accum_out=sums_scalar[:, c, q, t : t + 1])
+                    sum_on_vector(a_tiles[(c, q)][:, t, :], sums_vector[:, c, q, t : t + 1])
 
-        def quarter_sum(c, q):
-            return sums_vector[:, c, q, :] if vector_sums(c, q) else sums_scalar[:, c, q, :]
+        def sum_whole_row(c, t):
+            sum_on_scalar(a_tiles[(c, "row", t)][:], sums_scalar[:, c, 0, t : t + 1])
 
-        def add_quarter_sums(c):
+        def inverse_root(c, row_sums):
+            nc.gpsimd.tensor_tensor(out=d[:, c, :], in0=row_sums, in1=minus_half[:], op=ALU.pow)
+
+        def d_of_quarter_sums(c):
             left = sums_pool.tile([P, PACK], F32, name="left")
-            nc.gpsimd.tensor_tensor(out=left[:], in0=quarter_sum(c, 0), in1=quarter_sum(c, 1), op=ALU.add)
+            nc.gpsimd.tensor_tensor(
+                out=left[:], in0=sums_scalar[:, c, 0, :], in1=sums_scalar[:, c, 1, :], op=ALU.add
+            )
             right = sums_pool.tile([P, PACK], F32, name="right")
-            nc.gpsimd.tensor_tensor(out=right[:], in0=quarter_sum(c, 2), in1=quarter_sum(c, 3), op=ALU.add)
-            whole = sums_pool.tile([P, PACK], F32, name="whole")
-            nc.gpsimd.tensor_tensor(out=whole[:], in0=left[:], in1=right[:], op=ALU.add)
-            return whole
+            nc.gpsimd.tensor_tensor(
+                out=right[:], in0=sums_vector[:, c, 2, :], in1=sums_vector[:, c, 3, :], op=ALU.add
+            )
+            row_sums = sums_pool.tile([P, PACK], F32, name="row_sums")
+            nc.gpsimd.tensor_tensor(out=row_sums[:], in0=left[:], in1=right[:], op=ALU.add)
+            inverse_root(c, row_sums[:])
 
         folded = {}
         totals = {}
 
-        def fold_sum_tile(c, n):
+        def fold(c, n):
             if n == 0:
-                folded[c] = misc_psum.tile([P, BLOCK], F32, name="folded", tag="rows")
-            tile = sum_tiles[c][n]
-            w = piece(c)
+                folded[c] = side_psum.tile([P, BLOCK], F32, name="folded", tag="even")
+            w = PIECE[c]
             abreast = P * w // NODES
-            steps_ = NODES // w
-            if HALF1 and c == 1:
-                steps_, abreast, wd = 8, 32, 512
-            else:
-                wd = w
-            for r in range(steps_):
-                j0 = (n * steps_ + r) * abreast
-                for m in range(wd // P):
+            for r in range(NODES // w):
+                j0 = n * SUM_TILE_ROWS + r * abreast
+                for m in range(w // P):
                     nc.tensor.matmul(
                         folded[c][:, j0 : j0 + abreast],
-                        lhsT=tile[:, r, m * P : (m + 1) * P],
-                        rhs=picks[abreast * NODES // P][:],
+                        lhsT=sum_tiles[c][n][:, r, m * P : (m + 1) * P],
+                        rhs=picks[w][:],
                         start=(m == 0),
-                        stop=(m == wd // P - 1),
+                        stop=(m == w // P - 1),
                     )
 
-        def total_folded(c):
+        def total(c):
             by_row = sums_pool.tile([P, PACK, P], F32, name="by_row")
             nc.scalar.copy(out=by_row[:], in_=folded[c][:].rearrange("m (p t) -> m t p", t=PACK))
-            totals[c] = misc_psum.tile([P, PACK, P], F32, name="totals", tag="product")
+            totals[c] = side_psum.tile([P, PACK, P], F32, name="totals", tag="odd")
             for t in range(PACK):
-                if c in QUICK:
+                if c in QUICK_SUM_ROW_BLOCKS:
                     nc.tensor.transpose(totals[c][:, t, :], by_row[:, t, :], identity[:])
                 else:
-                    nc.tensor.matmul(totals[c][:, 0, t : t + 1], lhsT=by_row[:, t, :], rhs=one[:], start=True, stop=True)
+                    nc.tensor.matmul(
+                        totals[c][:, 0, t : t + 1], lhsT=by_row[:, t, :], rhs=one[:], start=True, stop=True
+                    )
 
-        def d_tensor(c):
-            whole = sums_pool.tile([P, PACK], F32, name="whole")
-            if c in QUICK:
+        def d_of_total(c):
+            row_sums = sums_pool.tile([P, PACK], F32, name="row_sums")
+            if c in QUICK_SUM_ROW_BLOCKS:
                 for t in range(PACK):
-                    junk = sums_pool.tile([P, P], BF16, name="junk")
+                    unused = sums_pool.tile([P, P], BF16, name="unused")
                     nc.scalar.activation(
-                        out=junk[:], in_=totals[c][:, t, :], func=ACT.Copy, accum_out=whole[:, t : t + 1]
+                        out=unused[:], in_=totals[c][:, t, :], func=ACT.Copy, accum_out=row_sums[:, t : t + 1]
                     )
             else:
-                nc.scalar.copy(out=whole[:], in_=totals[c][:, 0, :PACK])
-            if HALF1 and c == 1:
-                for q in range(2):
-                    nc.gpsimd.tensor_tensor(out=whole[:], in0=whole[:], in1=sums_vector[:, 1, q, :], op=ALU.add)
-            inverse_root(c, whole[:])
-
-        def inverse_root(c, whole):
-            nc.gpsimd.tensor_tensor(out=d[:, c, :], in0=whole, in1=minus_half[:], op=ALU.pow)
+                nc.scalar.copy(out=row_sums[:], in_=totals[c][:, 0, :PACK])
+            inverse_root(c, row_sums[:])
 
         def spread_d(bank, b):
             for t in range(PACK):
@@ -326,367 +281,251 @@ def tile_gcnresnet_pa_t_kernel(tc, x_pre, A, W_gc2, out):
                     identity[:],
                 )
 
-        acc = {}
-        passes = {}
-        a_tiles = {}
-        sum_tiles = {}
-        a_row_tiles = {}
-        scaled_tiles = {}
-        grouped_tiles = {}
-        code_tiles = {}
 
-        def whole(c, q):
-            return ((c, 2 * q), (c, 2 * q + 1))
-
-        order = [whole(0, 0), whole(1, 0), whole(2, 0)]
-        if XU:
-            order += [((0, 2), (1, 2)), whole(3, 0), ((2, 2), (3, 2)), ((0, 3), (1, 3)), ((2, 3), (3, 3))]
-        else:
-            order += [whole(3, 0), whole(0, 1), whole(1, 1), whole(2, 1), whole(3, 1)]
-        order += [whole(c, q) for c, q in ((4, 1), (4, 0), (5, 0), (5, 1), (6, 1), (6, 0), (7, 0), (7, 1))]
-        order += [whole(c, q) for q in (2, 3) for c in range(N_BLOCKS)]
-
-        def is_whole(s):
-            return order[s][0][0] == order[s][1][0]
-
-        def in_round_0(s):
-            return order[s][0][1] < 2 * ROUND_QUARTERS
+        units = [(c, q) for q in range(ROUND_QUARTERS) for c in range(4)]
+        units += [(c, q) for c in range(4, N_BLOCKS) for q in ((1, 0) if c % 2 == 0 else (0, 1))]
+        round_1 = len(units)
+        units += [(c, q) for q in range(ROUND_QUARTERS, 2 * ROUND_QUARTERS) for c in range(N_BLOCKS)]
+        first_step = [min(s for s in range(len(units)) if units[s][0] == c) for c in range(N_BLOCKS)]
+        d_step = [max(first - 2, 0) for first in first_step]
+        sum_steps = [0] + [s - t for c in WHOLE_ROW_BLOCKS for s in (d_step[c],) for t in range(PACK)]
 
         def scalar_rows(s):
-            if s < len(S_FIRST):
-                return S_FIRST[s]
-            return SCALAR_SCALE_ROWS if busy_scalar[s] else S_FREE
+            if units[s][1] >= ROUND_QUARTERS:
+                return PACK - 1 if s % GPSIMD_ROW_EVERY == 0 else PACK
+            if s == 0:
+                return UNIT_0_SCALAR_ROWS
+            return BUSY_SCALAR_ROWS if s - 1 in sum_steps else FREE_SCALAR_ROWS
 
         def gpsimd_columns(s):
-            if not in_round_0(s):
-                return GPSIMD_COLUMNS
-            if s < len(S_FIRST) or not is_whole(s):
-                return 0
-            return GC0 if scalar_rows(s) == SCALAR_SCALE_ROWS else GC0B
+            if units[s][1] >= ROUND_QUARTERS:
+                return GPSIMD_COLUMNS_1
+            return GPSIMD_COLUMNS_0 if scalar_rows(s) == FREE_SCALAR_ROWS else 0
 
-        def a_rows(c, b):
-            q = b // 2
-            lo = (b % 2) * BLOCK
-            if c in ROW_TILES and q < ROUND_QUARTERS:
-                return [a_row_tiles[(c, t)][:, q * QUARTER + lo : (q + 1) * QUARTER] for t in range(PACK)]
-            return [a_tiles[(c, q)][:, t, lo:] for t in range(PACK)]
+        scaled = {}
+        grouped = {}
+        codes = {}
+        scales = {}
+        d_banks = []
+        acc = {}
+        passes = {}
 
         def scale(s):
-            scaled = scaled_pool.tile([P, PACK, QUARTER], F32, name="scaled")
-            if in_round_0(s):
-                gs = list(range(scalar_rows(s), PACK))
+            c, q = units[s]
+            scaled[s] = scaled_pool.tile([P, PACK, QUARTER], F32, name="scaled")
+            if c in WHOLE_ROW_BLOCKS and q < ROUND_QUARTERS:
+                rows = [a_tiles[(c, "row", t)][:, q * QUARTER : (q + 1) * QUARTER] for t in range(PACK)]
             else:
-                gs = [PACK - 1] if G1 and s % G1 == 0 else []
-            parts = [(order[s][0], 0, QUARTER)] if is_whole(s) else [(order[s][0], 0, BLOCK), (order[s][1], BLOCK, QUARTER)]
-            for t in gs + [t for t in range(PACK) if t not in gs]:
-                for (c, b), lo, hi in parts:
-                    row = a_rows(c, b)[t][:, : hi - lo]
-                    if t in gs:
-                        nc.gpsimd.tensor_scalar(
-                            out=scaled[:, t, lo:hi],
-                            in0=row,
-                            scalar1=d[:, c, t : t + 1],
-                            scalar2=0.0,
-                            op0=ALU.mult,
-                            op1=ALU.add,
-                        )
-                    else:
-                        nc.scalar.activation(
-                            out=scaled[:, t, lo:hi], in_=row, func=ACT.Copy, scale=d[:, c, t : t + 1]
-                        )
-            scaled_tiles[s] = scaled
-
-        d_banks = {}
-        recent = []
-        halves = {}
+                rows = [a_tiles[(c, q)][:, t, :] for t in range(PACK)]
+            for t in range(scalar_rows(s), PACK):
+                nc.gpsimd.tensor_scalar(
+                    out=scaled[s][:, t, :],
+                    in0=rows[t],
+                    scalar1=d[:, c, t : t + 1],
+                    scalar2=0.0,
+                    op0=ALU.mult,
+                    op1=ALU.add,
+                )
+            for t in range(scalar_rows(s)):
+                nc.scalar.activation(out=scaled[s][:, t, :], in_=rows[t], func=ACT.Copy, scale=d[:, c, t : t + 1])
 
         def spread(s):
-            bs = [order[s][k][1] for k in range(2)]
-            halves[s] = sorted(range(2), key=lambda k: bs[k] not in d_banks)
-            for k in halves[s]:
-                b = bs[k]
-                if b in recent:
-                    recent.remove(b)
-                else:
-                    if len(recent) == 2:
-                        del_b = recent.pop(0)
-                        d_banks.pop(del_b)
-                    d_banks[b] = spread_psum.tile([P, BLOCK], F32, name="d_bank", tag="spread")
-                    spread_d(d_banks[b], b)
-                    if b in d_gpsimd and b < 2 * ROUND_QUARTERS and b not in spread_quarters:
-                        spread_quarters.add(b)
-                        nc.scalar.copy(out=d_gpsimd[b][:], in_=d_banks[b][:, BLOCK - max(GC0, GC0B) :])
-                recent.append(b)
-            bank_tiles[s] = [d_banks[b] for b in bs]
+            q = units[s][1]
+            if s > 0 and units[s - 1][1] == q:
+                return
+            d_banks.clear()
+            for k in range(2):
+                bank = spread_psum.tile([P, BLOCK], F32, name="d_bank", tag="spread")
+                spread_d(bank, 2 * q + k)
+                d_banks.append(bank)
+            if q < ROUND_QUARTERS and q not in spread_quarters:
+                spread_quarters.append(q)
+                nc.scalar.copy(out=d_gpsimd[q][:], in_=d_banks[1][:, BLOCK - GPSIMD_COLUMNS_0 :])
 
-        bank_tiles = {}
+        spread_quarters = []
 
         def multiply(s):
-            scaled = scaled_tiles[s]
-            grouped = grouped_tiles[s]
+            grouped[s] = grouped_pool.tile([P, QUARTER, PACK], BF16, name="grouped", align_bytes=64)
             vector_columns = QUARTER - gpsimd_columns(s)
-            for k in halves[s]:
+            for i0 in range(vector_columns, QUARTER, P):
+                j0 = i0 - vector_columns
+                nc.gpsimd.tensor_tensor(
+                    out=grouped[s][:, i0 : i0 + P, :],
+                    in0=scaled[s][:, :, i0 : i0 + P].rearrange("p t i -> p i t"),
+                    in1=d_gpsimd[units[s][1]][:, j0 : j0 + P].unsqueeze(2).to_broadcast([P, P, PACK]),
+                    op=ALU.mult,
+                )
+            for k in range(2):
                 lo = k * BLOCK
                 columns = min(BLOCK, vector_columns - lo)
                 nc.vector.tensor_tensor(
-                    out=grouped[:, lo : lo + columns, :].rearrange("p (n i) t -> p n t i", i=RUN),
-                    in0=scaled[:, :, lo : lo + columns].rearrange("p t (n i) -> p n t i", i=RUN),
-                    in1=bank_tiles[s][k][:, :columns]
+                    out=grouped[s][:, lo : lo + columns, :].rearrange("p (n i) t -> p n t i", i=RUN),
+                    in0=scaled[s][:, :, lo : lo + columns].rearrange("p t (n i) -> p n t i", i=RUN),
+                    in1=d_banks[k][:, :columns]
                     .rearrange("p (n i) -> p n i", i=RUN)
                     .unsqueeze(2)
                     .to_broadcast([P, columns // RUN, PACK, RUN]),
                     op=ALU.mult,
                 )
 
-        def multiply_gpsimd(s):
-            b = order[s][1][1]
-            scaled = scaled_tiles[s]
-            grouped = grouped_tiles[s]
-            vector_columns = QUARTER - gpsimd_columns(s)
-            width = max(GC0, GC0B) if in_round_0(s) else GPSIMD_COLUMNS
-            for i0 in range(vector_columns, QUARTER, P):
-                n = min(P, QUARTER - i0)
-                j0 = i0 - (QUARTER - width)
-                nc.gpsimd.tensor_tensor(
-                    out=grouped[:, i0 : i0 + n, :],
-                    in0=scaled[:, :, i0 : i0 + n].rearrange("p t i -> p i t"),
-                    in1=d_gpsimd[b][:, j0 : j0 + n].unsqueeze(2).to_broadcast([P, n, PACK]),
-                    op=ALU.mult,
-                )
-
-        def quantise(s):
-            codes = codes_pool.tile([P, QUARTER], U32, name="codes", align_bytes=64)
-            scales = codes_pool.tile([P, QUARTER], U8, name="scales", align_bytes=64)
+        def quantise(s, columns):
+            if s not in codes:
+                codes[s] = codes_pool.tile([P, QUARTER], U32, name="codes", align_bytes=64)
+                scales[s] = codes_pool.tile([P, QUARTER], U8, name="scales", align_bytes=64)
             nc.vector.quantize_mx(
-                out=codes[:].bitcast(FP8X4), scales=scales[:], in_=grouped_tiles[s][:].rearrange("p i t -> p (i t)")
+                out=codes[s][:, columns].bitcast(FP8X4),
+                scales=scales[s][:, columns],
+                in_=grouped[s][:, columns, :].rearrange("p i t -> p (i t)"),
             )
-            code_tiles[s] = (codes, scales)
 
-        def accumulate(s, ks=(0, 1)):
-            codes, scales = code_tiles[s]
-            for k in ks:
-                c, b = order[s][k]
-                if b not in acc:
-                    acc[b] = acc_psum.tile([P, BLOCK], F32, name="acc", tag="acc")
-                    passes[b] = 0
-                nc.tensor.matmul_mx(
-                    out=acc[b][:],
-                    lhsT=support_codes[:, c, :].bitcast(FP8X4),
-                    lhsT_scale=support_scales[:, c, :],
-                    rhs=codes[:, k * BLOCK : (k + 1) * BLOCK].bitcast(FP8X4),
-                    rhs_scale=scales[:, k * BLOCK : (k + 1) * BLOCK],
-                    start=(passes[b] == 0),
-                    stop=(passes[b] == N_BLOCKS - 1),
-                )
-                passes[b] += 1
+        def accumulate(s, k):
+            c, q = units[s]
+            b = 2 * q + k
+            if b not in acc:
+                acc[b] = acc_psum.tile([P, BLOCK], F32, name="acc", tag="acc")
+                passes[b] = 0
+            nc.tensor.matmul_mx(
+                out=acc[b][:],
+                lhsT=support_codes[:, c, :].bitcast(FP8X4),
+                lhsT_scale=support_scales[:, c, :],
+                rhs=codes[s][:, k * BLOCK : (k + 1) * BLOCK].bitcast(FP8X4),
+                rhs_scale=scales[s][:, k * BLOCK : (k + 1) * BLOCK],
+                start=(passes[b] == 0),
+                stop=(passes[b] == N_BLOCKS - 1),
+            )
+            passes[b] += 1
 
-        out_tiles = {}
+        rows_psum = {}
 
-        def empty_bank(b, copy, tag):
+        def turn_back(b, copies):
             out_t = out_pool.tile([P, BLOCK], F32, name="out_t")
-            copy(out=out_t[:], in_=acc[b][:])
-            rows_psum = misc_psum.tile([P, BLOCK // P, FEAT_OUT], F32, name="rows_psum", tag=tag)
-            for u in range(BLOCK // P):
-                nc.tensor.transpose(rows_psum[:, u, :], out_t[:, P * u : P * (u + 1)], identity[:])
-            out_tiles[b] = rows_psum
+            rows_psum[b] = side_psum.tile(
+                [P, BLOCK // P, FEAT_OUT], F32, name="rows_psum", tag="even" if b % 2 == 0 else "odd"
+            )
+            share = BLOCK // len(copies)
+            for k in range(len(copies)):
+                copies[k](out=out_t[:, k * share : (k + 1) * share], in_=acc[b][:, k * share : (k + 1) * share])
+                for i0 in range(k * share, (k + 1) * share, P):
+                    nc.tensor.transpose(rows_psum[b][:, i0 // P, :], out_t[:, i0 : i0 + P], identity[:])
 
-        def store_rows(b, copy, queue):
+        def store(b, copies, queue):
             rows = out_pool.tile([P, BLOCK // P, FEAT_OUT], F32, name="rows")
-            copy(out=rows[:], in_=out_tiles[b][:])
+            share = BLOCK // P // len(copies)
+            for k in range(len(copies)):
+                us = slice(k * share, (k + 1) * share)
+                copies[k](out=rows[:, us, :], in_=rows_psum[b][:, us, :])
             queue.dma_start(out=out_view[b], in_=rows[:])
 
-        def load(*keys):
-            for c, q in keys:
-                a_tiles[(c, q)] = load_quarter(c, q)
 
-        def load_block(c):
-            if c not in ROW_TILES:
-                load(*[(c, q) for q in load_order])
-                return
-            for t in range(PACK):
-                a_row_tiles[(c, t)] = a_pool.tile([P, NODES], BF16, name="a_row", tag="a")
-                nc.sync.dma_start(out=a_row_tiles[(c, t)][:], in_=a_view[c][:, t, :])
-
-        def sum_row(c, t):
-            row = a_row_tiles[(c, t)][:]
-            nc.scalar.activation(out=row, in_=row, func=ACT.Copy, accum_out=sums_scalar[:, c, 0, t : t + 1])
-
-        x_tiles = []
         for m in range(N_BLOCKS // 2):
-            x_pair = a_pool.tile([P, 2, PACK, FEAT_IN], BF16, name="x_pair", tag="a")
-            nc.sync.dma_start(out=x_pair[:], in_=x_view[m])
-            x_tiles.append(x_pair)
+            load_x_pair(m)
             if m == 0:
                 quantise_w()
-        load_block(0)
-        if HALF1:
-            load((1, 0))
-            sum_tiles[1] = load_half_sum_tiles(1)
-            load((1, 1))
-        else:
-            sum_tiles[1] = load_sum_tiles(1)
-            load((1, 0))
-        if 2 in TENSOR_SUM_ROW_BLOCKS:
-            sum_tiles[2] = load_sum_tiles(2)
-            load((2, 0))
-        else:
-            load_block(2)
+        for q in LOAD_ORDER:
+            load_quarter(0, q)
+        load_second_copy(1)
+        load_quarter(1, 0)
+        for q in LOAD_ORDER:
+            load_quarter(2, q)
+        load_second_copy(3)
+        load_quarter(3, 0)
 
-        def sums(c, *qs):
-            for q in qs:
-                sum_rows(c, q, a_tiles[(c, q)])
-
-        def d_scalar(c):
-            inverse_root(c, sums_scalar[:, c, 0, :] if c in ROW_TILES else add_quarter_sums(c)[:])
-
-        def load_sum(c):
-            sum_tiles[c] = load_sum_tiles(c)
-
-        busy_scalar = [False] * (len(order) + 1)
-        first_use = {c: min(s for s in range(len(order)) if c in (order[s][0][0], order[s][1][0])) for c in range(N_BLOCKS)}
-        jobs = {}
-        loads = {}
-
-        pre_jobs = {}
-
-        def add(table, s, f, least=0):
-            table.setdefault(max(s, least), []).append(f)
-
-        queue = []
-        for c in range(2, N_BLOCKS):
-            end = max(first_use[c] - (END_T if c in TENSOR_SUM_ROW_BLOCKS else END_S), 0)
-            if c in TENSOR_SUM_ROW_BLOCKS:
-                for n in range(4):
-                    add(jobs, end - 1 - (3 - n) // FOLD_PER, lambda c=c, n=n: fold_sum_tile(c, n), -1)
-                add(jobs if c in QUICK else pre_jobs, end, lambda c=c: total_folded(c))
-                add(jobs, end, lambda c=c: d_tensor(c))
-                if c > 2:
-                    queue.append((end - 1 - 3 // FOLD_PER - AHEAD_S, lambda c=c: load_sum(c)))
-            else:
-                for n, q in enumerate(load_order):
-                    s = max(end - 3 + n, 0)
-                    if c in ROW_TILES:
-                        add(jobs, s, lambda c=c, n=n: sum_row(c, n))
-                    else:
-                        add(jobs, s, lambda c=c, q=q: sums(c, q))
-                    if not vector_sums(c, q):
-                        busy_scalar[s + 1] = True
-                add(jobs, end, lambda c=c: d_scalar(c))
-                if c > 2:
-                    queue.append((end - 3 - AHEAD, lambda c=c: load_block(c)))
-        queued = {(1, 0), (2, 0)} | ({(1, 1)} if HALF1 else set()) | {(c, q) for c in range(N_BLOCKS) if c not in TENSOR_SUM_ROW_BLOCKS for q in range(ROUND_QUARTERS)}
-        for s in range(len(order)):
-            for c, b in order[s]:
-                if (c, b // 2) not in queued:
-                    queued.add((c, b // 2))
-                    queue.append((s - AHEAD_U, lambda k=(c, b // 2): load(k)))
-        for s, f in sorted(queue, key=lambda e: e[0]):
-            add(loads, s, f, -1)
+        turn_x(0)
         for c in range(N_BLOCKS + 1):
-            if c == 0:
-                turn_x(0, x_tiles[0][:, 0])
             if c + 1 < N_BLOCKS:
-                turn_x(c + 1, x_tiles[(c + 1) // 2][:, (c + 1) % 2])
+                turn_x(c + 1)
             if c < N_BLOCKS:
                 slope_times_x(c)
-            if c > 0:
-                quantise_h(c - 1)
+            if c >= 1:
+                multiply_h(c - 1)
             if c < N_BLOCKS:
                 leaky_relu(c)
-            if c >= LAG:
-                quantise_support(c - LAG)
-            for n in range(2 * PACK):
-                if V_ROWS_AT[n // 2] == c:
-                    q, t = (2, 3)[n // PACK], n % PACK
-                    sum_rows(0, q, a_tiles[(0, q)], (t,))
-            if S0 <= c < S0 + 4:
-                q = (0, 1)[(c - S0) // 2]
-                sum_rows(0, q, a_tiles[(0, q)], range(2 * ((c - S0) % 2), 2 * ((c - S0) % 2) + 2))
-            for n in range(2 if HALF1 else 4):
-                if FOLD_C[n] == c:
-                    fold_sum_tile(1, n)
-            if HALF1:
-                for n in range(2 * PACK):
-                    if V1_AT[n // 4] == c:
-                        sum_rows(1, n // PACK, a_tiles[(1, n // PACK)], (n % PACK,))
-        if TOT_FIRST:
-            total_folded(1)
-        for c in range(N_BLOCKS + 1 - LAG, N_BLOCKS):
-            quantise_support(c)
-        inverse_root(0, add_quarter_sums(0)[:])
-        if not TOT_FIRST:
-            total_folded(1)
-        if D1_FIRST:
-            d_tensor(1)
+            if c >= 2:
+                quantise_support(c - 2)
+            if N_BLOCKS - 4 <= c < N_BLOCKS:
+                pair = c - (N_BLOCKS - 4)
+                rows = (0, 1) if pair % 2 == 0 else (2, 3)
+                sum_quarter_rows(0, 2 + pair // 2, rows)
+                sum_quarter_rows(0, pair // 2, rows)
+            if c == N_BLOCKS - 1:
+                for n in range(SUM_TILES):
+                    fold(1, n)
+        total(1)
+        quantise_support(N_BLOCKS - 1)
+        d_of_quarter_sums(0)
+        d_of_total(1)
         scale(0)
-        if not D1_FIRST:
-            d_tensor(1)
-        steps = len(order)
-        for f in loads.get(-1, []) + jobs.get(-1, []):
-            f()
-        for s in range(steps + MXLAG + 3):
-            for f in loads.get(s, ()):
-                f()
-            if s < steps:
-                spread(s)
-            for f in pre_jobs.get(s, ()):
-                f()
-            if s < steps:
-                grouped = grouped_pool.tile([P, QUARTER, PACK], BF16, name="grouped", align_bytes=64)
-                grouped_tiles[s] = grouped
-            if GFIRST and s < steps:
-                multiply_gpsimd(s)
-            if s + 1 < steps:
+
+
+        moves = {}
+        for first, b0 in ((round_1, 0), (round_1 + 4, 2), (round_1 + N_BLOCKS + 1, 4)):
+            moves[first] = (turn_back, b0)
+            moves[first + 1] = (turn_back, b0 + 1)
+            moves[first + 2] = (store, b0)
+            moves[first + 3] = (store, b0 + 1)
+
+        all_columns = slice(0, QUARTER)
+        for s in range(len(units)):
+            for c in range(4, N_BLOCKS):
+                if c in WHOLE_ROW_BLOCKS and s == d_step[c] - PACK:
+                    load_whole_rows(c)
+                if c in TENSOR_SUM_ROW_BLOCKS and s == d_step[c] - 3:
+                    load_second_copy(c)
+            if s + LOAD_AHEAD < len(units):
+                c, q = units[s + LOAD_AHEAD]
+                if c in TENSOR_SUM_ROW_BLOCKS or q >= ROUND_QUARTERS:
+                    load_quarter(c, q)
+
+            spread(s)
+            for c in TENSOR_SUM_ROW_BLOCKS:
+                if c > 3 and s == d_step[c]:
+                    total(c)
+            if s + 1 < len(units):
                 scale(s + 1)
-            if not GFIRST and s < steps:
-                multiply_gpsimd(s)
-            if s < steps:
-                multiply(s)
-            if 1 <= s < steps or (s == steps and not SPLIT_LAST):
-                quantise(s - 1)
-            if MXLAG <= s < steps + MXLAG - (1 if SPLIT_LAST else 0):
-                accumulate(s - MXLAG)
-            if SPLIT_LAST and s == steps:
-                codes = codes_pool.tile([P, QUARTER], U32, name="codes", align_bytes=64)
-                scales = codes_pool.tile([P, QUARTER], U8, name="scales", align_bytes=64)
-                code_tiles[s - 1] = (codes, scales)
+            multiply(s)
+            if s >= 1:
+                quantise(s - 1, all_columns)
+            if s >= 2:
                 for k in range(2):
-                    half = slice(k * BLOCK, (k + 1) * BLOCK)
-                    nc.vector.quantize_mx(
-                        out=codes[:, half].bitcast(FP8X4),
-                        scales=scales[:, half],
-                        in_=grouped_tiles[s - 1][:, half, :].rearrange("p i t -> p (i t)"),
-                    )
-                    accumulate(s - 1, (k,))
-            for f in jobs.get(s, ()):
-                f()
-            if s in (13, 14):
-                j = s - 13
-                d_turned = misc_psum.tile([P, BLOCK], F32, name="d_turned", tag="rows")
-                spread_d(d_turned, 2 * (j + ROUND_QUARTERS) + 1)
-                nc.scalar.copy(out=d_gpsimd[2 * (j + ROUND_QUARTERS) + 1][:], in_=d_turned[:, BLOCK - GPSIMD_COLUMNS :])
-            for s0, kind, b in STORES:
-                if s == s0 and kind == "e":
-                    empty_bank(b, nc.scalar.copy, ("rows", "product")[b % 2])
-                elif s == s0:
-                    store_rows(b, nc.scalar.copy, nc.scalar)
-        if not SPLIT_LAST:
-            empty_bank(N_BLOCKS - 2, nc.scalar.copy, "rows")
-            empty_bank(N_BLOCKS - 1, nc.vector.tensor_copy, "product")
-            store_rows(N_BLOCKS - 2, nc.scalar.copy, nc.sync)
-            store_rows(N_BLOCKS - 1, nc.vector.tensor_copy, nc.sync)
-        else:
-            empty_bank(N_BLOCKS - 2, nc.scalar.copy, "rows")
-            b = N_BLOCKS - 1
-            out_t = out_pool.tile([P, BLOCK], F32, name="out_t")
-            rows_psum = misc_psum.tile([P, BLOCK // P, FEAT_OUT], F32, name="rows_psum", tag="product")
-            rows = out_pool.tile([P, BLOCK // P, FEAT_OUT], F32, name="rows")
-            engines = (nc.vector.tensor_copy, nc.scalar.copy)
-            for k in range(2):
-                engines[k](out=out_t[:, k * 256 : (k + 1) * 256], in_=acc[b][:, k * 256 : (k + 1) * 256])
-                for u in (2 * k, 2 * k + 1):
-                    nc.tensor.transpose(rows_psum[:, u, :], out_t[:, P * u : P * (u + 1)], identity[:])
-            store_rows(N_BLOCKS - 2, nc.scalar.copy, nc.sync)
-            for k in range(2):
-                engines[k](out=rows[:, 2 * k : 2 * k + 2, :], in_=rows_psum[:, 2 * k : 2 * k + 2, :])
-            nc.sync.dma_start(out=out_view[b], in_=rows[:])
+                    accumulate(s - 2, k)
+
+            for c in range(2, N_BLOCKS):
+                if c in TENSOR_SUM_ROW_BLOCKS:
+                    if s == d_step[c] - 1:
+                        for n in range(SUM_TILES):
+                            fold(c, n)
+                    if s == d_step[c]:
+                        if c == 3:
+                            total(c)
+                        d_of_total(c)
+                elif c in WHOLE_ROW_BLOCKS:
+                    if d_step[c] - PACK < s <= d_step[c]:
+                        sum_whole_row(c, s - (d_step[c] - PACK + 1))
+                    if s == d_step[c]:
+                        inverse_root(c, sums_scalar[:, c, 0, :])
+                elif s == d_step[c]:
+                    for q in LOAD_ORDER:
+                        sum_quarter_rows(c, q, range(PACK))
+                    d_of_quarter_sums(c)
+            q = s - d_step[N_BLOCKS - 1] - 1 + ROUND_QUARTERS
+            if ROUND_QUARTERS <= q < 2 * ROUND_QUARTERS:
+                d_turned = side_psum.tile([P, BLOCK], F32, name="d_turned", tag="even")
+                spread_d(d_turned, 2 * q + 1)
+                nc.scalar.copy(out=d_gpsimd[q][:], in_=d_turned[:, BLOCK - GPSIMD_COLUMNS_1 :])
+            if s in moves:
+                move, b = moves[s]
+                if move == turn_back:
+                    turn_back(b, (nc.scalar.copy,))
+                else:
+                    store(b, (nc.scalar.copy,), nc.scalar)
+
+        last = len(units) - 1
+        for k in range(2):
+            accumulate(last - 1, k)
+        for k in range(2):
+            quantise(last, slice(k * BLOCK, (k + 1) * BLOCK))
+            accumulate(last, k)
+        turn_back(N_BLOCKS - 2, (nc.scalar.copy,))
+        turn_back(N_BLOCKS - 1, (nc.vector.tensor_copy, nc.scalar.copy))
+        store(N_BLOCKS - 2, (nc.scalar.copy,), nc.sync)
+        store(N_BLOCKS - 1, (nc.vector.tensor_copy, nc.scalar.copy), nc.sync)

from contextlib import ExitStack

import concourse.mybir as mybir
from concourse.masks import make_identity

F32 = mybir.dt.float32
BF16 = mybir.dt.bfloat16
U32 = mybir.dt.uint32
U8 = mybir.dt.uint8
FP8X4 = mybir.dt.float8_e4m3fn_x4
ALU = mybir.AluOpType
ACT = mybir.ActivationFunctionType

P = 128
PACK = 4
NODES = 4096
FEAT_IN = 512
FEAT_OUT = 128
SLOPE = 0.2
BLOCK = P * PACK
N_BLOCKS = NODES // BLOCK
QUARTER = 2 * BLOCK
ROUND_QUARTERS = 2
RUN = 4
FLOPS = 2 * NODES * FEAT_IN * FEAT_OUT + 2 * NODES * NODES * FEAT_OUT

TENSOR_SUM_ROW_BLOCKS = (1, 3, 5, 7)
PIECE = {1: 1024, 3: 1024, 5: 1024, 7: 512}
SUM_TILE_ROWS = P
SUM_TILES = 4
QUICK_SUM_ROW_BLOCKS = (1, 3)
WHOLE_ROW_BLOCKS = (4, 6)
LOAD_ORDER = (0, 2, 1, 3)
A_TILES = 10
LOAD_AHEAD = 5
UNIT_0_SCALAR_ROWS = 2
BUSY_SCALAR_ROWS = 1
FREE_SCALAR_ROWS = 3
GPSIMD_COLUMNS_0 = P
GPSIMD_COLUMNS_1 = 2 * P
GPSIMD_ROW_EVERY = 4


def tile_gcnresnet_pa_t_kernel(tc, x_pre, A, W_gc2, out):
    nc = tc.nc
    a_view = A.rearrange("(c p t) i -> c p t i", p=P, t=PACK)
    x_view = x_pre.rearrange("(m h p t) k -> m p h t k", h=2, p=P, t=PACK)
    out_view = out.rearrange("(b u p) f -> b p u f", u=BLOCK // P, p=P)
    sum_views = {
        w: A.rearrange("n i -> (n i)").rearrange("(n r q w) -> n q r w", r=NODES // w, q=P, w=w)
        for w in (1024, 512)
    }

    with ExitStack() as ctx:
        keep = ctx.enter_context(tc.tile_pool(name="keep", bufs=1))
        a_pool = ctx.enter_context(tc.tile_pool(name="a_pool", bufs=A_TILES))
        sum_pool = ctx.enter_context(tc.tile_pool(name="sum_pool", bufs=SUM_TILES))
        scaled_pool = ctx.enter_context(tc.tile_pool(name="scaled_pool", bufs=2))
        grouped_pool = ctx.enter_context(tc.tile_pool(name="grouped_pool", bufs=3))
        codes_pool = ctx.enter_context(tc.tile_pool(name="codes_pool", bufs=3))
        first_pool = ctx.enter_context(tc.tile_pool(name="first_pool", bufs=2))
        sums_pool = ctx.enter_context(tc.tile_pool(name="sums_pool", bufs=2))
        out_pool = ctx.enter_context(tc.tile_pool(name="out_pool", bufs=2))
        spread_psum = ctx.enter_context(tc.psum_pool(name="spread_psum", bufs=2))
        acc_psum = ctx.enter_context(tc.psum_pool(name="acc_psum", bufs=ROUND_QUARTERS * 2))
        side_psum = ctx.enter_context(tc.psum_pool(name="side_psum", bufs=1))
        ctx.enter_context(tc.manual_schedule())

        identity = keep.tile([P, P], F32, name="identity")
        make_identity(nc, identity[:])
        picks = {}
        for w in (1024, 512):
            pick_f32 = keep.tile([P, P * w // NODES], F32, name="pick_f32_%d" % w)
            nc.vector.reduce_sum(
                out=pick_f32[:],
                in_=identity[:].rearrange("q (g e) -> q g e", e=NODES // w),
                axis=mybir.AxisListType.X,
            )
            picks[w] = keep.tile([P, P * w // NODES], BF16, name="pick_%d" % w)
            nc.vector.tensor_copy(out=picks[w][:], in_=pick_f32[:])
        one = keep.tile([P, 1], F32, name="one")
        nc.gpsimd.memset(one[:], 1.0)
        minus_half = keep.tile([P, PACK], F32, name="minus_half")
        nc.gpsimd.memset(minus_half[:], -0.5)
        sums_scalar = keep.tile([P, N_BLOCKS, 4, PACK], F32, name="sums_scalar")
        sums_vector = keep.tile([P, N_BLOCKS, 4, PACK], F32, name="sums_vector")
        d = keep.tile([P, N_BLOCKS, PACK], F32, name="d")
        d_gpsimd = []
        for q in range(2 * ROUND_QUARTERS):
            width = GPSIMD_COLUMNS_0 if q < ROUND_QUARTERS else GPSIMD_COLUMNS_1
            d_columns = keep.tile([P, width], F32, name="d_gpsimd_%d" % q)
            d_gpsimd.append(d_columns)
        support_codes = keep.tile([P, N_BLOCKS, FEAT_OUT], U32, name="support_codes", align_bytes=64)
        support_scales = keep.tile([P, N_BLOCKS, FEAT_OUT], U8, name="support_scales", align_bytes=64)
        w_codes = keep.tile([P, FEAT_OUT], U32, name="w_codes", align_bytes=64)
        w_scales = keep.tile([P, FEAT_OUT], U8, name="w_scales", align_bytes=64)


        x_pairs = []
        a_tiles = {}
        sum_tiles = {}

        def load_x_pair(m):
            x_pair = a_pool.tile([P, 2, PACK, FEAT_IN], BF16, name="x_pair", tag="a")
            nc.sync.dma_start(out=x_pair[:], in_=x_view[m])
            x_pairs.append(x_pair)

        def load_quarter(c, q):
            tile = a_pool.tile([P, PACK, QUARTER], BF16, name="a_quarter", tag="a")
            nc.sync.dma_start(out=tile[:], in_=a_view[c][:, :, q * QUARTER : (q + 1) * QUARTER])
            a_tiles[(c, q)] = tile

        def load_whole_rows(c):
            for t in range(PACK):
                tile = a_pool.tile([P, NODES], BF16, name="a_row", tag="a")
                nc.sync.dma_start(out=tile[:], in_=a_view[c][:, t, :])
                a_tiles[(c, "row", t)] = tile

        def load_second_copy(c):
            w = PIECE[c]
            sum_tiles[c] = []
            for n in range(SUM_TILES):
                tile = sum_pool.tile([P, NODES // w, w], BF16, name="a_sum", tag="a_sum")
                nc.sync.dma_start(out=tile[:], in_=sum_views[w][c * SUM_TILES + n])
                sum_tiles[c].append(tile)


        x_grouped = {}
        h_grouped = {}
        products = {}

        def quantise_w():
            w_rows = keep.tile([P, PACK, FEAT_OUT], BF16, name="w_rows")
            for u in range(2):
                nc.sync.dma_start(
                    out=w_rows[:, 2 * u : 2 * u + 2, :],
                    in_=W_gc2[256 * u : 256 * u + 256, :].rearrange("(q e) f -> q e f", e=2),
                )
            w_grouped = keep.tile([P, FEAT_OUT, PACK], BF16, name="w_grouped", align_bytes=64)
            nc.vector.tensor_copy(out=w_grouped[:], in_=w_rows[:].rearrange("q s f -> q f s"))
            nc.vector.quantize_mx(
                out=w_codes[:].bitcast(FP8X4),
                scales=w_scales[:],
                in_=w_grouped[:].rearrange("q f s -> q (f s)"),
            )

        def turn_x(c):
            x_words = x_pairs[c // 2][:, c % 2].bitcast(F32)
            grouped = first_pool.tile([P, BLOCK, PACK], BF16, name="x_grouped", align_bytes=64)
            grouped_words = grouped[:].bitcast(F32)
            for half in range(2):
                turned = spread_psum.tile([P, 2, 2, P], F32, name="turned", tag="spread")
                for t in range(2):
                    for u in range(2):
                        nc.tensor.transpose(
                            turned[:, t, u, :], x_words[:, 2 * half + t, P * u : P * u + P], identity[:]
                        )
                nc.scalar.copy(
                    out=grouped_words[:, 2 * P * half : 2 * P * (half + 1), :].rearrange("q (t p) u -> q t p u", t=2),
                    in_=turned[:].rearrange("q t u p -> q t p u"),
                )
            x_grouped[c] = grouped[:].rearrange("q n s -> q (n s)")

        def slope_times_x(c):
            h_grouped[c] = first_pool.tile([P, BLOCK * PACK], BF16, name="h_grouped", align_bytes=64)
            nc.vector.tensor_scalar(
                out=h_grouped[c][:], in0=x_grouped[c], scalar1=SLOPE, scalar2=None, op0=ALU.mult
            )

        def leaky_relu(c):
            nc.vector.tensor_tensor(out=h_grouped[c][:], in0=x_grouped[c], in1=h_grouped[c][:], op=ALU.max)

        def multiply_h(c):
            h_codes = first_pool.tile([P, BLOCK], U32, name="h_codes", align_bytes=64)
            h_scales = first_pool.tile([P, BLOCK], U8, name="h_scales", align_bytes=64)
            nc.vector.quantize_mx(out=h_codes[:].bitcast(FP8X4), scales=h_scales[:], in_=h_grouped[c][:])
            products[c] = acc_psum.tile([P, PACK, FEAT_OUT], F32, name="product", tag="acc")
            for t in range(PACK):
                nc.tensor.matmul_mx(
                    out=products[c][:, t, :],
                    lhsT=h_codes[:, P * t : P * (t + 1)].bitcast(FP8X4),
                    lhsT_scale=h_scales[:, P * t : P * (t + 1)],
                    rhs=w_codes[:].bitcast(FP8X4),
                    rhs_scale=w_scales[:],
                    start=True,
                    stop=True,
                )

        def quantise_support(c):
            s_grouped = first_pool.tile([P, FEAT_OUT, PACK], BF16, name="s_grouped", align_bytes=64)
            nc.scalar.copy(out=s_grouped[:], in_=products[c][:].rearrange("p t f -> p f t"))
            nc.vector.quantize_mx(
                out=support_codes[:, c, :].bitcast(FP8X4),
                scales=support_scales[:, c, :],
                in_=s_grouped[:].rearrange("p f t -> p (f t)"),
            )


        def sum_on_scalar(row, total):
            nc.scalar.activation(out=row, in_=row, func=ACT.Copy, accum_out=total)

        def sum_on_vector(row, total):
            nc.vector.tensor_scalar(
                out=row, in0=row, scalar1=1.0, scalar2=None, op0=ALU.mult, op1=ALU.add, accum_out=total
            )

        def sum_quarter_rows(c, q, rows):
            for t in rows:
                if q < ROUND_QUARTERS:
                    sum_on_scalar(a_tiles[(c, q)][:, t, :], sums_scalar[:, c, q, t : t + 1])
                else:
                    sum_on_vector(a_tiles[(c, q)][:, t, :], sums_vector[:, c, q, t : t + 1])

        def sum_whole_row(c, t):
            sum_on_scalar(a_tiles[(c, "row", t)][:], sums_scalar[:, c, 0, t : t + 1])

        def inverse_root(c, row_sums):
            nc.gpsimd.tensor_tensor(out=d[:, c, :], in0=row_sums, in1=minus_half[:], op=ALU.pow)

        def d_of_quarter_sums(c):
            left = sums_pool.tile([P, PACK], F32, name="left")
            nc.gpsimd.tensor_tensor(
                out=left[:], in0=sums_scalar[:, c, 0, :], in1=sums_scalar[:, c, 1, :], op=ALU.add
            )
            right = sums_pool.tile([P, PACK], F32, name="right")
            nc.gpsimd.tensor_tensor(
                out=right[:], in0=sums_vector[:, c, 2, :], in1=sums_vector[:, c, 3, :], op=ALU.add
            )
            row_sums = sums_pool.tile([P, PACK], F32, name="row_sums")
            nc.gpsimd.tensor_tensor(out=row_sums[:], in0=left[:], in1=right[:], op=ALU.add)
            inverse_root(c, row_sums[:])

        folded = {}
        totals = {}

        def fold(c, n):
            if n == 0:
                folded[c] = side_psum.tile([P, BLOCK], F32, name="folded", tag="even")
            w = PIECE[c]
            abreast = P * w // NODES
            for r in range(NODES // w):
                j0 = n * SUM_TILE_ROWS + r * abreast
                for m in range(w // P):
                    nc.tensor.matmul(
                        folded[c][:, j0 : j0 + abreast],
                        lhsT=sum_tiles[c][n][:, r, m * P : (m + 1) * P],
                        rhs=picks[w][:],
                        start=(m == 0),
                        stop=(m == w // P - 1),
                    )

        def total(c):
            by_row = sums_pool.tile([P, PACK, P], F32, name="by_row")
            nc.scalar.copy(out=by_row[:], in_=folded[c][:].rearrange("m (p t) -> m t p", t=PACK))
            totals[c] = side_psum.tile([P, PACK, P], F32, name="totals", tag="odd")
            for t in range(PACK):
                if c in QUICK_SUM_ROW_BLOCKS:
                    nc.tensor.transpose(totals[c][:, t, :], by_row[:, t, :], identity[:])
                else:
                    nc.tensor.matmul(
                        totals[c][:, 0, t : t + 1], lhsT=by_row[:, t, :], rhs=one[:], start=True, stop=True
                    )

        def d_of_total(c):
            row_sums = sums_pool.tile([P, PACK], F32, name="row_sums")
            if c in QUICK_SUM_ROW_BLOCKS:
                for t in range(PACK):
                    unused = sums_pool.tile([P, P], BF16, name="unused")
                    nc.scalar.activation(
                        out=unused[:], in_=totals[c][:, t, :], func=ACT.Copy, accum_out=row_sums[:, t : t + 1]
                    )
            else:
                nc.scalar.copy(out=row_sums[:], in_=totals[c][:, 0, :PACK])
            inverse_root(c, row_sums[:])

        def spread_d(bank, b):
            for t in range(PACK):
                nc.tensor.transpose(
                    bank[:].rearrange("m (q t) -> m t q", t=PACK)[:, t, :],
                    d[:, b, t : t + 1].to_broadcast([P, P]),
                    identity[:],
                )


        units = [(c, q) for q in range(ROUND_QUARTERS) for c in range(4)]
        units += [(c, q) for c in range(4, N_BLOCKS) for q in ((1, 0) if c % 2 == 0 else (0, 1))]
        round_1 = len(units)
        units += [(c, q) for q in range(ROUND_QUARTERS, 2 * ROUND_QUARTERS) for c in range(N_BLOCKS)]
        first_step = [min(s for s in range(len(units)) if units[s][0] == c) for c in range(N_BLOCKS)]
        d_step = [max(first - 2, 0) for first in first_step]
        sum_steps = [0] + [s - t for c in WHOLE_ROW_BLOCKS for s in (d_step[c],) for t in range(PACK)]

        def scalar_rows(s):
            if units[s][1] >= ROUND_QUARTERS:
                return PACK - 1 if s % GPSIMD_ROW_EVERY == 0 else PACK
            if s == 0:
                return UNIT_0_SCALAR_ROWS
            return BUSY_SCALAR_ROWS if s - 1 in sum_steps else FREE_SCALAR_ROWS

        def gpsimd_columns(s):
            if units[s][1] >= ROUND_QUARTERS:
                return GPSIMD_COLUMNS_1
            return GPSIMD_COLUMNS_0 if scalar_rows(s) == FREE_SCALAR_ROWS else 0

        scaled = {}
        grouped = {}
        codes = {}
        scales = {}
        d_banks = []
        acc = {}
        passes = {}

        def scale(s):
            c, q = units[s]
            scaled[s] = scaled_pool.tile([P, PACK, QUARTER], F32, name="scaled")
            if c in WHOLE_ROW_BLOCKS and q < ROUND_QUARTERS:
                rows = [a_tiles[(c, "row", t)][:, q * QUARTER : (q + 1) * QUARTER] for t in range(PACK)]
            else:
                rows = [a_tiles[(c, q)][:, t, :] for t in range(PACK)]
            for t in range(scalar_rows(s), PACK):
                nc.gpsimd.tensor_scalar(
                    out=scaled[s][:, t, :],
                    in0=rows[t],
                    scalar1=d[:, c, t : t + 1],
                    scalar2=0.0,
                    op0=ALU.mult,
                    op1=ALU.add,
                )
            for t in range(scalar_rows(s)):
                nc.scalar.activation(out=scaled[s][:, t, :], in_=rows[t], func=ACT.Copy, scale=d[:, c, t : t + 1])

        def spread(s):
            q = units[s][1]
            if s > 0 and units[s - 1][1] == q:
                return
            d_banks.clear()
            for k in range(2):
                bank = spread_psum.tile([P, BLOCK], F32, name="d_bank", tag="spread")
                spread_d(bank, 2 * q + k)
                d_banks.append(bank)
            if q < ROUND_QUARTERS and q not in spread_quarters:
                spread_quarters.append(q)
                nc.scalar.copy(out=d_gpsimd[q][:], in_=d_banks[1][:, BLOCK - GPSIMD_COLUMNS_0 :])

        spread_quarters = []

        def multiply(s):
            grouped[s] = grouped_pool.tile([P, QUARTER, PACK], BF16, name="grouped", align_bytes=64)
            vector_columns = QUARTER - gpsimd_columns(s)
            for i0 in range(vector_columns, QUARTER, P):
                j0 = i0 - vector_columns
                nc.gpsimd.tensor_tensor(
                    out=grouped[s][:, i0 : i0 + P, :],
                    in0=scaled[s][:, :, i0 : i0 + P].rearrange("p t i -> p i t"),
                    in1=d_gpsimd[units[s][1]][:, j0 : j0 + P].unsqueeze(2).to_broadcast([P, P, PACK]),
                    op=ALU.mult,
                )
            for k in range(2):
                lo = k * BLOCK
                columns = min(BLOCK, vector_columns - lo)
                nc.vector.tensor_tensor(
                    out=grouped[s][:, lo : lo + columns, :].rearrange("p (n i) t -> p n t i", i=RUN),
                    in0=scaled[s][:, :, lo : lo + columns].rearrange("p t (n i) -> p n t i", i=RUN),
                    in1=d_banks[k][:, :columns]
                    .rearrange("p (n i) -> p n i", i=RUN)
                    .unsqueeze(2)
                    .to_broadcast([P, columns // RUN, PACK, RUN]),
                    op=ALU.mult,
                )

        def quantise(s, columns):
            if s not in codes:
                codes[s] = codes_pool.tile([P, QUARTER], U32, name="codes", align_bytes=64)
                scales[s] = codes_pool.tile([P, QUARTER], U8, name="scales", align_bytes=64)
            nc.vector.quantize_mx(
                out=codes[s][:, columns].bitcast(FP8X4),
                scales=scales[s][:, columns],
                in_=grouped[s][:, columns, :].rearrange("p i t -> p (i t)"),
            )

        def accumulate(s, k):
            c, q = units[s]
            b = 2 * q + k
            if b not in acc:
                acc[b] = acc_psum.tile([P, BLOCK], F32, name="acc", tag="acc")
                passes[b] = 0
            nc.tensor.matmul_mx(
                out=acc[b][:],
                lhsT=support_codes[:, c, :].bitcast(FP8X4),
                lhsT_scale=support_scales[:, c, :],
                rhs=codes[s][:, k * BLOCK : (k + 1) * BLOCK].bitcast(FP8X4),
                rhs_scale=scales[s][:, k * BLOCK : (k + 1) * BLOCK],
                start=(passes[b] == 0),
                stop=(passes[b] == N_BLOCKS - 1),
            )
            passes[b] += 1

        rows_psum = {}

        def turn_back(b, copies):
            out_t = out_pool.tile([P, BLOCK], F32, name="out_t")
            rows_psum[b] = side_psum.tile(
                [P, BLOCK // P, FEAT_OUT], F32, name="rows_psum", tag="even" if b % 2 == 0 else "odd"
            )
            share = BLOCK // len(copies)
            for k in range(len(copies)):
                copies[k](out=out_t[:, k * share : (k + 1) * share], in_=acc[b][:, k * share : (k + 1) * share])
                for i0 in range(k * share, (k + 1) * share, P):
                    nc.tensor.transpose(rows_psum[b][:, i0 // P, :], out_t[:, i0 : i0 + P], identity[:])

        def store(b, copies, queue):
            rows = out_pool.tile([P, BLOCK // P, FEAT_OUT], F32, name="rows")
            share = BLOCK // P // len(copies)
            for k in range(len(copies)):
                us = slice(k * share, (k + 1) * share)
                copies[k](out=rows[:, us, :], in_=rows_psum[b][:, us, :])
            queue.dma_start(out=out_view[b], in_=rows[:])


        for m in range(N_BLOCKS // 2):
            load_x_pair(m)
            if m == 0:
                quantise_w()
        for q in LOAD_ORDER:
            load_quarter(0, q)
        load_second_copy(1)
        load_quarter(1, 0)
        for q in LOAD_ORDER:
            load_quarter(2, q)
        load_second_copy(3)
        load_quarter(3, 0)

        turn_x(0)
        for c in range(N_BLOCKS + 1):
            if c + 1 < N_BLOCKS:
                turn_x(c + 1)
            if c < N_BLOCKS:
                slope_times_x(c)
            if c >= 1:
                multiply_h(c - 1)
            if c < N_BLOCKS:
                leaky_relu(c)
            if c >= 2:
                quantise_support(c - 2)
            if N_BLOCKS - 4 <= c < N_BLOCKS:
                pair = c - (N_BLOCKS - 4)
                rows = (0, 1) if pair % 2 == 0 else (2, 3)
                sum_quarter_rows(0, 2 + pair // 2, rows)
                sum_quarter_rows(0, pair // 2, rows)
            if c == N_BLOCKS - 1:
                for n in range(SUM_TILES):
                    fold(1, n)
        total(1)
        quantise_support(N_BLOCKS - 1)
        d_of_quarter_sums(0)
        d_of_total(1)
        scale(0)


        moves = {}
        for first, b0 in ((round_1, 0), (round_1 + 4, 2), (round_1 + N_BLOCKS + 1, 4)):
            moves[first] = (turn_back, b0)
            moves[first + 1] = (turn_back, b0 + 1)
            moves[first + 2] = (store, b0)
            moves[first + 3] = (store, b0 + 1)

        all_columns = slice(0, QUARTER)
        for s in range(len(units)):
            for c in range(4, N_BLOCKS):
                if c in WHOLE_ROW_BLOCKS and s == d_step[c] - PACK:
                    load_whole_rows(c)
                if c in TENSOR_SUM_ROW_BLOCKS and s == d_step[c] - 3:
                    load_second_copy(c)
            if s + LOAD_AHEAD < len(units):
                c, q = units[s + LOAD_AHEAD]
                if c in TENSOR_SUM_ROW_BLOCKS or q >= ROUND_QUARTERS:
                    load_quarter(c, q)

            spread(s)
            for c in TENSOR_SUM_ROW_BLOCKS:
                if c > 3 and s == d_step[c]:
                    total(c)
            if s + 1 < len(units):
                scale(s + 1)
            multiply(s)
            if s >= 1:
                quantise(s - 1, all_columns)
            if s >= 2:
                for k in range(2):
                    accumulate(s - 2, k)

            for c in range(2, N_BLOCKS):
                if c in TENSOR_SUM_ROW_BLOCKS:
                    if s == d_step[c] - 1:
                        for n in range(SUM_TILES):
                            fold(c, n)
                    if s == d_step[c]:
                        if c == 3:
                            total(c)
                        d_of_total(c)
                elif c in WHOLE_ROW_BLOCKS:
                    if d_step[c] - PACK < s <= d_step[c]:
                        sum_whole_row(c, s - (d_step[c] - PACK + 1))
                    if s == d_step[c]:
                        inverse_root(c, sums_scalar[:, c, 0, :])
                elif s == d_step[c]:
                    for q in LOAD_ORDER:
                        sum_quarter_rows(c, q, range(PACK))
                    d_of_quarter_sums(c)
            q = s - d_step[N_BLOCKS - 1] - 1 + ROUND_QUARTERS
            if ROUND_QUARTERS <= q < 2 * ROUND_QUARTERS:
                d_turned = side_psum.tile([P, BLOCK], F32, name="d_turned", tag="even")
                spread_d(d_turned, 2 * q + 1)
                nc.scalar.copy(out=d_gpsimd[q][:], in_=d_turned[:, BLOCK - GPSIMD_COLUMNS_1 :])
            if s in moves:
                move, b = moves[s]
                if move == turn_back:
                    turn_back(b, (nc.scalar.copy,))
                else:
                    store(b, (nc.scalar.copy,), nc.scalar)

        last = len(units) - 1
        for k in range(2):
            accumulate(last - 1, k)
        for k in range(2):
            quantise(last, slice(k * BLOCK, (k + 1) * BLOCK))
            accumulate(last, k)
        turn_back(N_BLOCKS - 2, (nc.scalar.copy,))
        turn_back(N_BLOCKS - 1, (nc.vector.tensor_copy, nc.scalar.copy))
        store(N_BLOCKS - 2, (nc.scalar.copy,), nc.sync)
        store(N_BLOCKS - 1, (nc.vector.tensor_copy, nc.scalar.copy), nc.sync)
